import numpy as np
import ml_dtypes


def mxq(x, axis, fmt="e4m3"):
    dtype, down = {"e4m3": (ml_dtypes.float8_e4m3fn, 7), "e5m2": (ml_dtypes.float8_e5m2, 14)}[fmt]
    v = np.moveaxis(np.asarray(x, np.float32).astype(ml_dtypes.bfloat16).astype(np.float64), axis, -1)
    blocks = v.reshape(v.shape[:-1] + (-1, 32))
    amax = np.abs(blocks).max(-1, keepdims=True)
    byte = np.maximum(np.where(amax > 0, np.frexp(amax)[1] - 1 + 127, 0) - down, 1)
    scale = np.exp2(byte - 127.0)
    codes = (blocks / scale).astype(np.float32).astype(dtype).astype(np.float64)
    return np.moveaxis((codes * scale).reshape(v.shape), -1, axis)


WIDE = False


def mx_kscale(k):
    if not WIDE:
        return np.ones(k)
    levels = np.array([10, -10, 5, -5, 0])
    if k % 512:
        return np.exp2(np.random.permutation(np.resize(levels, k // 32))).repeat(32)
    a = np.empty((k // 512, 16))
    for p in range(k // 512):
        a[p, :8] = np.random.permutation(np.resize(levels, 8))
        for g in range(8):
            far = levels[np.abs(levels - a[p, g]) >= 10]
            a[p, g + 8] = far[np.random.randint(len(far))]
    return np.exp2(a.ravel()).repeat(32)


BF16 = ml_dtypes.bfloat16


def bf(x):
    return np.asarray(x, np.float32).astype(BF16)


def f64(x):
    return np.asarray(x).astype(np.float64)


B, C, H, W = 2, 512, 64, 64
N = H * W
KV = 0.05 * N / np.sqrt(C)


def draw0():
    s, t = mx_kscale(C), mx_kscale(C)
    return {"x": bf(np.random.standard_normal((B, C, H, W)) * s[None, :, None, None]),
            "mask": bf(np.random.random_sample((B, 1, H, W))),
            "W_q": bf(np.random.standard_normal((C, C)) / np.sqrt(C) / s[:, None]),
            "b_q": bf(np.random.standard_normal(C) * 0.3),
            "kv_know": bf(np.random.standard_normal((B, 1, C)) * KV * t),
            "kv_mask": bf(np.random.standard_normal((B, 1, C)) * KV * t),
            "W_out": bf(np.random.standard_normal((C, C)) / KV / t[:, None]),
            "b_out": bf(np.random.standard_normal(C) * 0.2)}


def core(x, mask, W_q, b_q, kv_know, kv_mask, W_out, b_out):
    x, mask = f64(x), f64(mask)
    b, c, h, w = x.shape
    xf = np.transpose(x, (0, 2, 3, 1)).reshape(b, h * w, c)
    q = (mxq(xf, 2, "e4m3") @ mxq(f64(W_q), 0, "e4m3")) + f64(b_q)
    q = q / np.linalg.norm(q, axis=-1, keepdims=True)
    m = np.transpose(mask, (0, 2, 3, 1)).reshape(b, h * w, 1)
    inv = 1.0 - m
    qu = q * inv
    qm = q * m
    out_know = f64(kv_know) * qu
    out_mask = f64(kv_mask) * qm
    out = out_know * inv + m * (0.3 * out_know + 0.7 * out_mask)
    return (mxq(out, 2, "e4m3") @ mxq(f64(W_out), 0, "e4m3")) + f64(b_out)


def e4m3fn_bytes(y):
    return np.clip(np.asarray(y, np.float64), -448.0, 448.0).astype(np.float32).astype(ml_dtypes.float8_e4m3fn).view(np.uint8)


def e4m3fn_values(b):
    return np.asarray(b, np.uint8).view(ml_dtypes.float8_e4m3fn).astype(np.float64)


def setup_inputs():
    d = draw0()
    x0 = np.asarray(d['x']).astype(np.float64)
    s = (np.max(np.abs(x0), axis=(0, 2, 3), keepdims=True) / 448.0).astype(np.float32)
    out = {}
    for k, v in d.items():
        if k == 'x':
            out['x_bytes'] = e4m3fn_bytes(x0 / s.astype(np.float64))
            out['x_scale'] = s
        else:
            out[k] = v
    return out


def reference(x_bytes, x_scale, mask, W_q, b_q, kv_know, kv_mask, W_out, b_out):
    return core(e4m3fn_values(x_bytes) * x_scale.astype(np.float64), mask, W_q, b_q, kv_know, kv_mask, W_out, b_out)

@@ -1,0 +1,527 @@
+from contextlib import ExitStack
+
+import concourse.mybir as mybir
+from concourse.masks import make_identity
+
+F32 = mybir.dt.float32
+BF16 = mybir.dt.bfloat16
+U32 = mybir.dt.uint32
+U8 = mybir.dt.uint8
+FP8 = mybir.dt.float8_e4m3fn
+FP8X4 = mybir.dt.float8_e4m3fn_x4
+ALU = mybir.AluOpType
+ACT = mybir.ActivationFunctionType
+AXIS = mybir.AxisListType
+
+B = 2
+C = 512
+N = 4096
+P = 128
+PACK = 4
+TILE = 128
+CHUNK = 512
+NT = CHUNK // TILE
+NTILES = B * N // TILE
+NCHUNKS = B * N // CHUNK
+PER_IMG = N // CHUNK
+BLK = 16
+Q = 8
+
+FLOPS = 2 * 2 * B * N * C * C
+
+X_LOADS = ((0, 0, 512), (0, 512, 512), (0, 1024, 1024), (0, 2048, 2048), (1, 0, 2048), (1, 2048, 2048))
+V_WIDENS = (9, 11)
+LIGHT = (2, 3, 4, 5, 6, 7, 17)
+TURNED_GATES = [(k, i) for k in range(2) for i in range(4)] + [(k, 3) for k in range(3, 8)]
+
+
+def tile_hydraattention_pb_t_kernel(tc, x_bytes, x_scale, mask, W_q, b_q, kv_know, kv_mask, W_out, b_out, out):
+    nc = tc.nc
+    out_rows = out.rearrange("b t c -> (b t) c")
+
+    with ExitStack() as ctx:
+        keep = ctx.enter_context(tc.tile_pool(name="keep", bufs=1))
+        work = ctx.enter_context(tc.tile_pool(name="work", bufs=3))
+        psum = ctx.enter_context(tc.psum_pool(name="psum", bufs=2))
+        ctx.enter_context(tc.manual_schedule())
+
+        mrow = keep.tile([P, P], BF16, name="mrow")
+        nc.vector.memset(mrow[:], 0.0)
+        nc.sync.dma_start(out=mrow[0:NTILES, :], in_=mask.rearrange("b o (r q) w -> (b o r) (q w)", q=2))
+        xs = keep.tile([P, PACK], F32, name="xs")
+        nc.sync.dma_start(out=xs[:], in_=x_scale.rearrange("o (p j) a b -> p (o j a b)", j=PACK))
+        x_tiles = []
+
+        def load_x(i):
+            img, t0, width = X_LOADS[i]
+            t = keep.tile([P, PACK, width], U8, name=f"xb{i}", align_bytes=64)
+            nc.sync.dma_start(out=t[:], in_=x_bytes[img].rearrange("(p j) h w -> p j (h w)", j=PACK)[:, :, t0 : t0 + width])
+            x_tiles.append((img * N + t0, width, t))
+
+        load_x(0)
+        kv_raw = []
+
+        def load_kv(img):
+            t = keep.tile([P, C], BF16, name=f"kv_raw{img}")
+            nc.vector.memset(t[96:P, :], 0.0)
+            nc.sync.dma_start(out=t[0:48, :], in_=kv_know[img].rearrange("o c -> (o c)").partition_broadcast(48))
+            nc.sync.dma_start(out=t[48:96, :], in_=kv_mask[img].rearrange("o c -> (o c)").partition_broadcast(48))
+            kv_raw.append(t)
+
+        wq_raw = keep.tile([P, PACK, C], BF16, name="wq_raw")
+        nc.sync.dma_start(out=wq_raw[:], in_=W_q.rearrange("(p j) w -> p j w", j=PACK))
+        load_kv(0)
+        bq_raw = keep.tile([P, C], BF16, name="bq_raw")
+        nc.sync.dma_start(out=bq_raw[:], in_=b_q.partition_broadcast(P))
+        load_x(1)
+
+        load_x(2)
+        wo_raw = keep.tile([P, PACK, C], BF16, name="wo_raw")
+        nc.sync.dma_start(out=wo_raw[:], in_=W_out.rearrange("(p j) w -> p j w", j=PACK))
+        bo = keep.tile([P, C], BF16, name="bo")
+        nc.sync.dma_start(out=bo[:], in_=b_out.partition_broadcast(P))
+        load_kv(1)
+        load_x(3)
+        load_x(4)
+        load_x(5)
+
+        planes = {}
+        xcodes = {}
+        gcodes = {}
+        batch = {}
+
+        def widen(k, chunks, j, eng):
+            t0 = k * CHUNK
+            w = chunks * CHUNK
+            if j == 0:
+                pl = work.tile([P, PACK, 2 * CHUNK], BF16, name="planes", align_bytes=64)
+                for c in range(chunks):
+                    planes[k + c] = pl[:, :, c * CHUNK : (c + 1) * CHUNK]
+                planes["w", k] = pl
+            for start, width, t in x_tiles:
+                if start <= t0 < start + width:
+                    src = t[:, j, t0 - start : t0 - start + w].bitcast(FP8)
+            dst = planes["w", k][:, j, 0:w]
+            if eng == "s":
+                nc.scalar.activation(out=dst, in_=src, func=ACT.Copy, scale=xs[:, j : j + 1])
+            else:
+                nc.vector.tensor_scalar(out=dst, in0=src, scalar1=xs[:, j : j + 1], scalar2=None, op0=ALU.mult)
+
+        def batch_half(s, half):
+            if s not in batch:
+                nm = "batch" if s >= 2 else f"batch{s + 1}"
+                batch[s] = work.tile([P, 2, CHUNK, PACK], BF16, name=nm, bufs=1, align_bytes=64)
+            return batch[s][:, half]
+
+        def interleave(k, part, parts, eng):
+            dst_all = batch_half(k - 1, 0)
+            w = CHUNK // parts
+            dst = dst_all[:, part * w : (part + 1) * w, :]
+            src = planes[k][:, :, part * w : (part + 1) * w].rearrange("p j w -> p w j")
+            if eng == "g":
+                nc.gpsimd.tensor_scalar(out=dst, in0=src, scalar1=1.0, scalar2=0.0, op0=ALU.mult, op1=ALU.add)
+            elif eng == "s":
+                nc.scalar.copy(out=dst, in_=src)
+            else:
+                nc.vector.tensor_copy(out=dst, in_=src)
+
+        def quantize_half(s, h):
+            if h == 0:
+                codes = work.tile([P, 2, CHUNK], U32, name="codes", align_bytes=64)
+                scales = work.tile([P, 2, CHUNK], U8, name="scales", align_bytes=64)
+                gcodes[s - 2] = (codes[:, 1], scales[:, 1])
+            codes, scales = gcodes[s - 2]
+            cols = slice(h * 256, (h + 1) * 256)
+            nc.vector.quantize_mx(out=codes[:, cols].bitcast(FP8X4), scales=scales[:, cols], in_=batch[s][:, 1, cols].rearrange("p w j -> p (w j)"))
+
+        def quantize(s):
+            lo = 0 if s + 1 < NCHUNKS else 1
+            hi = 2 if s - 2 >= 0 else 1
+            codes = work.tile([P, 2, CHUNK], U32, name="codes", align_bytes=64)
+            scales = work.tile([P, 2, CHUNK], U8, name="scales", align_bytes=64)
+            nc.vector.quantize_mx(
+                out=codes[:, lo:hi].rearrange("p h w -> p (h w)").bitcast(FP8X4),
+                scales=scales[:, lo:hi].rearrange("p h w -> p (h w)"),
+                in_=batch.pop(s)[:, lo:hi].rearrange("p h w j -> p (h w j)"),
+            )
+            if lo == 0:
+                xcodes[s + 1] = (codes[:, 0], scales[:, 0])
+            if hi == 2:
+                gcodes[s - 2] = (codes[:, 1], scales[:, 1])
+
+        warm = keep.tile([P, 1], F32, name="warm")
+        nc.vector.memset(warm[:], 1.0)
+        nc.scalar.activation(out=warm[:], in_=warm[:], func=ACT.Abs_reciprocal_sqrt)
+        ident = keep.tile([P, P], F32, name="ident", align_bytes=64)
+        make_identity(nc, ident[:])
+        ident_b = keep.tile([P, P], BF16, name="ident_b", align_bytes=64)
+        nc.vector.tensor_copy(out=ident_b[:], in_=ident[:])
+        sel = keep.tile([P, BLK], F32, name="sel")
+        nc.vector.tensor_reduce(out=sel[:], in_=ident[:].rearrange("p (q i) -> p i q", q=Q), axis=AXIS.X, op=ALU.add)
+        pieces = keep.tile([P, NTILES // BLK, Q, BLK], BF16, name="pieces", align_bytes=64)
+        nc.vector.memset(pieces[:], 0.0)
+
+        mrow32 = keep.tile([P, P], F32, name="mrow32", align_bytes=64)
+        nc.vector.tensor_copy(out=mrow32[:], in_=mrow[:])
+        m_ps = psum.tile([P, P], F32, name="m_ps", tag="tr")
+        nc.tensor.transpose(m_ps[:], mrow32[:], ident[:])
+        m = keep.tile([P, NTILES], F32, name="m")
+        nc.scalar.copy(out=m[:], in_=m_ps[:, 0:NTILES])
+        t1 = keep.tile([P, NTILES], F32, name="t1")
+        t2 = keep.tile([P, NTILES], F32, name="t2")
+        t3 = keep.tile([P, NTILES], F32, name="t3")
+        t4 = keep.tile([P, NTILES], F32, name="t4")
+        sg = keep.tile([P, NTILES], F32, name="sg")
+        inv_sg = keep.tile([P, NTILES], F32, name="inv_sg")
+        v = keep.tile([P, 2, NTILES], F32, name="v")
+        rest = [keep.tile([P, 2, NTILES], F32, name=f"rest{i}") for i in range(2)]
+
+        def g_affine(dst, src, a, b):
+            nc.gpsimd.tensor_scalar(out=dst, in0=src, scalar1=a, scalar2=b, op0=ALU.mult, op1=ALU.add)
+
+        widen(0, 1, 0, "s")
+        widen(0, 1, 1, "v")
+        widen(0, 1, 2, "v")
+        nc.vector.tensor_scalar(out=t1[:], in0=m[:], scalar1=1.4, scalar2=-1.7, op0=ALU.mult, op1=ALU.add)
+        nc.vector.tensor_scalar(out=t3[:], in0=m[:], scalar1=0.7, scalar2=None, op0=ALU.mult)
+        widen(0, 1, 3, "v")
+        nc.vector.tensor_mul(out=t2[:], in0=t1[:], in1=m[:])
+        nc.vector.tensor_mul(out=t4[:], in0=t3[:], in1=m[:])
+        interleave(0, 0, 2, "v")
+        nc.vector.tensor_scalar(out=sg[:], in0=t2[:], scalar1=1.0, scalar2=None, op0=ALU.add)
+        interleave(0, 1, 2, "v")
+        nc.vector.reciprocal(out=inv_sg[:], in_=sg[:])
+
+        wq_grouped = keep.tile([P, C, PACK], BF16, name="wq_grouped", align_bytes=64)
+        wq_codes = keep.tile([P, C], U32, name="wq_codes", align_bytes=64)
+        wq_scales = keep.tile([P, C], U8, name="wq_scales", align_bytes=64)
+
+        def permute_wq(u, eng):
+            dst = wq_grouped[:, u * 256 : (u + 1) * 256, :].rearrange("p (m e) j -> p m e j", e=2)
+            src = wq_raw[:].rearrange("p j (m u e) -> p u m e j", u=2, e=2)[:, u]
+            if eng == "g":
+                g_affine(dst, src, 1.0, 0.0)
+            else:
+                nc.scalar.copy(out=dst, in_=src)
+
+        permute_wq(0, "s")
+        permute_wq(1, "s")
+        nc.gpsimd.tensor_mul(out=v[:, 1, :], in0=t4[:], in1=inv_sg[:])
+        quantize(-1)
+        bq = keep.tile([P, C], BF16, name="bq")
+        nc.scalar.copy(out=bq[:].rearrange("p (u m e) -> p u m e", u=2, e=2), in_=bq_raw[:].rearrange("p (m u e) -> p u m e", u=2, e=2))
+
+
+        def piece(i):
+            res = v if i == 0 else rest[i - 1]
+            for h in range(2):
+                src = res[:, h, :].rearrange("p (b i) -> p b i", i=BLK)
+                g_affine(pieces[:, :, 3 * h + i, :], src, 1.0, 0.0)
+                if i < 2:
+                    nc.gpsimd.tensor_sub(out=rest[i][:, h, :].rearrange("p (b i) -> p b i", i=BLK), in0=src, in1=pieces[:, :, 3 * h + i, :])
+
+        nc.vector.quantize_mx(out=wq_codes[:].bitcast(FP8X4), scales=wq_scales[:], in_=wq_grouped[:].rearrange("p w j -> p (w j)"))
+        for j in range(PACK):
+            widen(1, 1, j, "v")
+
+        q0 = {}
+        gate = {}
+        qb = {}
+        ss = {}
+        rn = {}
+        gt = {}
+        tr = {}
+        y_ps = {}
+
+        def mm1(k, i):
+            codes, scales = xcodes[k]
+            cols = slice(i * TILE, (i + 1) * TILE)
+            q0[k, i] = psum.tile([P, C], F32, name="q0")
+            nc.tensor.matmul_mx(out=q0[k, i][:], lhsT=codes[:, cols].bitcast(FP8X4), lhsT_scale=scales[:, cols],
+                                rhs=wq_codes[:].bitcast(FP8X4), rhs_scale=wq_scales[:], start=True, stop=True)
+
+        mm1(0, 0)
+        mm1(0, 1)
+
+        pt = keep.tile([P, 4, P], BF16, name="pt", align_bytes=64)
+        ptm = keep.tile([P, BLK, 4, P], BF16, name="ptm", align_bytes=64)
+
+        def turn_pieces():
+            ps = psum.tile([P, 4, P], BF16, name="pt_ps", tag="tr")
+            for b in range(4):
+                nc.tensor.transpose(ps[:, b, :], pieces[:, b].rearrange("p q i -> p (q i)"), ident_b[:])
+            nc.scalar.copy(out=pt[:], in_=ps[:])
+
+        def mask_pieces(ii):
+            nc.vector.tensor_scalar(out=ptm[:, ii], in0=pt[:], scalar1=sel[:, ii : ii + 1], scalar2=None, op0=ALU.mult)
+
+        interleave(1, 0, 2, "g")
+        interleave(1, 1, 2, "g")
+
+        kv_rows = []
+
+        def permute_rows(img):
+            r = keep.tile([P, C], BF16, name=f"kv_rows{img}", align_bytes=64)
+            nc.scalar.copy(out=r[:].rearrange("p (u m e) -> p u m e", u=2, e=2), in_=kv_raw[img][:].rearrange("p (m u e) -> p u m e", u=2, e=2))
+            kv_rows.append(r)
+
+        kcol = keep.tile([P, 4], F32, name="kcol")
+        dcol = keep.tile([P, 4], F32, name="dcol")
+
+        def take_columns():
+            ps = psum.tile([P, 4, P], BF16, name="kv_ps", tag="tr")
+            for r in range(4):
+                nc.tensor.transpose(ps[:, r, :], kv_rows[0][:, r * P : (r + 1) * P], ident_b[:])
+            nc.vector.tensor_copy(out=kcol[:], in_=ps[:, :, 0])
+            nc.vector.tensor_sub(out=dcol[:], in0=ps[:, :, 48], in1=kcol[:])
+
+        gate_t = {}
+
+        def spread_rho(todo):
+            ps = psum.tile([P, 4, TILE], F32, name="rho_ps", tag="tr")
+            for n, (k, i) in enumerate(todo):
+                t = k * NT + i
+                nc.tensor.transpose(ps[:, n, :], v[:, 1, t : t + 1].to_broadcast([P, P]), ident[:])
+            return ps
+
+        def gate_columns(todo, ps, first=0):
+            for n, (k, i) in enumerate(todo, first):
+                gate_t[k, i] = keep.tile([P, 4, TILE], F32, name=f"gate_t{k}_{i}", align_bytes=64)
+                for r in range(4):
+                    nc.scalar.activation(out=gate_t[k, i][:, r, :], in_=ps[:, n, :], func=ACT.Identity, scale=dcol[:, r : r + 1], bias=kcol[:, r : r + 1])
+
+        wo_grouped = keep.tile([P, C, PACK], BF16, name="wo_grouped", align_bytes=64)
+        wo_codes = keep.tile([P, C], U32, name="wo_codes", align_bytes=64)
+        wo_scales = keep.tile([P, C], U8, name="wo_scales", align_bytes=64)
+
+
+        def make_gate(k, i):
+            t = k * NT + i
+            img = k // PER_IMG
+            gate[k, i] = psum.tile([P, C], F32, name="gate")
+            if (k, i) in TURNED_GATES:
+                for r in range(4):
+                    nc.tensor.transpose(gate[k, i][:, r * P : (r + 1) * P], gate_t[k, i][:, r, :], ident[:])
+            else:
+                nc.tensor.matmul(gate[k, i][:], lhsT=ptm[:, t % BLK, t // BLK, :], rhs=kv_rows[img][:], start=True, stop=True)
+
+        def add_bias(k, i):
+            qb[k, i] = work.tile([P, C], F32, name="qb", bufs=10)
+            nc.vector.tensor_add(out=qb[k, i][:], in0=q0.pop((k, i))[:], in1=bq[:])
+
+        def squares(k, i):
+            if k not in ss:
+                ss[k] = work.tile([P, NT], F32, name="ss")
+            t = k * NT + i
+            junk = work.tile([P, C], BF16, name="junk", bufs=8)
+            nc.scalar.activation(out=junk[:], in_=qb[k, i][:], func=ACT.Square, scale=inv_sg[:, t : t + 1], accum_out=ss[k][:, i : i + 1])
+
+        def root(k):
+            rn[k] = work.tile([P, NT], F32, name="rn")
+            nc.scalar.activation(out=rn[k][:], in_=ss[k][:], func=ACT.Abs_reciprocal_sqrt)
+
+        def gating(k, i):
+            gt[k, i] = work.tile([P, C], BF16, name="gt", bufs=6, align_bytes=64)
+            nc.vector.scalar_tensor_tensor(out=gt[k, i][:], in0=gate.pop((k, i))[:], scalar=rn[k][:, i : i + 1], in1=qb.pop((k, i))[:], op0=ALU.mult, op1=ALU.mult)
+
+        def turn(k, h):
+            tr[k, h] = psum.tile([P, 2, 2, TILE], F32, name="tr", tag="tr")
+            for a in range(2):
+                words = gt.pop((k, 2 * h + a))[:].bitcast(F32)
+                for u in range(2):
+                    nc.tensor.transpose(tr[k, h][:, a, u, :], words[:, u * 128 : (u + 1) * 128], ident[:])
+
+        def unload(k, h):
+            dst = batch_half(k + 2, 1).rearrange("p w j -> p (w j)").bitcast(F32)[:, h * 512 : (h + 1) * 512]
+            nc.scalar.copy(out=dst.rearrange("p (a r u) -> p a r u", a=2, u=2), in_=tr.pop((k, h))[:].rearrange("p a u r -> p a r u"))
+
+        def mm2(k, i):
+            codes, scales = gcodes[k]
+            cols = slice(i * TILE, (i + 1) * TILE)
+            y_ps[k, i] = psum.tile([P, C], F32, name="y_ps")
+            nc.tensor.matmul_mx(out=y_ps[k, i][:], lhsT=codes[:, cols].bitcast(FP8X4), lhsT_scale=scales[:, cols],
+                                rhs=wo_codes[:].bitcast(FP8X4), rhs_scale=wo_scales[:], start=True, stop=True)
+
+        y_sb = {}
+
+        def finish(k, i, eng):
+            h = i // 2
+            if (k, h) not in y_sb:
+                y_sb[k, h] = work.tile([P, 2, C], F32, name=f"y{h}", bufs=3)
+            y = y_sb[k, h][:, i % 2, :]
+            src = y_ps.pop((k, i))
+            if eng == "v":
+                nc.vector.tensor_add(out=y, in0=src[:], in1=bo[:])
+            else:
+                nc.scalar.copy(out=y, in_=src[:])
+
+        def add_out(k, i):
+            y = y_sb[k, i // 2][:, i % 2, :]
+            nc.gpsimd.tensor_add(out=y, in0=y, in1=bo[:])
+
+        def store(k, h):
+            t0 = (k * NT + 2 * h) * TILE
+            nc.sync.dma_start(out=out_rows[t0 : t0 + 2 * TILE, :].rearrange("(a p) c -> p a c", p=P), in_=y_sb.pop((k, h))[:])
+
+        def store_one(k, i):
+            t0 = (k * NT + i) * TILE
+            nc.sync.dma_start(out=out_rows[t0 : t0 + TILE, :], in_=y_sb[k, i // 2][:, i % 2, :])
+
+        def step(s):
+            new = s < NCHUNKS
+            mid = 0 <= s - 1 < NCHUNKS
+            old = 0 <= s - 2 < NCHUNKS
+            fill = s + 2 < NCHUNKS
+            pair = s + 4 - s % 2
+            todo = [g for g in TURNED_GATES if g[0] == s]
+            if s in V_WIDENS:
+                widen(pair, 2, 3, "v")
+            if s >= 2:
+                quantize(s)
+            if s == 2:
+                nc.vector.quantize_mx(out=wo_codes[:].bitcast(FP8X4), scales=wo_scales[:], in_=wo_grouped[:].rearrange("p w j -> p (w j)"))
+            if s >= 2 and pair < NCHUNKS:
+                widen(pair, 2, 2 * (s % 2), "s")
+                if s not in V_WIDENS:
+                    widen(pair, 2, 2 * (s % 2) + 1, "s")
+            if fill and s >= 2:
+                interleave(s + 2, 0, 2, "g")
+                interleave(s + 2, 1, 2, "g")
+            if old:
+                mm2(s - 2, 0)
+                mm2(s - 2, 1)
+            if s <= 1:
+                add_bias(s, 0)
+                add_bias(s, 1)
+            if s == 0:
+                take_columns()
+                rho0 = spread_rho(todo)
+                gate_columns(todo[:2], rho0)
+            if mid:
+                gating(s - 1, 1)
+                gating(s - 1, 0)
+                make_gate(s - 1, 2)
+                make_gate(s - 1, 3)
+                turn(s - 1, 0)
+            by_scalar = (1,) if s in LIGHT else (1, 0)
+            if old:
+                for i in by_scalar:
+                    finish(s - 2, i, "s")
+                    add_out(s - 2, i)
+            if mid and s >= 2:
+                unload(s - 1, 0)
+            if new and s >= 2:
+                add_bias(s, 0)
+                add_bias(s, 1)
+            if new:
+                mm1(s, 2)
+                mm1(s, 3)
+                squares(s, 1)
+                squares(s, 0)
+            if s == 1:
+                unload(0, 0)
+            if s == 2:
+                turn_pieces()
+            if old and 0 not in by_scalar:
+                finish(s - 2, 0, "v")
+            if old:
+                mm2(s - 2, 2)
+                mm2(s - 2, 3)
+            if mid:
+                gating(s - 1, 3)
+                gating(s - 1, 2)
+                turn(s - 1, 1)
+                unload(s - 1, 1)
+            if new:
+                add_bias(s, 3)
+                add_bias(s, 2)
+                squares(s, 3)
+                squares(s, 2)
+                root(s)
+            if s <= 1:
+                for j in range(2):
+                    widen(2 * s + 2, 2, 2 + j, "v")
+                quantize(s)
+            if s == 0:
+                for i in range(4):
+                    interleave(2 + i // 2, i % 2, 2, "g")
+                g_affine(v[:, 0, :], v[:, 1, :], -1.0, 1.0)
+                for i in range(3):
+                    piece(i)
+            if s == 2:
+                for ii in range(8, 12):
+                    mask_pieces(ii)
+            if s + 1 < NCHUNKS:
+                mm1(s + 1, 0)
+                mm1(s + 1, 1)
+            if todo:
+                if s == 0:
+                    gate_columns(todo[2:], rho0, 2)
+                else:
+                    gate_columns(todo, spread_rho(todo))
+            if new:
+                make_gate(s, 0)
+                make_gate(s, 1)
+            if s == 0:
+                widen(4, 2, 0, "s")
+                widen(4, 2, 1, "s")
+            if old:
+                for i in (3, 2):
+                    finish(s - 2, i, "v")
+                store(s - 2, 0)
+                store(s - 2, 1)
+            if s in (2, 3, 4):
+                for ii in [(12, 13, 14, 15), (0, 1, 2, 3), (4, 5, 6, 7)][s - 2]:
+                    mask_pieces(ii)
+            if s == 1:
+                nc.vector.tensor_copy(out=wo_grouped[:], in_=wo_raw[:].rearrange("p j w -> p w j"))
+            if s == 5:
+                permute_rows(1)
+
+        def last_steps():
+            k = NCHUNKS - 1
+            s = NCHUNKS
+            quantize(s)
+            mm2(k - 1, 0)
+            mm2(k - 1, 1)
+            gating(k, 1)
+            gating(k, 0)
+            make_gate(k, 2)
+            make_gate(k, 3)
+            turn(k, 0)
+            finish(k - 1, 1, "s")
+            add_out(k - 1, 1)
+            unload(k, 0)
+            finish(k - 1, 0, "v")
+            store(k - 1, 0)
+            mm2(k - 1, 2)
+            mm2(k - 1, 3)
+            gating(k, 3)
+            gating(k, 2)
+            turn(k, 1)
+            unload(k, 1)
+            quantize_half(s + 1, 0)
+            mm2(k, 0)
+            mm2(k, 1)
+            finish(k - 1, 3, "v")
+            finish(k - 1, 2, "v")
+            store(k - 1, 1)
+            quantize_half(s + 1, 1)
+            finish(k, 0, "s")
+            add_out(k, 0)
+            finish(k, 1, "v")
+            mm2(k, 2)
+            mm2(k, 3)
+            store_one(k, 1)
+            finish(k, 2, "v")
+            store_one(k, 0)
+            finish(k, 3, "v")
+            store_one(k, 2)
+            store_one(k, 3)
+
+        permute_rows(0)
+        widen(2, 2, 0, "s")
+        widen(2, 2, 1, "s")
+        for s in range(NCHUNKS):
+            step(s)
+        last_steps()

@@ -17,6 +17,7 @@ B = 2
 C = 512
 N = 4096
 P = 128
+HALF = 64
 PACK = 4
 TILE = 128
 CHUNK = 512
@@ -24,15 +25,13 @@ NT = CHUNK // TILE
 NTILES = B * N // TILE
 NCHUNKS = B * N // CHUNK
 PER_IMG = N // CHUNK
-BLK = 16
-Q = 8
+PIECES = 3
 
 FLOPS = 2 * 2 * B * N * C * C
 
 X_LOADS = ((0, 0, 512), (0, 512, 512), (0, 1024, 1024), (0, 2048, 2048), (1, 0, 2048), (1, 2048, 2048))
-V_WIDENS = (9, 11)
-LIGHT = (2, 3, 4, 5, 6, 7, 17)
-TURNED_GATES = [(k, i) for k in range(2) for i in range(4)] + [(k, 3) for k in range(3, 8)]
+FIRST_TURNED = 3
+LAST = NT - 1
 
 
 def tile_hydraattention_pb_t_kernel(tc, x_bytes, x_scale, mask, W_q, b_q, kv_know, kv_mask, W_out, b_out, out):
@@ -42,14 +41,16 @@ def tile_hydraattention_pb_t_kernel(tc, x_bytes, x_scale, mask, W_q, b_q, kv_kno
     with ExitStack() as ctx:
         keep = ctx.enter_context(tc.tile_pool(name="keep", bufs=1))
         work = ctx.enter_context(tc.tile_pool(name="work", bufs=3))
-        psum = ctx.enter_context(tc.psum_pool(name="psum", bufs=2))
+        psum = ctx.enter_context(tc.psum_pool(name="psum", bufs=1))
         ctx.enter_context(tc.manual_schedule())
 
-        mrow = keep.tile([P, P], BF16, name="mrow")
-        nc.vector.memset(mrow[:], 0.0)
-        nc.sync.dma_start(out=mrow[0:NTILES, :], in_=mask.rearrange("b o (r q) w -> (b o r) (q w)", q=2))
-        xs = keep.tile([P, PACK], F32, name="xs")
-        nc.sync.dma_start(out=xs[:], in_=x_scale.rearrange("o (p j) a b -> p (o j a b)", j=PACK))
+        s_banks = [f"s{i}" for i in range(4)]
+        v_banks = [f"v{i}" for i in range(4)]
+
+        def take(banks, shape, dtype):
+            tag = banks.pop(0)
+            return psum.tile(shape, dtype, name="bank_" + tag, tag=tag), tag
+
         x_tiles = []
 
         def load_x(i):
@@ -58,470 +59,442 @@ def tile_hydraattention_pb_t_kernel(tc, x_bytes, x_scale, mask, W_q, b_q, kv_kno
             nc.sync.dma_start(out=t[:], in_=x_bytes[img].rearrange("(p j) h w -> p j (h w)", j=PACK)[:, :, t0 : t0 + width])
             x_tiles.append((img * N + t0, width, t))
 
+        kv_all = {}
+        kv_half = {}
+
+        def load_kv_all(img):
+            kv_all[img] = keep.tile([P, 2, C], BF16, name=f"kv_all{img}")
+            for h, vec in enumerate((kv_know, kv_mask)):
+                nc.sync.dma_start(out=kv_all[img][:, h, :], in_=vec[img].rearrange("o c -> (o c)").partition_broadcast(P))
+
+        def load_kv_half(img):
+            kv_half[img] = keep.tile([P, C], BF16, name=f"kv_half{img}")
+            for h, vec in enumerate((kv_know, kv_mask)):
+                nc.sync.dma_start(out=kv_half[img][h * HALF : (h + 1) * HALF, :], in_=vec[img].rearrange("o c -> (o c)").partition_broadcast(HALF))
+
+        xs = keep.tile([P, PACK], F32, name="xs")
+        nc.sync.dma_start(out=xs[:], in_=x_scale.rearrange("o (p j) a b -> p (o j a b)", j=PACK))
         load_x(0)
-        kv_raw = []
-
-        def load_kv(img):
-            t = keep.tile([P, C], BF16, name=f"kv_raw{img}")
-            nc.vector.memset(t[96:P, :], 0.0)
-            nc.sync.dma_start(out=t[0:48, :], in_=kv_know[img].rearrange("o c -> (o c)").partition_broadcast(48))
-            nc.sync.dma_start(out=t[48:96, :], in_=kv_mask[img].rearrange("o c -> (o c)").partition_broadcast(48))
-            kv_raw.append(t)
-
         wq_raw = keep.tile([P, PACK, C], BF16, name="wq_raw")
         nc.sync.dma_start(out=wq_raw[:], in_=W_q.rearrange("(p j) w -> p j w", j=PACK))
-        load_kv(0)
-        bq_raw = keep.tile([P, C], BF16, name="bq_raw")
-        nc.sync.dma_start(out=bq_raw[:], in_=b_q.partition_broadcast(P))
+        bq_raw = keep.tile([P, PACK], BF16, name="bq_raw")
+        nc.sync.dma_start(out=bq_raw[:], in_=b_q.rearrange("(p t) -> p t", t=PACK))
         load_x(1)
-
+        mrow = keep.tile([P, P], BF16, name="mrow", align_bytes=64)
+        nc.sync.dma_start(out=mrow[0:NTILES, :], in_=mask.rearrange("b o (r q) w -> (b o r) (q w)", q=2))
         load_x(2)
+        load_kv_half(0)
         wo_raw = keep.tile([P, PACK, C], BF16, name="wo_raw")
         nc.sync.dma_start(out=wo_raw[:], in_=W_out.rearrange("(p j) w -> p j w", j=PACK))
+        load_x(3)
         bo = keep.tile([P, C], BF16, name="bo")
         nc.sync.dma_start(out=bo[:], in_=b_out.partition_broadcast(P))
-        load_kv(1)
-        load_x(3)
+        load_kv_half(1)
+        load_kv_all(0)
         load_x(4)
+        load_kv_all(1)
         load_x(5)
 
         planes = {}
+        grouped = {}
         xcodes = {}
         gcodes = {}
-        batch = {}
 
-        def widen(k, chunks, j, eng):
+        def widen(k, j, eng):
             t0 = k * CHUNK
-            w = chunks * CHUNK
-            if j == 0:
-                pl = work.tile([P, PACK, 2 * CHUNK], BF16, name="planes", align_bytes=64)
-                for c in range(chunks):
-                    planes[k + c] = pl[:, :, c * CHUNK : (c + 1) * CHUNK]
-                planes["w", k] = pl
+            if k not in planes:
+                planes[k] = work.tile([P, PACK, CHUNK], BF16, name="planes", align_bytes=64)
             for start, width, t in x_tiles:
                 if start <= t0 < start + width:
-                    src = t[:, j, t0 - start : t0 - start + w].bitcast(FP8)
-            dst = planes["w", k][:, j, 0:w]
+                    src = t[:, j, t0 - start : t0 - start + CHUNK].bitcast(FP8)
             if eng == "s":
-                nc.scalar.activation(out=dst, in_=src, func=ACT.Copy, scale=xs[:, j : j + 1])
+                nc.scalar.activation(out=planes[k][:, j, :], in_=src, func=ACT.Copy, scale=xs[:, j : j + 1])
             else:
-                nc.vector.tensor_scalar(out=dst, in0=src, scalar1=xs[:, j : j + 1], scalar2=None, op0=ALU.mult)
+                nc.vector.tensor_scalar(out=planes[k][:, j, :], in0=src, scalar1=xs[:, j : j + 1], scalar2=None, op0=ALU.mult)
 
-        def batch_half(s, half):
-            if s not in batch:
-                nm = "batch" if s >= 2 else f"batch{s + 1}"
-                batch[s] = work.tile([P, 2, CHUNK, PACK], BF16, name=nm, bufs=1, align_bytes=64)
-            return batch[s][:, half]
-
-        def interleave(k, part, parts, eng):
-            dst_all = batch_half(k - 1, 0)
-            w = CHUNK // parts
-            dst = dst_all[:, part * w : (part + 1) * w, :]
-            src = planes[k][:, :, part * w : (part + 1) * w].rearrange("p j w -> p w j")
+        def interleave(k, eng):
+            grouped[k] = work.tile([P, CHUNK, PACK], BF16, name="grouped", bufs=2, align_bytes=64)
+            src = planes.pop(k)[:].rearrange("p j w -> p w j")
             if eng == "g":
-                nc.gpsimd.tensor_scalar(out=dst, in0=src, scalar1=1.0, scalar2=0.0, op0=ALU.mult, op1=ALU.add)
-            elif eng == "s":
-                nc.scalar.copy(out=dst, in_=src)
+                nc.gpsimd.tensor_scalar(out=grouped[k][:], in0=src, scalar1=1.0, scalar2=0.0, op0=ALU.mult, op1=ALU.add)
             else:
-                nc.vector.tensor_copy(out=dst, in_=src)
+                nc.vector.tensor_copy(out=grouped[k][:], in_=src)
 
-        def quantize_half(s, h):
-            if h == 0:
-                codes = work.tile([P, 2, CHUNK], U32, name="codes", align_bytes=64)
-                scales = work.tile([P, 2, CHUNK], U8, name="scales", align_bytes=64)
-                gcodes[s - 2] = (codes[:, 1], scales[:, 1])
-            codes, scales = gcodes[s - 2]
-            cols = slice(h * 256, (h + 1) * 256)
-            nc.vector.quantize_mx(out=codes[:, cols].bitcast(FP8X4), scales=scales[:, cols], in_=batch[s][:, 1, cols].rearrange("p w j -> p (w j)"))
+        def quantize(src, name):
+            codes = work.tile([P, CHUNK], U32, name=name + "codes", bufs=2, align_bytes=64)
+            scales = work.tile([P, CHUNK], U8, name=name + "scales", bufs=2, align_bytes=64)
+            nc.vector.quantize_mx(out=codes[:].bitcast(FP8X4), scales=scales[:], in_=src[:].rearrange("p w j -> p (w j)"))
+            return codes, scales
 
-        def quantize(s):
-            lo = 0 if s + 1 < NCHUNKS else 1
-            hi = 2 if s - 2 >= 0 else 1
-            codes = work.tile([P, 2, CHUNK], U32, name="codes", align_bytes=64)
-            scales = work.tile([P, 2, CHUNK], U8, name="scales", align_bytes=64)
-            nc.vector.quantize_mx(
-                out=codes[:, lo:hi].rearrange("p h w -> p (h w)").bitcast(FP8X4),
-                scales=scales[:, lo:hi].rearrange("p h w -> p (h w)"),
-                in_=batch.pop(s)[:, lo:hi].rearrange("p h w j -> p (h w j)"),
-            )
-            if lo == 0:
-                xcodes[s + 1] = (codes[:, 0], scales[:, 0])
-            if hi == 2:
-                gcodes[s - 2] = (codes[:, 1], scales[:, 1])
+        def quantize_x(k):
+            xcodes[k] = quantize(grouped.pop(k), "x")
 
-        warm = keep.tile([P, 1], F32, name="warm")
-        nc.vector.memset(warm[:], 1.0)
-        nc.scalar.activation(out=warm[:], in_=warm[:], func=ACT.Abs_reciprocal_sqrt)
         ident = keep.tile([P, P], F32, name="ident", align_bytes=64)
         make_identity(nc, ident[:])
+        nc.vector.memset(mrow[HALF:P, :], 0.0)
+        pcs = [keep.tile([P, 2, HALF], BF16, name=f"pieces{i}", align_bytes=64) for i in range(2)]
+        for t in pcs:
+            nc.vector.memset(t[:], 0.0)
         ident_b = keep.tile([P, P], BF16, name="ident_b", align_bytes=64)
         nc.vector.tensor_copy(out=ident_b[:], in_=ident[:])
-        sel = keep.tile([P, BLK], F32, name="sel")
-        nc.vector.tensor_reduce(out=sel[:], in_=ident[:].rearrange("p (q i) -> p i q", q=Q), axis=AXIS.X, op=ALU.add)
-        pieces = keep.tile([P, NTILES // BLK, Q, BLK], BF16, name="pieces", align_bytes=64)
-        nc.vector.memset(pieces[:], 0.0)
+        sel = keep.tile([P, NT], F32, name="sel")
+        nc.vector.tensor_reduce(out=sel[:], in_=ident[:].rearrange("p (h q i) -> p i h q", h=2, i=NT)[:, :, :, 0:PIECES], axis=AXIS.XY, op=ALU.add)
 
-        mrow32 = keep.tile([P, P], F32, name="mrow32", align_bytes=64)
-        nc.vector.tensor_copy(out=mrow32[:], in_=mrow[:])
-        m_ps = psum.tile([P, P], F32, name="m_ps", tag="tr")
-        nc.tensor.transpose(m_ps[:], mrow32[:], ident[:])
-        m = keep.tile([P, NTILES], F32, name="m")
-        nc.scalar.copy(out=m[:], in_=m_ps[:, 0:NTILES])
-        t1 = keep.tile([P, NTILES], F32, name="t1")
-        t2 = keep.tile([P, NTILES], F32, name="t2")
-        t3 = keep.tile([P, NTILES], F32, name="t3")
-        t4 = keep.tile([P, NTILES], F32, name="t4")
-        sg = keep.tile([P, NTILES], F32, name="sg")
-        inv_sg = keep.tile([P, NTILES], F32, name="inv_sg")
-        v = keep.tile([P, 2, NTILES], F32, name="v")
-        rest = [keep.tile([P, 2, NTILES], F32, name=f"rest{i}") for i in range(2)]
-
-        def g_affine(dst, src, a, b):
-            nc.gpsimd.tensor_scalar(out=dst, in0=src, scalar1=a, scalar2=b, op0=ALU.mult, op1=ALU.add)
-
-        widen(0, 1, 0, "s")
-        widen(0, 1, 1, "v")
-        widen(0, 1, 2, "v")
-        nc.vector.tensor_scalar(out=t1[:], in0=m[:], scalar1=1.4, scalar2=-1.7, op0=ALU.mult, op1=ALU.add)
-        nc.vector.tensor_scalar(out=t3[:], in0=m[:], scalar1=0.7, scalar2=None, op0=ALU.mult)
-        widen(0, 1, 3, "v")
-        nc.vector.tensor_mul(out=t2[:], in0=t1[:], in1=m[:])
-        nc.vector.tensor_mul(out=t4[:], in0=t3[:], in1=m[:])
-        interleave(0, 0, 2, "v")
-        nc.vector.tensor_scalar(out=sg[:], in0=t2[:], scalar1=1.0, scalar2=None, op0=ALU.add)
-        interleave(0, 1, 2, "v")
-        nc.vector.reciprocal(out=inv_sg[:], in_=sg[:])
-
-        wq_grouped = keep.tile([P, C, PACK], BF16, name="wq_grouped", align_bytes=64)
+        wq_grouped = keep.tile([P, PACK, TILE, PACK], BF16, name="wq_grouped", align_bytes=64)
         wq_codes = keep.tile([P, C], U32, name="wq_codes", align_bytes=64)
         wq_scales = keep.tile([P, C], U8, name="wq_scales", align_bytes=64)
 
-        def permute_wq(u, eng):
-            dst = wq_grouped[:, u * 256 : (u + 1) * 256, :].rearrange("p (m e) j -> p m e j", e=2)
-            src = wq_raw[:].rearrange("p j (m u e) -> p u m e j", u=2, e=2)[:, u]
-            if eng == "g":
-                g_affine(dst, src, 1.0, 0.0)
-            else:
-                nc.scalar.copy(out=dst, in_=src)
+        def quantize_wq(u):
+            cols = slice(u * 2 * TILE, (u + 1) * 2 * TILE)
+            nc.vector.quantize_mx(out=wq_codes[:, cols].bitcast(FP8X4), scales=wq_scales[:, cols],
+                                  in_=wq_grouped[:, 2 * u : 2 * u + 2].rearrange("p t m j -> p (t m j)"))
 
-        permute_wq(0, "s")
-        permute_wq(1, "s")
-        nc.gpsimd.tensor_mul(out=v[:, 1, :], in0=t4[:], in1=inv_sg[:])
-        quantize(-1)
-        bq = keep.tile([P, C], BF16, name="bq")
-        nc.scalar.copy(out=bq[:].rearrange("p (u m e) -> p u m e", u=2, e=2), in_=bq_raw[:].rearrange("p (m u e) -> p u m e", u=2, e=2))
+        widen(0, LAST, "s")
+        for u in range(2):
+            nc.scalar.copy(out=wq_grouped[:, 2 * u : 2 * u + 2], in_=wq_raw[:].rearrange("p j (m t) -> p t m j", t=PACK)[:, 2 * u : 2 * u + 2])
+        bq = keep.tile([P, PACK], F32, name="bq")
+        nc.scalar.copy(out=bq[:], in_=bq_raw[:])
+        for j in range(LAST):
+            widen(0, j, "v")
+        interleave(0, "v")
+        quantize_wq(0)
+        quantize_x(0)
+        quantize_wq(1)
 
-
-        def piece(i):
-            res = v if i == 0 else rest[i - 1]
-            for h in range(2):
-                src = res[:, h, :].rearrange("p (b i) -> p b i", i=BLK)
-                g_affine(pieces[:, :, 3 * h + i, :], src, 1.0, 0.0)
-                if i < 2:
-                    nc.gpsimd.tensor_sub(out=rest[i][:, h, :].rearrange("p (b i) -> p b i", i=BLK), in0=src, in1=pieces[:, :, 3 * h + i, :])
-
-        nc.vector.quantize_mx(out=wq_codes[:].bitcast(FP8X4), scales=wq_scales[:], in_=wq_grouped[:].rearrange("p w j -> p (w j)"))
-        for j in range(PACK):
-            widen(1, 1, j, "v")
-
-        q0 = {}
-        gate = {}
-        qb = {}
-        ss = {}
-        rn = {}
-        gt = {}
-        tr = {}
-        y_ps = {}
-
-        def mm1(k, i):
-            codes, scales = xcodes[k]
-            cols = slice(i * TILE, (i + 1) * TILE)
-            q0[k, i] = psum.tile([P, C], F32, name="q0")
-            nc.tensor.matmul_mx(out=q0[k, i][:], lhsT=codes[:, cols].bitcast(FP8X4), lhsT_scale=scales[:, cols],
-                                rhs=wq_codes[:].bitcast(FP8X4), rhs_scale=wq_scales[:], start=True, stop=True)
-
-        mm1(0, 0)
-        mm1(0, 1)
-
-        pt = keep.tile([P, 4, P], BF16, name="pt", align_bytes=64)
-        ptm = keep.tile([P, BLK, 4, P], BF16, name="ptm", align_bytes=64)
-
-        def turn_pieces():
-            ps = psum.tile([P, 4, P], BF16, name="pt_ps", tag="tr")
-            for b in range(4):
-                nc.tensor.transpose(ps[:, b, :], pieces[:, b].rearrange("p q i -> p (q i)"), ident_b[:])
-            nc.scalar.copy(out=pt[:], in_=ps[:])
-
-        def mask_pieces(ii):
-            nc.vector.tensor_scalar(out=ptm[:, ii], in0=pt[:], scalar1=sel[:, ii : ii + 1], scalar2=None, op0=ALU.mult)
-
-        interleave(1, 0, 2, "g")
-        interleave(1, 1, 2, "g")
-
-        kv_rows = []
-
-        def permute_rows(img):
-            r = keep.tile([P, C], BF16, name=f"kv_rows{img}", align_bytes=64)
-            nc.scalar.copy(out=r[:].rearrange("p (u m e) -> p u m e", u=2, e=2), in_=kv_raw[img][:].rearrange("p (m u e) -> p u m e", u=2, e=2))
-            kv_rows.append(r)
-
-        kcol = keep.tile([P, 4], F32, name="kcol")
-        dcol = keep.tile([P, 4], F32, name="dcol")
-
-        def take_columns():
-            ps = psum.tile([P, 4, P], BF16, name="kv_ps", tag="tr")
-            for r in range(4):
-                nc.tensor.transpose(ps[:, r, :], kv_rows[0][:, r * P : (r + 1) * P], ident_b[:])
-            nc.vector.tensor_copy(out=kcol[:], in_=ps[:, :, 0])
-            nc.vector.tensor_sub(out=dcol[:], in0=ps[:, :, 48], in1=kcol[:])
-
-        gate_t = {}
-
-        def spread_rho(todo):
-            ps = psum.tile([P, 4, TILE], F32, name="rho_ps", tag="tr")
-            for n, (k, i) in enumerate(todo):
-                t = k * NT + i
-                nc.tensor.transpose(ps[:, n, :], v[:, 1, t : t + 1].to_broadcast([P, P]), ident[:])
-            return ps
-
-        def gate_columns(todo, ps, first=0):
-            for n, (k, i) in enumerate(todo, first):
-                gate_t[k, i] = keep.tile([P, 4, TILE], F32, name=f"gate_t{k}_{i}", align_bytes=64)
-                for r in range(4):
-                    nc.scalar.activation(out=gate_t[k, i][:, r, :], in_=ps[:, n, :], func=ACT.Identity, scale=dcol[:, r : r + 1], bias=kcol[:, r : r + 1])
-
-        wo_grouped = keep.tile([P, C, PACK], BF16, name="wo_grouped", align_bytes=64)
         wo_codes = keep.tile([P, C], U32, name="wo_codes", align_bytes=64)
         wo_scales = keep.tile([P, C], U8, name="wo_scales", align_bytes=64)
+        wo_grouped = keep.tile([P, C, PACK], BF16, name="wo_grouped", align_bytes=64)
 
+        ab = keep.tile([P, 2, NTILES], F32, name="ab")
 
-        def make_gate(k, i):
-            t = k * NT + i
-            img = k // PER_IMG
-            gate[k, i] = psum.tile([P, C], F32, name="gate")
-            if (k, i) in TURNED_GATES:
-                for r in range(4):
-                    nc.tensor.transpose(gate[k, i][:, r * P : (r + 1) * P], gate_t[k, i][:, r, :], ident[:])
+        def mask_weights():
+            m_ps, tag = take(v_banks, [P, P], BF16)
+            nc.tensor.transpose(m_ps[:], mrow[:], ident_b[:])
+            inv = keep.tile([P, NTILES], F32, name="inv")
+            damp = keep.tile([P, NTILES], F32, name="damp")
+            m07 = keep.tile([P, NTILES], F32, name="m07")
+            m = m_ps[:, 0:NTILES]
+            nc.vector.tensor_scalar(out=inv[:], in0=m, scalar1=-1.0, scalar2=1.0, op0=ALU.mult, op1=ALU.add)
+            nc.vector.tensor_scalar(out=damp[:], in0=m, scalar1=-0.7, scalar2=1.0, op0=ALU.mult, op1=ALU.add)
+            nc.vector.tensor_scalar(out=m07[:], in0=m, scalar1=0.7, scalar2=None, op0=ALU.mult)
+            nc.vector.tensor_mul(out=ab[:, 0, :], in0=inv[:], in1=damp[:])
+            nc.vector.tensor_mul(out=ab[:, 1, :], in0=m, in1=m07[:])
+            v_banks.append(tag)
+
+        kv_rows = {img: keep.tile([P, NT, C], BF16, name=f"kv_rows{img}", align_bytes=64) for img in range(B)}
+
+        def by_plane(vec):
+            return vec.rearrange("p (m t) -> p t m", t=PACK)
+
+        def select_kv(img, i, eng):
+            dst = kv_rows[img][:, i, :].rearrange("p (t m) -> p t m", t=PACK)
+            if eng == "g":
+                nc.gpsimd.tensor_scalar(out=dst, in0=by_plane(kv_half[img][:]), scalar1=sel[:, i : i + 1], scalar2=0.0, op0=ALU.mult, op1=ALU.add)
             else:
-                nc.tensor.matmul(gate[k, i][:], lhsT=ptm[:, t % BLK, t // BLK, :], rhs=kv_rows[img][:], start=True, stop=True)
+                nc.vector.tensor_scalar(out=dst, in0=by_plane(kv_half[img][:]), scalar1=sel[:, i : i + 1], scalar2=None, op0=ALU.mult)
 
-        def add_bias(k, i):
-            qb[k, i] = work.tile([P, C], F32, name="qb", bufs=10)
-            nc.vector.tensor_add(out=qb[k, i][:], in0=q0.pop((k, i))[:], in1=bq[:])
+        q0 = {}
+        qb = {}
+        qt = {}
+        ss = {}
+        rs = {}
+        pw = {}
+        rest = {}
+        turned = {}
+        rows_of = {}
+        terms = {}
+        gate = {}
+        gated = {}
+        y_ps = {}
+        y_sb = {}
+
+        def is_turned(k, i):
+            return k >= FIRST_TURNED and i == LAST
+
+        def mm1(k, t):
+            codes, scales = xcodes[k]
+            cols = slice(t * TILE, (t + 1) * TILE)
+            q0[k, t] = take(s_banks, [P, CHUNK], F32)
+            nc.tensor.matmul_mx(out=q0[k, t][0][:], lhsT=wq_codes[:, cols].bitcast(FP8X4), lhsT_scale=wq_scales[:, cols],
+                                rhs=codes[:].bitcast(FP8X4), rhs_scale=scales[:], start=True, stop=True)
+
+        def add_bias(k, t):
+            if k not in qb:
+                qb[k] = work.tile([P, PACK, CHUNK], F32, name="qb", bufs=4, align_bytes=64)
+            ps, tag = q0.pop((k, t))
+            nc.scalar.activation(out=qb[k][:, t, :], in_=ps[:], func=ACT.Identity, bias=bq[:, t : t + 1])
+            s_banks.append(tag)
+
+        def turn_q(k, i):
+            qt[k, i] = take(s_banks, [P, PACK, TILE], F32)
+            for t in range(PACK):
+                nc.tensor.transpose(qt[k, i][0][:, t, :], qb[k][:, t, i * TILE : (i + 1) * TILE], ident[:])
 
         def squares(k, i):
             if k not in ss:
                 ss[k] = work.tile([P, NT], F32, name="ss")
-            t = k * NT + i
-            junk = work.tile([P, C], BF16, name="junk", bufs=8)
-            nc.scalar.activation(out=junk[:], in_=qb[k, i][:], func=ACT.Square, scale=inv_sg[:, t : t + 1], accum_out=ss[k][:, i : i + 1])
+            junk = work.tile([P, C], BF16, name="junk", bufs=NT)
+            ps, tag = qt.pop((k, i))
+            nc.scalar.activation(out=junk[:], in_=ps[:].rearrange("p t m -> p (t m)"), func=ACT.Square, accum_out=ss[k][:, i : i + 1])
+            s_banks.append(tag)
 
         def root(k):
-            rn[k] = work.tile([P, NT], F32, name="rn")
-            nc.scalar.activation(out=rn[k][:], in_=ss[k][:], func=ACT.Abs_reciprocal_sqrt)
+            rs[k] = work.tile([P, NT], F32, name="rs")
+            nc.scalar.activation(out=rs[k][:], in_=ss.pop(k)[:], func=ACT.Abs_reciprocal_sqrt)
+
+        def piece(k, q):
+            return pcs[k % 2][:, :, q * NT : (q + 1) * NT]
+
+        def split_first(k):
+            pw[k] = work.tile([P, 2, NT], F32, name="pw")
+            spread = rs[k][:].unsqueeze(1).to_broadcast([P, 2, NT])
+            weights = ab[:, :, k * NT : (k + 1) * NT]
+            nc.vector.tensor_mul(out=pw[k][:], in0=weights, in1=spread)
+            nc.vector.tensor_mul(out=piece(k, 0), in0=weights, in1=spread)
+
+        def split_second(k):
+            rest[k] = work.tile([P, 2, NT], F32, name="rest")
+            nc.vector.tensor_sub(out=rest[k][:], in0=pw[k][:], in1=piece(k, 0))
+            nc.vector.tensor_sub(out=piece(k, 1), in0=pw[k][:], in1=piece(k, 0))
+
+        def split_third(k):
+            nc.vector.tensor_sub(out=piece(k, 2), in0=rest.pop(k)[:], in1=piece(k, 1))
+
+        def weigh_last(k):
+            pw[k] = work.tile([P, 2, 1], F32, name="pt")
+            t = k * NT + LAST
+            nc.vector.tensor_scalar(out=pw[k][:], in0=ab[:, :, t : t + 1], scalar1=rs[k][:, LAST : LAST + 1], scalar2=None, op0=ALU.mult)
+
+        def turn_pieces(k):
+            turned[k] = take(s_banks, [P, P], BF16)
+            nc.tensor.transpose(turned[k][0][:], pcs[k % 2][:].rearrange("p h x -> p (h x)"), ident_b[:])
+
+        def unload_pieces(k):
+            rows_of[k] = work.tile([P, P], BF16, name="rows_of", bufs=2, align_bytes=64)
+            ps, tag = turned.pop(k)
+            nc.scalar.copy(out=rows_of[k][:], in_=ps[:])
+            s_banks.append(tag)
+
+        def gate_terms(k, eng):
+            terms[k] = work.tile([P, 2, PACK, TILE], F32, name="terms", bufs=2, align_bytes=64)
+            col = pw[k].shape[2] - 1
+            for h in range(2):
+                src = by_plane(kv_all[k // PER_IMG][:, h, :])
+                if eng == "g":
+                    nc.gpsimd.tensor_scalar(out=terms[k][:, h], in0=src, scalar1=pw[k][:, h, col : col + 1], scalar2=0.0, op0=ALU.mult, op1=ALU.add)
+                else:
+                    nc.scalar.activation(out=terms[k][:, h], in_=src, func=ACT.Copy, scale=pw[k][:, h, col : col + 1])
+
+        def make_gate(k, i, banks=v_banks):
+            gate[k, i] = take(banks, [P, PACK, TILE], F32) + (banks,)
+            ps = gate[k, i][0]
+            for t in range(PACK):
+                cols = slice(t * TILE, (t + 1) * TILE)
+                if is_turned(k, i):
+                    for h in range(2):
+                        nc.tensor.matmul(ps[:, t, :], lhsT=terms[k][:, h, t, :], rhs=ident[:], is_transpose=True, start=h == 0, stop=h == 1)
+                else:
+                    nc.tensor.matmul(ps[:, t, :], lhsT=kv_rows[k // PER_IMG][:, i, cols], rhs=rows_of[k][:], start=True, stop=True)
 
         def gating(k, i):
-            gt[k, i] = work.tile([P, C], BF16, name="gt", bufs=6, align_bytes=64)
-            nc.vector.scalar_tensor_tensor(out=gt[k, i][:], in0=gate.pop((k, i))[:], scalar=rn[k][:, i : i + 1], in1=qb.pop((k, i))[:], op0=ALU.mult, op1=ALU.mult)
+            if k not in gated:
+                gated[k] = work.tile([P, CHUNK, PACK], BF16, name="gated", bufs=2, align_bytes=64)
+            ps, tag, banks = gate.pop((k, i))
+            toks = slice(i * TILE, (i + 1) * TILE)
+            nc.vector.tensor_tensor(out=gated[k][:, toks, :].rearrange("p (c e) t -> p c t e", e=2),
+                                    in0=ps[:].rearrange("p t (c e) -> p c t e", e=2),
+                                    in1=qb[k][:, :, toks].rearrange("p t (c e) -> p c t e", e=2), op=ALU.mult)
+            banks.append(tag)
 
-        def turn(k, h):
-            tr[k, h] = psum.tile([P, 2, 2, TILE], F32, name="tr", tag="tr")
-            for a in range(2):
-                words = gt.pop((k, 2 * h + a))[:].bitcast(F32)
-                for u in range(2):
-                    nc.tensor.transpose(tr[k, h][:, a, u, :], words[:, u * 128 : (u + 1) * 128], ident[:])
+        def quantize_g(k):
+            gcodes[k] = quantize(gated.pop(k), "g")
 
-        def unload(k, h):
-            dst = batch_half(k + 2, 1).rearrange("p w j -> p (w j)").bitcast(F32)[:, h * 512 : (h + 1) * 512]
-            nc.scalar.copy(out=dst.rearrange("p (a r u) -> p a r u", a=2, u=2), in_=tr.pop((k, h))[:].rearrange("p a u r -> p a r u"))
-
-        def mm2(k, i):
+        def mm2(k, i, banks=v_banks):
             codes, scales = gcodes[k]
             cols = slice(i * TILE, (i + 1) * TILE)
-            y_ps[k, i] = psum.tile([P, C], F32, name="y_ps")
-            nc.tensor.matmul_mx(out=y_ps[k, i][:], lhsT=codes[:, cols].bitcast(FP8X4), lhsT_scale=scales[:, cols],
+            y_ps[k, i] = take(banks, [P, C], F32) + (banks,)
+            nc.tensor.matmul_mx(out=y_ps[k, i][0][:], lhsT=codes[:, cols].bitcast(FP8X4), lhsT_scale=scales[:, cols],
                                 rhs=wo_codes[:].bitcast(FP8X4), rhs_scale=wo_scales[:], start=True, stop=True)
 
-        y_sb = {}
-
         def finish(k, i, eng):
-            h = i // 2
-            if (k, h) not in y_sb:
-                y_sb[k, h] = work.tile([P, 2, C], F32, name=f"y{h}", bufs=3)
-            y = y_sb[k, h][:, i % 2, :]
-            src = y_ps.pop((k, i))
+            if k not in y_sb:
+                y_sb[k] = work.tile([P, NT, C], F32, name="y", bufs=9)
+            y = y_sb[k][:, i, :]
+            ps, tag, banks = y_ps.pop((k, i))
             if eng == "v":
-                nc.vector.tensor_add(out=y, in0=src[:], in1=bo[:])
+                nc.vector.tensor_add(out=y, in0=ps[:], in1=bo[:])
             else:
-                nc.scalar.copy(out=y, in_=src[:])
+                nc.scalar.copy(out=y, in_=ps[:])
+            banks.append(tag)
 
         def add_out(k, i):
-            y = y_sb[k, i // 2][:, i % 2, :]
-            nc.gpsimd.tensor_add(out=y, in0=y, in1=bo[:])
+            nc.gpsimd.tensor_add(out=y_sb[k][:, i, :], in0=y_sb[k][:, i, :], in1=bo[:])
 
-        def store(k, h):
-            t0 = (k * NT + 2 * h) * TILE
-            nc.sync.dma_start(out=out_rows[t0 : t0 + 2 * TILE, :].rearrange("(a p) c -> p a c", p=P), in_=y_sb.pop((k, h))[:])
-
-        def store_one(k, i):
-            t0 = (k * NT + i) * TILE
-            nc.sync.dma_start(out=out_rows[t0 : t0 + TILE, :], in_=y_sb[k, i // 2][:, i % 2, :])
+        def store(k, a0, a1):
+            t0 = (k * NT + a0) * TILE
+            nc.sync.dma_start(out=out_rows[t0 : t0 + (a1 - a0) * TILE, :].rearrange("(a p) c -> p a c", p=P), in_=y_sb[k][:, a0:a1, :])
 
         def step(s):
-            new = s < NCHUNKS
-            mid = 0 <= s - 1 < NCHUNKS
-            old = 0 <= s - 2 < NCHUNKS
-            fill = s + 2 < NCHUNKS
-            pair = s + 4 - s % 2
-            todo = [g for g in TURNED_GATES if g[0] == s]
-            if s in V_WIDENS:
-                widen(pair, 2, 3, "v")
-            if s >= 2:
-                quantize(s)
-            if s == 2:
-                nc.vector.quantize_mx(out=wo_codes[:].bitcast(FP8X4), scales=wo_scales[:], in_=wo_grouped[:].rearrange("p w j -> p (w j)"))
-            if s >= 2 and pair < NCHUNKS:
-                widen(pair, 2, 2 * (s % 2), "s")
-                if s not in V_WIDENS:
-                    widen(pair, 2, 2 * (s % 2) + 1, "s")
-            if fill and s >= 2:
-                interleave(s + 2, 0, 2, "g")
-                interleave(s + 2, 1, 2, "g")
-            if old:
-                mm2(s - 2, 0)
-                mm2(s - 2, 1)
-            if s <= 1:
-                add_bias(s, 0)
-                add_bias(s, 1)
+            mid = 1 <= s
+            old = 2 <= s
+            older = 3 <= s
+            late = s + 2 >= NCHUNKS
+            ahead = s + 1 < NCHUNKS
+            fill = s + 3 < NCHUNKS and s != 2
             if s == 0:
-                take_columns()
-                rho0 = spread_rho(todo)
-                gate_columns(todo[:2], rho0)
+                for j in range(PACK):
+                    widen(1, j, "v")
+                mask_weights()
+                interleave(1, "v")
+                for j in range(PACK):
+                    widen(2, j, "v")
+                quantize_x(1)
+                interleave(2, "v")
+                for i in range(NT):
+                    select_kv(0, i, "v")
             if mid:
-                gating(s - 1, 1)
-                gating(s - 1, 0)
-                make_gate(s - 1, 2)
-                make_gate(s - 1, 3)
-                turn(s - 1, 0)
-            by_scalar = (1,) if s in LIGHT else (1, 0)
-            if old:
-                for i in by_scalar:
-                    finish(s - 2, i, "s")
-                    add_out(s - 2, i)
-            if mid and s >= 2:
-                unload(s - 1, 0)
-            if new and s >= 2:
-                add_bias(s, 0)
-                add_bias(s, 1)
-            if new:
-                mm1(s, 2)
-                mm1(s, 3)
-                squares(s, 1)
-                squares(s, 0)
-            if s == 1:
-                unload(0, 0)
-            if s == 2:
-                turn_pieces()
-            if old and 0 not in by_scalar:
-                finish(s - 2, 0, "v")
-            if old:
-                mm2(s - 2, 2)
-                mm2(s - 2, 3)
+                split_first(s - 1)
+            if mid and ahead:
+                quantize_x(s + 1)
+            if not ahead:
+                quantize_g(s - 3)
             if mid:
-                gating(s - 1, 3)
-                gating(s - 1, 2)
-                turn(s - 1, 1)
-                unload(s - 1, 1)
-            if new:
-                add_bias(s, 3)
-                add_bias(s, 2)
-                squares(s, 3)
-                squares(s, 2)
-                root(s)
-            if s <= 1:
-                for j in range(2):
-                    widen(2 * s + 2, 2, 2 + j, "v")
-                quantize(s)
-            if s == 0:
-                for i in range(4):
-                    interleave(2 + i // 2, i % 2, 2, "g")
-                g_affine(v[:, 0, :], v[:, 1, :], -1.0, 1.0)
-                for i in range(3):
-                    piece(i)
-            if s == 2:
-                for ii in range(8, 12):
-                    mask_pieces(ii)
-            if s + 1 < NCHUNKS:
-                mm1(s + 1, 0)
-                mm1(s + 1, 1)
-            if todo:
-                if s == 0:
-                    gate_columns(todo[2:], rho0, 2)
-                else:
-                    gate_columns(todo, spread_rho(todo))
-            if new:
-                make_gate(s, 0)
-                make_gate(s, 1)
-            if s == 0:
-                widen(4, 2, 0, "s")
-                widen(4, 2, 1, "s")
-            if old:
-                for i in (3, 2):
-                    finish(s - 2, i, "v")
-                store(s - 2, 0)
-                store(s - 2, 1)
-            if s in (2, 3, 4):
-                for ii in [(12, 13, 14, 15), (0, 1, 2, 3), (4, 5, 6, 7)][s - 2]:
-                    mask_pieces(ii)
+                split_second(s - 1)
             if s == 1:
+                widen(3, 2, "v")
+                widen(3, LAST, "v")
+            if s == 2:
+                for j in range(LAST):
+                    widen(5, j, "v")
+            if older and ahead:
+                quantize_g(s - 3)
+            if not ahead:
+                gating(s - 2, 1)
+            if mid:
+                split_third(s - 1)
+            if s == 1:
+                interleave(3, "v")
                 nc.vector.tensor_copy(out=wo_grouped[:], in_=wo_raw[:].rearrange("p j w -> p w j"))
-            if s == 5:
-                permute_rows(1)
+                for i in range(NT):
+                    select_kv(1, i, "v")
+                nc.vector.quantize_mx(out=wo_codes[:].bitcast(FP8X4), scales=wo_scales[:], in_=wo_grouped[:].rearrange("p w j -> p (w j)"))
+            if old and not late:
+                widen(s + 2, LAST, "v")
+                interleave(s + 2, "g")
+            if late:
+                weigh_last(s - 1)
+            if s - 1 >= FIRST_TURNED:
+                gate_terms(s - 1, "g")
+            for t in (2, 1, 0, 3):
+                add_bias(s, t)
+            if fill:
+                widen(s + 3, 0, "s")
+                widen(s + 3, 1, "s")
+            if late:
+                if ahead:
+                    gating(s - 2, 1)
+                mm2(s - 3, 0)
+            for i in range(NT):
+                turn_q(s, i)
+            if late:
+                finish(s - 3, 0, "s")
+                add_out(s - 3, 0)
+            if old:
+                if not late:
+                    gating(s - 2, 1)
+                gating(s - 2, 0)
+            if older:
+                if not late:
+                    mm2(s - 3, 0)
+                mm2(s - 3, 1)
+            if old:
+                gating(s - 2, 3)
+                gating(s - 2, 2)
+            squares(s, 1)
+            squares(s, 0)
+            if older:
+                mm2(s - 3, 2)
+                mm2(s - 3, 3)
+            if mid:
+                turn_pieces(s - 1)
+            if ahead:
+                mm1(s + 1, 0)
+            squares(s, 3)
+            squares(s, 2)
+            if ahead:
+                mm1(s + 1, 1)
+                mm1(s + 1, 2)
+            if mid:
+                unload_pieces(s - 1)
+            if ahead:
+                mm1(s + 1, 3)
+            if fill and mid:
+                widen(s + 3, 2, "s")
+            root(s)
+            if older:
+                finish(s - 3, 1, "v")
+                if not late:
+                    finish(s - 3, 0, "v")
+                finish(s - 3, 3, "v")
+                finish(s - 3, 2, "v")
+                store(s - 3, 0, NT)
+            if mid:
+                for i in range(NT):
+                    make_gate(s - 1, i)
 
-        def last_steps():
+        def drain():
             k = NCHUNKS - 1
-            s = NCHUNKS
-            quantize(s)
-            mm2(k - 1, 0)
-            mm2(k - 1, 1)
+            split_first(k)
+            quantize_g(k - 2)
+            split_second(k)
+            gating(k - 1, 1)
+            split_third(k)
+            for i in range(3):
+                mm2(k - 2, i, s_banks)
+            turn_pieces(k)
+            finish(k - 2, 0, "s")
+            add_out(k - 2, 0)
+            unload_pieces(k)
+            finish(k - 2, 1, "s")
+            add_out(k - 2, 1)
+            gate_terms(k, "s")
+            mm2(k - 2, 3, s_banks)
+            gating(k - 1, 0)
+            gating(k - 1, 3)
+            gating(k - 1, 2)
+            for i in range(NT):
+                make_gate(k, i)
+            finish(k - 2, 3, "v")
+            finish(k - 2, 2, "v")
+            store(k - 2, 0, NT)
+            quantize_g(k - 1)
+            for i in range(NT):
+                mm2(k - 1, i, s_banks)
+            finish(k - 1, 0, "s")
+            add_out(k - 1, 0)
+            finish(k - 1, 1, "s")
             gating(k, 1)
             gating(k, 0)
-            make_gate(k, 2)
-            make_gate(k, 3)
-            turn(k, 0)
-            finish(k - 1, 1, "s")
-            add_out(k - 1, 1)
-            unload(k, 0)
-            finish(k - 1, 0, "v")
-            store(k - 1, 0)
-            mm2(k - 1, 2)
-            mm2(k - 1, 3)
             gating(k, 3)
             gating(k, 2)
-            turn(k, 1)
-            unload(k, 1)
-            quantize_half(s + 1, 0)
-            mm2(k, 0)
-            mm2(k, 1)
-            finish(k - 1, 3, "v")
             finish(k - 1, 2, "v")
-            store(k - 1, 1)
-            quantize_half(s + 1, 1)
-            finish(k, 0, "s")
-            add_out(k, 0)
+            quantize_g(k)
+            add_out(k - 1, 1)
+            for i in range(NT):
+                mm2(k, i)
+            finish(k - 1, 3, "v")
+            store(k - 1, 2, NT)
+            finish(k, 0, "v")
+            store(k - 1, 0, 2)
             finish(k, 1, "v")
-            mm2(k, 2)
-            mm2(k, 3)
-            store_one(k, 1)
+            store(k, 0, 2)
             finish(k, 2, "v")
-            store_one(k, 0)
+            store(k, 2, 3)
             finish(k, 3, "v")
-            store_one(k, 2)
-            store_one(k, 3)
+            store(k, 3, 4)
 
-        permute_rows(0)
-        widen(2, 2, 0, "s")
-        widen(2, 2, 1, "s")
+        for t in range(PACK):
+            mm1(0, t)
         for s in range(NCHUNKS):
             step(s)
-        last_steps()
+        drain()

@@ -30,8 +30,9 @@ PIECES = 3
 FLOPS = 2 * 2 * B * N * C * C
 
 X_LOADS = ((0, 0, 512), (0, 512, 512), (0, 1024, 1024), (0, 2048, 2048), (1, 0, 2048), (1, 2048, 2048))
-FIRST_TURNED = 3
+TURNED = range(2, 15)
 LAST = NT - 1
+PLANE_ORDER = (1, 0, 3, 2)
 
 
 def tile_hydraattention_pb_t_kernel(tc, x_bytes, x_scale, mask, W_q, b_q, kv_know, kv_mask, W_out, b_out, out):
@@ -87,7 +88,7 @@ def tile_hydraattention_pb_t_kernel(tc, x_bytes, x_scale, mask, W_q, b_q, kv_kno
         wo_raw = keep.tile([P, PACK, C], BF16, name="wo_raw")
         nc.sync.dma_start(out=wo_raw[:], in_=W_out.rearrange("(p j) w -> p j w", j=PACK))
         load_x(3)
-        bo = keep.tile([P, C], BF16, name="bo")
+        bo = keep.tile([P, C], BF16, name="bo", align_bytes=64)
         nc.sync.dma_start(out=bo[:], in_=b_out.partition_broadcast(P))
         load_kv_half(1)
         load_kv_all(0)
@@ -165,6 +166,7 @@ def tile_hydraattention_pb_t_kernel(tc, x_bytes, x_scale, mask, W_q, b_q, kv_kno
         wo_scales = keep.tile([P, C], U8, name="wo_scales", align_bytes=64)
         wo_grouped = keep.tile([P, C, PACK], BF16, name="wo_grouped", align_bytes=64)
 
+        bo_cols = keep.tile([P, PACK], F32, name="bo_cols")
         ab = keep.tile([P, 2, NTILES], F32, name="ab")
 
         def mask_weights():
@@ -196,6 +198,7 @@ def tile_hydraattention_pb_t_kernel(tc, x_bytes, x_scale, mask, W_q, b_q, kv_kno
         q0 = {}
         qb = {}
         qt = {}
+        q_turned = set()
         ss = {}
         rs = {}
         pw = {}
@@ -209,7 +212,7 @@ def tile_hydraattention_pb_t_kernel(tc, x_bytes, x_scale, mask, W_q, b_q, kv_kno
         y_sb = {}
 
         def is_turned(k, i):
-            return k >= FIRST_TURNED and i == LAST
+            return k in TURNED and i == LAST
 
         def mm1(k, t):
             codes, scales = xcodes[k]
@@ -225,10 +228,14 @@ def tile_hydraattention_pb_t_kernel(tc, x_bytes, x_scale, mask, W_q, b_q, kv_kno
             nc.scalar.activation(out=qb[k][:, t, :], in_=ps[:], func=ACT.Identity, bias=bq[:, t : t + 1])
             s_banks.append(tag)
 
-        def turn_q(k, i):
-            qt[k, i] = take(s_banks, [P, PACK, TILE], F32)
-            for t in range(PACK):
-                nc.tensor.transpose(qt[k, i][0][:, t, :], qb[k][:, t, i * TILE : (i + 1) * TILE], ident[:])
+        def turn_q(k, planes_done, tiles):
+            for i in tiles:
+                if (k, i) not in qt:
+                    qt[k, i] = take(s_banks, [P, PACK, TILE], F32)
+                for t in planes_done:
+                    if (k, i, t) not in q_turned:
+                        q_turned.add((k, i, t))
+                        nc.tensor.transpose(qt[k, i][0][:, t, :], qb[k][:, t, i * TILE : (i + 1) * TILE], ident[:])
 
         def squares(k, i):
             if k not in ss:
@@ -327,6 +334,44 @@ def tile_hydraattention_pb_t_kernel(tc, x_bytes, x_scale, mask, W_q, b_q, kv_kno
                 nc.scalar.copy(out=y, in_=ps[:])
             banks.append(tag)
 
+        y_turned = {}
+
+        def mm2_turned(k, i0, banks):
+            codes, scales = gcodes[k]
+            toks = slice(i0 * TILE, (i0 + 2) * TILE)
+            held = []
+            for u in range(2):
+                ps, tag = take(banks, [P, 2, 2 * TILE], F32)
+                held.append((ps, tag, banks))
+                for e in range(2):
+                    cols = slice((2 * u + e) * TILE, (2 * u + e + 1) * TILE)
+                    nc.tensor.matmul_mx(out=ps[:, e, :], lhsT=wo_codes[:, cols].bitcast(FP8X4), lhsT_scale=wo_scales[:, cols],
+                                        rhs=codes[:, toks].bitcast(FP8X4), rhs_scale=scales[:, toks], start=True, stop=True)
+            y_turned[k, i0] = held
+
+        def bias_turned(k, i0):
+            yt = work.tile([P, PACK, 2 * TILE], F32, name="yt", bufs=2, align_bytes=64)
+            for u, (ps, tag, banks) in enumerate(y_turned[k, i0]):
+                for e in range(2):
+                    j = 2 * u + e
+                    nc.scalar.activation(out=yt[:, j, :], in_=ps[:, e, :], func=ACT.Identity, bias=bo_cols[:, j : j + 1])
+                banks.append(tag)
+            y_turned[k, i0] = yt
+
+        def turn_back(k, i0, banks):
+            yt = y_turned.pop((k, i0))
+            for a in range(2):
+                y_ps[k, i0 + a] = take(banks, [P, C], F32) + (banks,)
+                for j in range(PACK):
+                    nc.tensor.transpose(y_ps[k, i0 + a][0][:, j * TILE : (j + 1) * TILE], yt[:, j, a * TILE : (a + 1) * TILE], ident[:])
+
+        def turn_bo():
+            ps, tag = take(v_banks, [P, PACK, TILE], BF16)
+            for j in range(PACK):
+                nc.tensor.transpose(ps[:, j, :], bo[:, j * TILE : (j + 1) * TILE], ident_b[:])
+            nc.vector.tensor_copy(out=bo_cols[:], in_=ps[:, :, 0])
+            v_banks.append(tag)
+
         def add_out(k, i):
             nc.gpsimd.tensor_add(out=y_sb[k][:, i, :], in0=y_sb[k][:, i, :], in1=bo[:])
 
@@ -340,7 +385,7 @@ def tile_hydraattention_pb_t_kernel(tc, x_bytes, x_scale, mask, W_q, b_q, kv_kno
             older = 3 <= s
             late = s + 2 >= NCHUNKS
             ahead = s + 1 < NCHUNKS
-            fill = s + 3 < NCHUNKS and s != 2
+            fill = s + 3 < NCHUNKS
             if s == 0:
                 for j in range(PACK):
                     widen(1, j, "v")
@@ -352,75 +397,87 @@ def tile_hydraattention_pb_t_kernel(tc, x_bytes, x_scale, mask, W_q, b_q, kv_kno
                 interleave(2, "v")
                 for i in range(NT):
                     select_kv(0, i, "v")
+            if late:
+                quantize_g(s - 3)
             if mid:
                 split_first(s - 1)
             if mid and ahead:
                 quantize_x(s + 1)
             if not ahead:
-                quantize_g(s - 3)
+                gating(s - 2, 0)
             if mid:
                 split_second(s - 1)
             if s == 1:
                 widen(3, 2, "v")
-                widen(3, LAST, "v")
             if s == 2:
-                for j in range(LAST):
-                    widen(5, j, "v")
-            if older and ahead:
-                quantize_g(s - 3)
-            if not ahead:
-                gating(s - 2, 1)
+                widen(5, 1, "v")
+                widen(5, 2, "v")
+            if mid and not late:
+                widen(s + 2, LAST, "v")
+            if late:
+                make_gate(s - 2, LAST)
+                gating(s - 2, LAST if not ahead else 0)
             if mid:
                 split_third(s - 1)
+            if older and not late:
+                quantize_g(s - 3)
             if s == 1:
                 interleave(3, "v")
                 nc.vector.tensor_copy(out=wo_grouped[:], in_=wo_raw[:].rearrange("p j w -> p w j"))
-                for i in range(NT):
-                    select_kv(1, i, "v")
+                widen(4, 2, "v")
                 nc.vector.quantize_mx(out=wo_codes[:].bitcast(FP8X4), scales=wo_scales[:], in_=wo_grouped[:].rearrange("p w j -> p (w j)"))
+                turn_bo()
+                select_kv(1, 0, "v")
+                select_kv(1, 1, "v")
             if old and not late:
-                widen(s + 2, LAST, "v")
                 interleave(s + 2, "g")
             if late:
                 weigh_last(s - 1)
-            if s - 1 >= FIRST_TURNED:
+            if s - 1 in TURNED:
                 gate_terms(s - 1, "g")
-            for t in (2, 1, 0, 3):
+            if old and not late:
+                make_gate(s - 2, LAST)
+            order = PLANE_ORDER if mid else tuple(range(PACK))
+            for n, t in enumerate(order):
                 add_bias(s, t)
+                if late and n == 0:
+                    mm2(s - 3, 2, s_banks)
+                else:
+                    turn_q(s, order[: n + 1], range(n if late else n + 1))
+                if old and n < 2:
+                    make_gate(s - 2, n + 1)
+            if late:
+                finish(s - 3, 2, "s")
+                add_out(s - 3, 2)
+                turn_q(s, order, [LAST])
             if fill:
                 widen(s + 3, 0, "s")
-                widen(s + 3, 1, "s")
-            if late:
-                if ahead:
-                    gating(s - 2, 1)
-                mm2(s - 3, 0)
-            for i in range(NT):
-                turn_q(s, i)
-            if late:
-                finish(s - 3, 0, "s")
-                add_out(s - 3, 0)
+                if s != 2:
+                    widen(s + 3, 1, "s")
             if old:
+                gating(s - 2, 1)
                 if not late:
-                    gating(s - 2, 1)
-                gating(s - 2, 0)
+                    gating(s - 2, 0)
             if older:
-                if not late:
-                    mm2(s - 3, 0)
+                mm2(s - 3, 0)
                 mm2(s - 3, 1)
             if old:
-                gating(s - 2, 3)
+                if ahead:
+                    gating(s - 2, 3)
                 gating(s - 2, 2)
-            squares(s, 1)
-            squares(s, 0)
-            if older:
+            order = (3, 2, 1, 0) if fill and s != 2 else (1, 0, 3, 2)
+            squares(s, order[0])
+            squares(s, order[1])
+            if older and not late:
                 mm2(s - 3, 2)
-                mm2(s - 3, 3)
             if mid:
                 turn_pieces(s - 1)
+            if older:
+                mm2(s - 3, 3)
             if ahead:
                 mm1(s + 1, 0)
-            squares(s, 3)
-            squares(s, 2)
+            squares(s, order[2])
+            squares(s, order[3])
             if ahead:
                 mm1(s + 1, 1)
                 mm1(s + 1, 2)
@@ -428,70 +485,85 @@ def tile_hydraattention_pb_t_kernel(tc, x_bytes, x_scale, mask, W_q, b_q, kv_kno
                 unload_pieces(s - 1)
             if ahead:
                 mm1(s + 1, 3)
-            if fill and mid:
+            if fill and older:
                 widen(s + 3, 2, "s")
             root(s)
+            if s == 2:
+                select_kv(1, 2, "v")
+                select_kv(1, 3, "v")
             if older:
                 finish(s - 3, 1, "v")
-                if not late:
-                    finish(s - 3, 0, "v")
+                finish(s - 3, 0, "v")
                 finish(s - 3, 3, "v")
-                finish(s - 3, 2, "v")
+                if not late:
+                    finish(s - 3, 2, "v")
                 store(s - 3, 0, NT)
             if mid:
-                for i in range(NT):
-                    make_gate(s - 1, i)
+                make_gate(s - 1, 0)
+
+        def quantize_half(k, h):
+            if h == 0:
+                codes = work.tile([P, CHUNK], U32, name="gcodes", bufs=2, align_bytes=64)
+                scales = work.tile([P, CHUNK], U8, name="gscales", bufs=2, align_bytes=64)
+                gcodes[k] = (codes, scales)
+            codes, scales = gcodes[k]
+            cols = slice(h * 2 * TILE, (h + 1) * 2 * TILE)
+            nc.vector.quantize_mx(out=codes[:, cols].bitcast(FP8X4), scales=scales[:, cols], in_=gated[k][:, cols, :].rearrange("p w j -> p (w j)"))
 
         def drain():
             k = NCHUNKS - 1
-            split_first(k)
+            for i in (LAST, 1, 2):
+                make_gate(k - 1, i)
             quantize_g(k - 2)
+            split_first(k)
+            gating(k - 1, 0)
             split_second(k)
-            gating(k - 1, 1)
+            gating(k - 1, LAST)
             split_third(k)
-            for i in range(3):
-                mm2(k - 2, i, s_banks)
+            mm2(k - 2, 1, s_banks)
+            mm2_turned(k - 2, 2, s_banks)
             turn_pieces(k)
-            finish(k - 2, 0, "s")
-            add_out(k - 2, 0)
-            unload_pieces(k)
+            mm2(k - 2, 0)
             finish(k - 2, 1, "s")
             add_out(k - 2, 1)
-            gate_terms(k, "s")
-            mm2(k - 2, 3, s_banks)
-            gating(k - 1, 0)
-            gating(k - 1, 3)
+            unload_pieces(k)
+            bias_turned(k - 2, 2)
             gating(k - 1, 2)
-            for i in range(NT):
+            gating(k - 1, 1)
+            for i in (0, 1, LAST):
                 make_gate(k, i)
-            finish(k - 2, 3, "v")
-            finish(k - 2, 2, "v")
-            store(k - 2, 0, NT)
+            turn_back(k - 2, 2, s_banks)
+            finish(k - 2, 0, "v")
+            make_gate(k, 2)
             quantize_g(k - 1)
-            for i in range(NT):
-                mm2(k - 1, i, s_banks)
-            finish(k - 1, 0, "s")
-            add_out(k - 1, 0)
-            finish(k - 1, 1, "s")
+            store(k - 2, 0, 2)
+            mm2_turned(k - 1, 2, s_banks)
+            finish(k - 2, 2, "s")
+            finish(k - 2, 3, "s")
+            store(k - 2, 2, NT)
+            bias_turned(k - 1, 2)
             gating(k, 1)
             gating(k, 0)
+            mm2(k - 1, 0)
+            mm2(k - 1, 1)
+            turn_back(k - 1, 2, s_banks)
             gating(k, 3)
+            for i in (0, 1):
+                finish(k - 1, i, "v")
+                store(k - 1, i, i + 1)
+            quantize_half(k, 0)
+            mm2(k, 0)
+            mm2(k, 1)
+            for i in (2, 3):
+                finish(k - 1, i, "s")
+                store(k - 1, i, i + 1)
             gating(k, 2)
-            finish(k - 1, 2, "v")
-            quantize_g(k)
-            add_out(k - 1, 1)
+            quantize_half(k, 1)
+            mm2(k, 2)
+            mm2(k, 3)
             for i in range(NT):
-                mm2(k, i)
-            finish(k - 1, 3, "v")
-            store(k - 1, 2, NT)
-            finish(k, 0, "v")
-            store(k - 1, 0, 2)
-            finish(k, 1, "v")
-            store(k, 0, 2)
-            finish(k, 2, "v")
-            store(k, 2, 3)
-            finish(k, 3, "v")
-            store(k, 3, 4)
+                finish(k, i, "v")
+                store(k, i, i + 1)
 
         for t in range(PACK):
             mm1(0, t)

@@ -26,11 +26,12 @@ NTILES = B * N // TILE
 NCHUNKS = B * N // CHUNK
 PER_IMG = N // CHUNK
 PIECES = 3
+RUN = 4
 
 FLOPS = 2 * 2 * B * N * C * C
 
 X_LOADS = ((0, 0, 512), (0, 512, 512), (0, 1024, 1024), (0, 2048, 2048), (1, 0, 2048), (1, 2048, 2048))
-TURNED = range(2, 15)
+TURNED = range(1, 14)
 LAST = NT - 1
 PLANE_ORDER = (1, 0, 3, 2)
 
@@ -104,7 +105,7 @@ def tile_hydraattention_pb_t_kernel(tc, x_bytes, x_scale, mask, W_q, b_q, kv_kno
         def widen(k, j, eng):
             t0 = k * CHUNK
             if k not in planes:
-                planes[k] = work.tile([P, PACK, CHUNK], BF16, name="planes", align_bytes=64)
+                planes[k] = work.tile([P, PACK, CHUNK], BF16, name="planes", bufs=4, align_bytes=64)
             for start, width, t in x_tiles:
                 if start <= t0 < start + width:
                     src = t[:, j, t0 - start : t0 - start + CHUNK].bitcast(FP8)
@@ -115,11 +116,11 @@ def tile_hydraattention_pb_t_kernel(tc, x_bytes, x_scale, mask, W_q, b_q, kv_kno
 
         def interleave(k, eng):
             grouped[k] = work.tile([P, CHUNK, PACK], BF16, name="grouped", bufs=2, align_bytes=64)
-            src = planes.pop(k)[:].rearrange("p j w -> p w j")
+            src = planes.pop(k)[:]
             if eng == "g":
-                nc.gpsimd.tensor_scalar(out=grouped[k][:], in0=src, scalar1=1.0, scalar2=0.0, op0=ALU.mult, op1=ALU.add)
+                nc.gpsimd.tensor_scalar(out=grouped[k][:], in0=src.rearrange("p j w -> p w j"), scalar1=1.0, scalar2=0.0, op0=ALU.mult, op1=ALU.add)
             else:
-                nc.vector.tensor_copy(out=grouped[k][:], in_=src)
+                nc.vector.tensor_copy(out=grouped[k][:].rearrange("p (c e) j -> p c j e", e=RUN), in_=src.rearrange("p j (c e) -> p c j e", e=RUN))
 
         def quantize(src, name):
             codes = work.tile([P, CHUNK], U32, name=name + "codes", bufs=2, align_bytes=64)
@@ -152,7 +153,8 @@ def tile_hydraattention_pb_t_kernel(tc, x_bytes, x_scale, mask, W_q, b_q, kv_kno
 
         widen(0, LAST, "s")
         for u in range(2):
-            nc.scalar.copy(out=wq_grouped[:, 2 * u : 2 * u + 2], in_=wq_raw[:].rearrange("p j (m t) -> p t m j", t=PACK)[:, 2 * u : 2 * u + 2])
+            nc.scalar.copy(out=wq_grouped[:, 2 * u : 2 * u + 2].rearrange("p t m j -> p m j t"),
+                           in_=wq_raw[:].rearrange("p j (m t) -> p m j t", t=PACK)[:, :, :, 2 * u : 2 * u + 2])
         bq = keep.tile([P, PACK], F32, name="bq")
         nc.scalar.copy(out=bq[:], in_=bq_raw[:])
         for j in range(LAST):
@@ -188,12 +190,16 @@ def tile_hydraattention_pb_t_kernel(tc, x_bytes, x_scale, mask, W_q, b_q, kv_kno
         def by_plane(vec):
             return vec.rearrange("p (m t) -> p t m", t=PACK)
 
-        def select_kv(img, i, eng):
-            dst = kv_rows[img][:, i, :].rearrange("p (t m) -> p t m", t=PACK)
-            if eng == "g":
-                nc.gpsimd.tensor_scalar(out=dst, in0=by_plane(kv_half[img][:]), scalar1=sel[:, i : i + 1], scalar2=0.0, op0=ALU.mult, op1=ALU.add)
-            else:
-                nc.vector.tensor_scalar(out=dst, in0=by_plane(kv_half[img][:]), scalar1=sel[:, i : i + 1], scalar2=None, op0=ALU.mult)
+        kv_planes = {}
+
+        def permute_kv(img):
+            kv_planes[img] = keep.tile([P, PACK, TILE], BF16, name=f"kv_planes{img}", align_bytes=64)
+            nc.vector.tensor_copy(out=kv_planes[img][:], in_=by_plane(kv_half[img][:]))
+
+        def select_kv(img):
+            for i in range(NT):
+                nc.vector.tensor_scalar(out=kv_rows[img][:, i, :], in0=kv_planes[img][:].rearrange("p t m -> p (t m)"),
+                                        scalar1=sel[:, i : i + 1], scalar2=None, op0=ALU.mult)
 
         q0 = {}
         qb = {}
@@ -272,25 +278,22 @@ def tile_hydraattention_pb_t_kernel(tc, x_bytes, x_scale, mask, W_q, b_q, kv_kno
             t = k * NT + LAST
             nc.vector.tensor_scalar(out=pw[k][:], in0=ab[:, :, t : t + 1], scalar1=rs[k][:, LAST : LAST + 1], scalar2=None, op0=ALU.mult)
 
-        def turn_pieces(k):
-            turned[k] = take(s_banks, [P, P], BF16)
+        def turn_pieces(k, banks=s_banks):
+            turned[k] = take(banks, [P, P], BF16) + (banks,)
             nc.tensor.transpose(turned[k][0][:], pcs[k % 2][:].rearrange("p h x -> p (h x)"), ident_b[:])
 
         def unload_pieces(k):
             rows_of[k] = work.tile([P, P], BF16, name="rows_of", bufs=2, align_bytes=64)
-            ps, tag = turned.pop(k)
+            ps, tag, banks = turned.pop(k)
             nc.scalar.copy(out=rows_of[k][:], in_=ps[:])
-            s_banks.append(tag)
+            banks.append(tag)
 
-        def gate_terms(k, eng):
+        def gate_terms(k):
             terms[k] = work.tile([P, 2, PACK, TILE], F32, name="terms", bufs=2, align_bytes=64)
             col = pw[k].shape[2] - 1
             for h in range(2):
                 src = by_plane(kv_all[k // PER_IMG][:, h, :])
-                if eng == "g":
-                    nc.gpsimd.tensor_scalar(out=terms[k][:, h], in0=src, scalar1=pw[k][:, h, col : col + 1], scalar2=0.0, op0=ALU.mult, op1=ALU.add)
-                else:
-                    nc.scalar.activation(out=terms[k][:, h], in_=src, func=ACT.Copy, scale=pw[k][:, h, col : col + 1])
+                nc.gpsimd.tensor_scalar(out=terms[k][:, h], in0=src, scalar1=pw[k][:, h, col : col + 1], scalar2=0.0, op0=ALU.mult, op1=ALU.add)
 
         def make_gate(k, i, banks=v_banks):
             gate[k, i] = take(banks, [P, PACK, TILE], F32) + (banks,)
@@ -325,7 +328,7 @@ def tile_hydraattention_pb_t_kernel(tc, x_bytes, x_scale, mask, W_q, b_q, kv_kno
 
         def finish(k, i, eng):
             if k not in y_sb:
-                y_sb[k] = work.tile([P, NT, C], F32, name="y", bufs=9)
+                y_sb[k] = work.tile([P, NT, C], F32, name="y", bufs=8)
             y = y_sb[k][:, i, :]
             ps, tag, banks = y_ps.pop((k, i))
             if eng == "v":
@@ -379,13 +382,22 @@ def tile_hydraattention_pb_t_kernel(tc, x_bytes, x_scale, mask, W_q, b_q, kv_kno
             t0 = (k * NT + a0) * TILE
             nc.sync.dma_start(out=out_rows[t0 : t0 + (a1 - a0) * TILE, :].rearrange("(a p) c -> p a c", p=P), in_=y_sb[k][:, a0:a1, :])
 
+        def empty_q(s, gates):
+            order = PLANE_ORDER if s else tuple(range(PACK))
+            for n, t in enumerate(order):
+                add_bias(s, t)
+                turn_q(s, order[: n + 1], range(n + 1))
+                if n < len(gates):
+                    make_gate(s - 2, gates[n])
+
         def step(s):
             mid = 1 <= s
             old = 2 <= s
             older = 3 <= s
             late = s + 2 >= NCHUNKS
-            ahead = s + 1 < NCHUNKS
             fill = s + 3 < NCHUNKS
+            held = late
+            hold = not fill
             if s == 0:
                 for j in range(PACK):
                     widen(1, j, "v")
@@ -395,109 +407,94 @@ def tile_hydraattention_pb_t_kernel(tc, x_bytes, x_scale, mask, W_q, b_q, kv_kno
                     widen(2, j, "v")
                 quantize_x(1)
                 interleave(2, "v")
-                for i in range(NT):
-                    select_kv(0, i, "v")
-            if late:
-                quantize_g(s - 3)
             if mid:
                 split_first(s - 1)
-            if mid and ahead:
                 quantize_x(s + 1)
-            if not ahead:
-                gating(s - 2, 0)
-            if mid:
                 split_second(s - 1)
             if s == 1:
-                widen(3, 2, "v")
+                nc.vector.tensor_copy(out=wo_grouped[:].rearrange("p (c e) j -> p c j e", e=RUN), in_=wo_raw[:].rearrange("p j (c e) -> p c j e", e=RUN))
             if s == 2:
-                widen(5, 1, "v")
-                widen(5, 2, "v")
-            if mid and not late:
+                interleave(4, "v")
+            if older and not late:
                 widen(s + 2, LAST, "v")
             if late:
-                make_gate(s - 2, LAST)
-                gating(s - 2, LAST if not ahead else 0)
+                quantize_g(s - 3)
             if mid:
                 split_third(s - 1)
             if older and not late:
                 quantize_g(s - 3)
             if s == 1:
-                interleave(3, "v")
-                nc.vector.tensor_copy(out=wo_grouped[:], in_=wo_raw[:].rearrange("p j w -> p w j"))
+                select_kv(0)
+                widen(4, 1, "v")
                 widen(4, 2, "v")
+                widen(4, LAST, "v")
+                permute_kv(1)
                 nc.vector.quantize_mx(out=wo_codes[:].bitcast(FP8X4), scales=wo_scales[:], in_=wo_grouped[:].rearrange("p w j -> p (w j)"))
                 turn_bo()
-                select_kv(1, 0, "v")
-                select_kv(1, 1, "v")
-            if old and not late:
+                widen(5, 1, "v")
+                widen(5, 2, "v")
+            if older and not late:
                 interleave(s + 2, "g")
-            if late:
+            if late or s == 2:
                 weigh_last(s - 1)
-            if s - 1 in TURNED:
-                gate_terms(s - 1, "g")
-            if old and not late:
+            if old:
+                gate_terms(s - 1)
+            if old:
                 make_gate(s - 2, LAST)
-            order = PLANE_ORDER if mid else tuple(range(PACK))
-            for n, t in enumerate(order):
-                add_bias(s, t)
-                if late and n == 0:
-                    mm2(s - 3, 2, s_banks)
-                else:
-                    turn_q(s, order[: n + 1], range(n if late else n + 1))
-                if old and n < 2:
-                    make_gate(s - 2, n + 1)
-            if late:
-                finish(s - 3, 2, "s")
-                add_out(s - 3, 2)
-                turn_q(s, order, [LAST])
+            empty_q(s, () if not old else ((1,) if held else (1, 2)))
+            if held:
+                finish(s - 4, LAST, "s")
+                make_gate(s - 2, 2)
+                add_out(s - 4, LAST)
+                store(s - 4, LAST, NT)
             if fill:
                 widen(s + 3, 0, "s")
-                if s != 2:
+                if older:
                     widen(s + 3, 1, "s")
+            if s == 0:
+                widen(3, 1, "v")
+                widen(3, 2, "v")
+                widen(3, LAST, "v")
+                permute_kv(0)
+                interleave(3, "v")
             if old:
                 gating(s - 2, 1)
-                if not late:
-                    gating(s - 2, 0)
+                gating(s - 2, 0)
             if older:
                 mm2(s - 3, 0)
                 mm2(s - 3, 1)
             if old:
-                if ahead:
-                    gating(s - 2, 3)
+                gating(s - 2, 3)
                 gating(s - 2, 2)
-            order = (3, 2, 1, 0) if fill and s != 2 else (1, 0, 3, 2)
+            order = (3, 2, 1, 0) if fill and older else (1, 0, 3, 2)
             squares(s, order[0])
             squares(s, order[1])
-            if older and not late:
+            if older:
                 mm2(s - 3, 2)
             if mid:
                 turn_pieces(s - 1)
             if older:
                 mm2(s - 3, 3)
-            if ahead:
-                mm1(s + 1, 0)
+            mm1(s + 1, 0)
             squares(s, order[2])
             squares(s, order[3])
-            if ahead:
-                mm1(s + 1, 1)
-                mm1(s + 1, 2)
+            mm1(s + 1, 1)
+            mm1(s + 1, 2)
             if mid:
                 unload_pieces(s - 1)
-            if ahead:
-                mm1(s + 1, 3)
+            mm1(s + 1, 3)
             if fill and older:
                 widen(s + 3, 2, "s")
             root(s)
-            if s == 2:
-                select_kv(1, 2, "v")
-                select_kv(1, 3, "v")
+            if s == 1:
+                select_kv(1)
             if older:
                 finish(s - 3, 1, "v")
                 finish(s - 3, 0, "v")
-                finish(s - 3, 3, "v")
-                if not late:
-                    finish(s - 3, 2, "v")
-                store(s - 3, 0, NT)
+                if not hold:
+                    finish(s - 3, LAST, "v")
+                finish(s - 3, 2, "v")
+                store(s - 3, 0, LAST if hold else NT)
             if mid:
                 make_gate(s - 1, 0)
 
@@ -512,45 +509,77 @@ def tile_hydraattention_pb_t_kernel(tc, x_bytes, x_scale, mask, W_q, b_q, kv_kno
 
         def drain():
             k = NCHUNKS - 1
-            for i in (LAST, 1, 2):
-                make_gate(k - 1, i)
+            make_gate(k - 2, LAST)
+            quantize_g(k - 3)
+            split_first(k - 1)
+            gating(k - 2, 0)
+            split_second(k - 1)
+            gating(k - 2, LAST)
+            split_third(k - 1)
+            empty_q(k, (1, 2))
+            mm2(k - 3, 0)
+            finish(k - 4, LAST, "s")
+            add_out(k - 4, LAST)
+            store(k - 4, LAST, NT)
+            turn_pieces(k - 1, v_banks)
+            gating(k - 2, 1)
+            mm2(k - 3, 1)
+            squares(k, 1)
+            squares(k, 0)
+            unload_pieces(k - 1)
+            make_gate(k - 1, 0)
+            gating(k - 2, 2)
+            make_gate(k - 1, 1)
+            squares(k, 3)
+            squares(k, 2)
+            root(k)
+            finish(k - 3, 0, "v")
+            make_gate(k - 1, LAST)
+            finish(k - 3, 1, "v")
+            make_gate(k - 1, 2)
+            store(k - 3, 0, 2)
+            mm2_turned(k - 3, 2, s_banks)
             quantize_g(k - 2)
-            split_first(k)
-            gating(k - 1, 0)
-            split_second(k)
-            gating(k - 1, LAST)
-            split_third(k)
-            mm2(k - 2, 1, s_banks)
-            mm2_turned(k - 2, 2, s_banks)
-            turn_pieces(k)
-            mm2(k - 2, 0)
-            finish(k - 2, 1, "s")
-            add_out(k - 2, 1)
-            unload_pieces(k)
-            bias_turned(k - 2, 2)
-            gating(k - 1, 2)
+            bias_turned(k - 3, 2)
             gating(k - 1, 1)
-            for i in (0, 1, LAST):
-                make_gate(k, i)
-            turn_back(k - 2, 2, s_banks)
-            finish(k - 2, 0, "v")
-            make_gate(k, 2)
+            gating(k - 1, 0)
+            mm2(k - 2, 0, s_banks)
+            mm2(k - 2, 3, s_banks)
+            mm2(k - 2, 1)
+            mm2(k - 2, 2)
+            turn_back(k - 3, 2, s_banks)
+            split_first(k)
+            gating(k - 1, LAST)
+            split_second(k)
+            gating(k - 1, 2)
+            split_third(k)
+            turn_pieces(k, v_banks)
+            finish(k - 3, 2, "s")
+            unload_pieces(k)
+            finish(k - 3, 3, "s")
+            store(k - 3, 2, NT)
+            finish(k - 2, 1, "v")
             quantize_g(k - 1)
-            store(k - 2, 0, 2)
+            for i in (0, 1, 3):
+                make_gate(k, i)
             mm2_turned(k - 1, 2, s_banks)
-            finish(k - 2, 2, "s")
-            finish(k - 2, 3, "s")
-            store(k - 2, 2, NT)
+            for i in (0, 3):
+                finish(k - 2, i, "s")
+                add_out(k - 2, i)
+            finish(k - 2, 2, "v")
+            store(k - 2, 1, 3)
+            make_gate(k, 2)
+            mm2(k - 1, 0, s_banks)
+            mm2(k - 1, 1, s_banks)
             bias_turned(k - 1, 2)
+            store(k - 2, 0, 1)
             gating(k, 1)
             gating(k, 0)
-            mm2(k - 1, 0)
-            mm2(k - 1, 1)
             turn_back(k - 1, 2, s_banks)
             gating(k, 3)
-            for i in (0, 1):
-                finish(k - 1, i, "v")
-                store(k - 1, i, i + 1)
+            store(k - 2, 3, 4)
+            finish(k - 1, 0, "v")
+            store(k - 1, 0, 1)
             quantize_half(k, 0)
             mm2(k, 0)
             mm2(k, 1)
@@ -558,15 +587,22 @@ def tile_hydraattention_pb_t_kernel(tc, x_bytes, x_scale, mask, W_q, b_q, kv_kno
                 finish(k - 1, i, "s")
                 store(k - 1, i, i + 1)
             gating(k, 2)
+            finish(k - 1, 1, "v")
+            store(k - 1, 1, 2)
             quantize_half(k, 1)
             mm2(k, 2)
             mm2(k, 3)
-            for i in range(NT):
+            finish(k, 0, "s")
+            add_out(k, 0)
+            for i in (1, 2):
                 finish(k, i, "v")
                 store(k, i, i + 1)
+            store(k, 0, 1)
+            finish(k, LAST, "v")
+            store(k, LAST, NT)
 
         for t in range(PACK):
             mm1(0, t)
-        for s in range(NCHUNKS):
+        for s in range(NCHUNKS - 1):
             step(s)
         drain()

@@ -17,11 +17,13 @@ B = 2
 C = 512
 N = 4096
 P = 128
-HALF = 64
+HALF = P // 2
 PACK = 4
 TILE = 128
 CHUNK = 512
 NT = CHUNK // TILE
+LAST = NT - 1
+LAST_PLANE = PACK - 1
 NTILES = B * N // TILE
 NCHUNKS = B * N // CHUNK
 PER_IMG = N // CHUNK
@@ -32,8 +34,8 @@ FLOPS = 2 * 2 * B * N * C * C
 
 X_LOADS = ((0, 0, 512), (0, 512, 512), (0, 1024, 1024), (0, 2048, 2048), (1, 0, 2048), (1, 2048, 2048))
 TURNED = range(1, 14)
-LAST = NT - 1
-PLANE_ORDER = (1, 0, 3, 2)
+PAIRS = (1, 0, 3, 2)
+BACKWARDS = (3, 2, 1, 0)
 
 
 def tile_hydraattention_pb_t_kernel(tc, x_bytes, x_scale, mask, W_q, b_q, kv_know, kv_mask, W_out, b_out, out):
@@ -46,12 +48,12 @@ def tile_hydraattention_pb_t_kernel(tc, x_bytes, x_scale, mask, W_q, b_q, kv_kno
         psum = ctx.enter_context(tc.psum_pool(name="psum", bufs=1))
         ctx.enter_context(tc.manual_schedule())
 
-        s_banks = [f"s{i}" for i in range(4)]
-        v_banks = [f"v{i}" for i in range(4)]
+        free = {"s": [f"a{i}" for i in range(4)], "v": [f"b{i}" for i in range(4)]}
 
-        def take(banks, shape, dtype):
-            tag = banks.pop(0)
-            return psum.tile(shape, dtype, name="bank_" + tag, tag=tag), tag
+        def take(role, shape, dtype):
+            home = free[role]
+            tag = home.pop(0)
+            return psum.tile(shape, dtype, name="bank_" + tag, tag=tag), tag, home
 
         x_tiles = []
 
@@ -114,28 +116,34 @@ def tile_hydraattention_pb_t_kernel(tc, x_bytes, x_scale, mask, W_q, b_q, kv_kno
             else:
                 nc.vector.tensor_scalar(out=planes[k][:, j, :], in0=src, scalar1=xs[:, j : j + 1], scalar2=None, op0=ALU.mult)
 
+        def interleave_on_vector(dst, src):
+            nc.vector.tensor_copy(out=dst.rearrange("p (c e) j -> p c j e", e=RUN), in_=src.rearrange("p j (c e) -> p c j e", e=RUN))
+
         def interleave(k, eng):
             grouped[k] = work.tile([P, CHUNK, PACK], BF16, name="grouped", bufs=2, align_bytes=64)
             src = planes.pop(k)[:]
             if eng == "g":
                 nc.gpsimd.tensor_scalar(out=grouped[k][:], in0=src.rearrange("p j w -> p w j"), scalar1=1.0, scalar2=0.0, op0=ALU.mult, op1=ALU.add)
             else:
-                nc.vector.tensor_copy(out=grouped[k][:].rearrange("p (c e) j -> p c j e", e=RUN), in_=src.rearrange("p j (c e) -> p c j e", e=RUN))
+                interleave_on_vector(grouped[k][:], src)
 
-        def quantize(src, name):
+        def code_tiles(name):
             codes = work.tile([P, CHUNK], U32, name=name + "codes", bufs=2, align_bytes=64)
             scales = work.tile([P, CHUNK], U8, name=name + "scales", bufs=2, align_bytes=64)
-            nc.vector.quantize_mx(out=codes[:].bitcast(FP8X4), scales=scales[:], in_=src[:].rearrange("p w j -> p (w j)"))
             return codes, scales
 
+        def quantize(codes, scales, src):
+            nc.vector.quantize_mx(out=codes.bitcast(FP8X4), scales=scales, in_=src)
+
         def quantize_x(k):
-            xcodes[k] = quantize(grouped.pop(k), "x")
+            xcodes[k] = code_tiles("x")
+            quantize(xcodes[k][0][:], xcodes[k][1][:], grouped.pop(k)[:].rearrange("p w j -> p (w j)"))
 
         ident = keep.tile([P, P], F32, name="ident", align_bytes=64)
         make_identity(nc, ident[:])
         nc.vector.memset(mrow[HALF:P, :], 0.0)
-        pcs = [keep.tile([P, 2, HALF], BF16, name=f"pieces{i}", align_bytes=64) for i in range(2)]
-        for t in pcs:
+        pieces = [keep.tile([P, 2, HALF], BF16, name=f"pieces{i}", align_bytes=64) for i in range(2)]
+        for t in pieces:
             nc.vector.memset(t[:], 0.0)
         ident_b = keep.tile([P, P], BF16, name="ident_b", align_bytes=64)
         nc.vector.tensor_copy(out=ident_b[:], in_=ident[:])
@@ -148,16 +156,15 @@ def tile_hydraattention_pb_t_kernel(tc, x_bytes, x_scale, mask, W_q, b_q, kv_kno
 
         def quantize_wq(u):
             cols = slice(u * 2 * TILE, (u + 1) * 2 * TILE)
-            nc.vector.quantize_mx(out=wq_codes[:, cols].bitcast(FP8X4), scales=wq_scales[:, cols],
-                                  in_=wq_grouped[:, 2 * u : 2 * u + 2].rearrange("p t m j -> p (t m j)"))
+            quantize(wq_codes[:, cols], wq_scales[:, cols], wq_grouped[:, 2 * u : 2 * u + 2].rearrange("p t m j -> p (t m j)"))
 
-        widen(0, LAST, "s")
+        widen(0, LAST_PLANE, "s")
         for u in range(2):
             nc.scalar.copy(out=wq_grouped[:, 2 * u : 2 * u + 2].rearrange("p t m j -> p m j t"),
                            in_=wq_raw[:].rearrange("p j (m t) -> p m j t", t=PACK)[:, :, :, 2 * u : 2 * u + 2])
         bq = keep.tile([P, PACK], F32, name="bq")
         nc.scalar.copy(out=bq[:], in_=bq_raw[:])
-        for j in range(LAST):
+        for j in range(LAST_PLANE):
             widen(0, j, "v")
         interleave(0, "v")
         quantize_wq(0)
@@ -167,29 +174,30 @@ def tile_hydraattention_pb_t_kernel(tc, x_bytes, x_scale, mask, W_q, b_q, kv_kno
         wo_codes = keep.tile([P, C], U32, name="wo_codes", align_bytes=64)
         wo_scales = keep.tile([P, C], U8, name="wo_scales", align_bytes=64)
         wo_grouped = keep.tile([P, C, PACK], BF16, name="wo_grouped", align_bytes=64)
-
         bo_cols = keep.tile([P, PACK], F32, name="bo_cols")
         ab = keep.tile([P, 2, NTILES], F32, name="ab")
 
-        def mask_weights():
-            m_ps, tag = take(v_banks, [P, P], BF16)
-            nc.tensor.transpose(m_ps[:], mrow[:], ident_b[:])
-            inv = keep.tile([P, NTILES], F32, name="inv")
-            damp = keep.tile([P, NTILES], F32, name="damp")
-            m07 = keep.tile([P, NTILES], F32, name="m07")
-            m = m_ps[:, 0:NTILES]
+        m_ps, m_tag, m_home = take("v", [P, P], BF16)
+        nc.tensor.transpose(m_ps[:], mrow[:], ident_b[:])
+        m = m_ps[:, 0:NTILES]
+        inv = keep.tile([P, NTILES], F32, name="inv")
+        damp = keep.tile([P, NTILES], F32, name="damp")
+        m07 = keep.tile([P, NTILES], F32, name="m07")
+
+        def mask_factors():
             nc.vector.tensor_scalar(out=inv[:], in0=m, scalar1=-1.0, scalar2=1.0, op0=ALU.mult, op1=ALU.add)
             nc.vector.tensor_scalar(out=damp[:], in0=m, scalar1=-0.7, scalar2=1.0, op0=ALU.mult, op1=ALU.add)
             nc.vector.tensor_scalar(out=m07[:], in0=m, scalar1=0.7, scalar2=None, op0=ALU.mult)
+
+        def mask_weights():
             nc.vector.tensor_mul(out=ab[:, 0, :], in0=inv[:], in1=damp[:])
             nc.vector.tensor_mul(out=ab[:, 1, :], in0=m, in1=m07[:])
-            v_banks.append(tag)
-
-        kv_rows = {img: keep.tile([P, NT, C], BF16, name=f"kv_rows{img}", align_bytes=64) for img in range(B)}
+            m_home.append(m_tag)
 
         def by_plane(vec):
             return vec.rearrange("p (m t) -> p t m", t=PACK)
 
+        kv_rows = {img: keep.tile([P, NT, C], BF16, name=f"kv_rows{img}", align_bytes=64) for img in range(B)}
         kv_planes = {}
 
         def permute_kv(img):
@@ -201,313 +209,311 @@ def tile_hydraattention_pb_t_kernel(tc, x_bytes, x_scale, mask, W_q, b_q, kv_kno
                 nc.vector.tensor_scalar(out=kv_rows[img][:, i, :], in0=kv_planes[img][:].rearrange("p t m -> p (t m)"),
                                         scalar1=sel[:, i : i + 1], scalar2=None, op0=ALU.mult)
 
-        q0 = {}
-        qb = {}
-        qt = {}
+        def turn_bo():
+            ps, tag, home = take("v", [P, PACK, TILE], BF16)
+            for j in range(PACK):
+                nc.tensor.transpose(ps[:, j, :], bo[:, j * TILE : (j + 1) * TILE], ident_b[:])
+            nc.vector.tensor_copy(out=bo_cols[:], in_=ps[:, :, 0])
+            home.append(tag)
+
+        q_ps = {}
+        q_sb = {}
+        qt_ps = {}
         q_turned = set()
         ss = {}
         rs = {}
-        pw = {}
+        weights = {}
         rest = {}
-        turned = {}
-        rows_of = {}
+        pieces_ps = {}
+        piece_rows = {}
         terms = {}
         gate = {}
         gated = {}
         y_ps = {}
         y_sb = {}
+        yt_ps = {}
+        yt_sb = {}
 
-        def is_turned(k, i):
-            return k in TURNED and i == LAST
-
-        def mm1(k, t):
+        def mm1(k, t, role="s"):
             codes, scales = xcodes[k]
             cols = slice(t * TILE, (t + 1) * TILE)
-            q0[k, t] = take(s_banks, [P, CHUNK], F32)
-            nc.tensor.matmul_mx(out=q0[k, t][0][:], lhsT=wq_codes[:, cols].bitcast(FP8X4), lhsT_scale=wq_scales[:, cols],
+            q_ps[k, t] = take(role, [P, CHUNK], F32)
+            nc.tensor.matmul_mx(out=q_ps[k, t][0][:], lhsT=wq_codes[:, cols].bitcast(FP8X4), lhsT_scale=wq_scales[:, cols],
                                 rhs=codes[:].bitcast(FP8X4), rhs_scale=scales[:], start=True, stop=True)
 
         def add_bias(k, t):
-            if k not in qb:
-                qb[k] = work.tile([P, PACK, CHUNK], F32, name="qb", bufs=4, align_bytes=64)
-            ps, tag = q0.pop((k, t))
-            nc.scalar.activation(out=qb[k][:, t, :], in_=ps[:], func=ACT.Identity, bias=bq[:, t : t + 1])
-            s_banks.append(tag)
+            if k not in q_sb:
+                q_sb[k] = work.tile([P, PACK, CHUNK], F32, name="qb", bufs=4, align_bytes=64)
+            ps, tag, home = q_ps.pop((k, t))
+            nc.scalar.activation(out=q_sb[k][:, t, :], in_=ps[:], func=ACT.Identity, bias=bq[:, t : t + 1])
+            home.append(tag)
 
         def turn_q(k, planes_done, tiles):
             for i in tiles:
-                if (k, i) not in qt:
-                    qt[k, i] = take(s_banks, [P, PACK, TILE], F32)
+                if (k, i) not in qt_ps:
+                    qt_ps[k, i] = take("s", [P, PACK, TILE], F32)
                 for t in planes_done:
                     if (k, i, t) not in q_turned:
                         q_turned.add((k, i, t))
-                        nc.tensor.transpose(qt[k, i][0][:, t, :], qb[k][:, t, i * TILE : (i + 1) * TILE], ident[:])
+                        nc.tensor.transpose(qt_ps[k, i][0][:, t, :], q_sb[k][:, t, i * TILE : (i + 1) * TILE], ident[:])
 
         def squares(k, i):
             if k not in ss:
                 ss[k] = work.tile([P, NT], F32, name="ss")
             junk = work.tile([P, C], BF16, name="junk", bufs=NT)
-            ps, tag = qt.pop((k, i))
+            ps, tag, home = qt_ps.pop((k, i))
             nc.scalar.activation(out=junk[:], in_=ps[:].rearrange("p t m -> p (t m)"), func=ACT.Square, accum_out=ss[k][:, i : i + 1])
-            s_banks.append(tag)
+            home.append(tag)
 
         def root(k):
             rs[k] = work.tile([P, NT], F32, name="rs")
             nc.scalar.activation(out=rs[k][:], in_=ss.pop(k)[:], func=ACT.Abs_reciprocal_sqrt)
 
         def piece(k, q):
-            return pcs[k % 2][:, :, q * NT : (q + 1) * NT]
+            return pieces[k % 2][:, :, q * NT : (q + 1) * NT]
 
         def split_first(k):
-            pw[k] = work.tile([P, 2, NT], F32, name="pw")
+            weights[k] = work.tile([P, 2, NT], F32, name="pw")
             spread = rs[k][:].unsqueeze(1).to_broadcast([P, 2, NT])
-            weights = ab[:, :, k * NT : (k + 1) * NT]
-            nc.vector.tensor_mul(out=pw[k][:], in0=weights, in1=spread)
-            nc.vector.tensor_mul(out=piece(k, 0), in0=weights, in1=spread)
+            nc.vector.tensor_mul(out=weights[k][:], in0=ab[:, :, k * NT : (k + 1) * NT], in1=spread)
+            nc.vector.tensor_mul(out=piece(k, 0), in0=ab[:, :, k * NT : (k + 1) * NT], in1=spread)
 
         def split_second(k):
             rest[k] = work.tile([P, 2, NT], F32, name="rest")
-            nc.vector.tensor_sub(out=rest[k][:], in0=pw[k][:], in1=piece(k, 0))
-            nc.vector.tensor_sub(out=piece(k, 1), in0=pw[k][:], in1=piece(k, 0))
+            nc.vector.tensor_sub(out=rest[k][:], in0=weights[k][:], in1=piece(k, 0))
+            nc.vector.tensor_sub(out=piece(k, 1), in0=weights[k][:], in1=piece(k, 0))
 
         def split_third(k):
             nc.vector.tensor_sub(out=piece(k, 2), in0=rest.pop(k)[:], in1=piece(k, 1))
 
         def weigh_last(k):
-            pw[k] = work.tile([P, 2, 1], F32, name="pt")
+            weights[k] = work.tile([P, 2, 1], F32, name="pt")
             t = k * NT + LAST
-            nc.vector.tensor_scalar(out=pw[k][:], in0=ab[:, :, t : t + 1], scalar1=rs[k][:, LAST : LAST + 1], scalar2=None, op0=ALU.mult)
+            nc.vector.tensor_scalar(out=weights[k][:], in0=ab[:, :, t : t + 1], scalar1=rs[k][:, LAST : LAST + 1], scalar2=None, op0=ALU.mult)
 
-        def turn_pieces(k, banks=s_banks):
-            turned[k] = take(banks, [P, P], BF16) + (banks,)
-            nc.tensor.transpose(turned[k][0][:], pcs[k % 2][:].rearrange("p h x -> p (h x)"), ident_b[:])
+        def turn_pieces(k, role="s"):
+            pieces_ps[k] = take(role, [P, P], BF16)
+            nc.tensor.transpose(pieces_ps[k][0][:], pieces[k % 2][:].rearrange("p h x -> p (h x)"), ident_b[:])
 
         def unload_pieces(k):
-            rows_of[k] = work.tile([P, P], BF16, name="rows_of", bufs=2, align_bytes=64)
-            ps, tag, banks = turned.pop(k)
-            nc.scalar.copy(out=rows_of[k][:], in_=ps[:])
-            banks.append(tag)
+            piece_rows[k] = work.tile([P, P], BF16, name="rows_of", bufs=2, align_bytes=64)
+            ps, tag, home = pieces_ps.pop(k)
+            nc.scalar.copy(out=piece_rows[k][:], in_=ps[:])
+            home.append(tag)
 
         def gate_terms(k):
             terms[k] = work.tile([P, 2, PACK, TILE], F32, name="terms", bufs=2, align_bytes=64)
-            col = pw[k].shape[2] - 1
+            col = weights[k].shape[2] - 1
             for h in range(2):
-                src = by_plane(kv_all[k // PER_IMG][:, h, :])
-                nc.gpsimd.tensor_scalar(out=terms[k][:, h], in0=src, scalar1=pw[k][:, h, col : col + 1], scalar2=0.0, op0=ALU.mult, op1=ALU.add)
+                nc.gpsimd.tensor_scalar(out=terms[k][:, h], in0=by_plane(kv_all[k // PER_IMG][:, h, :]),
+                                        scalar1=weights[k][:, h, col : col + 1], scalar2=0.0, op0=ALU.mult, op1=ALU.add)
 
-        def make_gate(k, i, banks=v_banks):
-            gate[k, i] = take(banks, [P, PACK, TILE], F32) + (banks,)
+        def make_gate(k, i):
+            gate[k, i] = take("v", [P, PACK, TILE], F32)
             ps = gate[k, i][0]
             for t in range(PACK):
-                cols = slice(t * TILE, (t + 1) * TILE)
-                if is_turned(k, i):
+                if k in TURNED and i == LAST:
                     for h in range(2):
                         nc.tensor.matmul(ps[:, t, :], lhsT=terms[k][:, h, t, :], rhs=ident[:], is_transpose=True, start=h == 0, stop=h == 1)
                 else:
-                    nc.tensor.matmul(ps[:, t, :], lhsT=kv_rows[k // PER_IMG][:, i, cols], rhs=rows_of[k][:], start=True, stop=True)
+                    nc.tensor.matmul(ps[:, t, :], lhsT=kv_rows[k // PER_IMG][:, i, t * TILE : (t + 1) * TILE], rhs=piece_rows[k][:], start=True, stop=True)
 
         def gating(k, i):
             if k not in gated:
                 gated[k] = work.tile([P, CHUNK, PACK], BF16, name="gated", bufs=2, align_bytes=64)
-            ps, tag, banks = gate.pop((k, i))
-            toks = slice(i * TILE, (i + 1) * TILE)
-            nc.vector.tensor_tensor(out=gated[k][:, toks, :].rearrange("p (c e) t -> p c t e", e=2),
+            ps, tag, home = gate.pop((k, i))
+            pixels = slice(i * TILE, (i + 1) * TILE)
+            nc.vector.tensor_tensor(out=gated[k][:, pixels, :].rearrange("p (c e) t -> p c t e", e=2),
                                     in0=ps[:].rearrange("p t (c e) -> p c t e", e=2),
-                                    in1=qb[k][:, :, toks].rearrange("p t (c e) -> p c t e", e=2), op=ALU.mult)
-            banks.append(tag)
+                                    in1=q_sb[k][:, :, pixels].rearrange("p t (c e) -> p c t e", e=2), op=ALU.mult)
+            home.append(tag)
 
         def quantize_g(k):
-            gcodes[k] = quantize(gated.pop(k), "g")
+            gcodes[k] = code_tiles("g")
+            quantize(gcodes[k][0][:], gcodes[k][1][:], gated.pop(k)[:].rearrange("p w j -> p (w j)"))
 
-        def mm2(k, i, banks=v_banks):
+        def quantize_g_half(k, h):
+            if h == 0:
+                gcodes[k] = code_tiles("g")
+            pixels = slice(h * 2 * TILE, (h + 1) * 2 * TILE)
+            quantize(gcodes[k][0][:, pixels], gcodes[k][1][:, pixels], gated[k][:, pixels, :].rearrange("p w j -> p (w j)"))
+
+        def mm2(k, i, role="v"):
             codes, scales = gcodes[k]
-            cols = slice(i * TILE, (i + 1) * TILE)
-            y_ps[k, i] = take(banks, [P, C], F32) + (banks,)
-            nc.tensor.matmul_mx(out=y_ps[k, i][0][:], lhsT=codes[:, cols].bitcast(FP8X4), lhsT_scale=scales[:, cols],
+            pixels = slice(i * TILE, (i + 1) * TILE)
+            y_ps[k, i] = take(role, [P, C], F32)
+            nc.tensor.matmul_mx(out=y_ps[k, i][0][:], lhsT=codes[:, pixels].bitcast(FP8X4), lhsT_scale=scales[:, pixels],
                                 rhs=wo_codes[:].bitcast(FP8X4), rhs_scale=wo_scales[:], start=True, stop=True)
 
         def finish(k, i, eng):
             if k not in y_sb:
                 y_sb[k] = work.tile([P, NT, C], F32, name="y", bufs=8)
-            y = y_sb[k][:, i, :]
-            ps, tag, banks = y_ps.pop((k, i))
+            ps, tag, home = y_ps.pop((k, i))
             if eng == "v":
-                nc.vector.tensor_add(out=y, in0=ps[:], in1=bo[:])
+                nc.vector.tensor_add(out=y_sb[k][:, i, :], in0=ps[:], in1=bo[:])
             else:
-                nc.scalar.copy(out=y, in_=ps[:])
-            banks.append(tag)
-
-        y_turned = {}
-
-        def mm2_turned(k, i0, banks):
-            codes, scales = gcodes[k]
-            toks = slice(i0 * TILE, (i0 + 2) * TILE)
-            held = []
-            for u in range(2):
-                ps, tag = take(banks, [P, 2, 2 * TILE], F32)
-                held.append((ps, tag, banks))
-                for e in range(2):
-                    cols = slice((2 * u + e) * TILE, (2 * u + e + 1) * TILE)
-                    nc.tensor.matmul_mx(out=ps[:, e, :], lhsT=wo_codes[:, cols].bitcast(FP8X4), lhsT_scale=wo_scales[:, cols],
-                                        rhs=codes[:, toks].bitcast(FP8X4), rhs_scale=scales[:, toks], start=True, stop=True)
-            y_turned[k, i0] = held
-
-        def bias_turned(k, i0):
-            yt = work.tile([P, PACK, 2 * TILE], F32, name="yt", bufs=2, align_bytes=64)
-            for u, (ps, tag, banks) in enumerate(y_turned[k, i0]):
-                for e in range(2):
-                    j = 2 * u + e
-                    nc.scalar.activation(out=yt[:, j, :], in_=ps[:, e, :], func=ACT.Identity, bias=bo_cols[:, j : j + 1])
-                banks.append(tag)
-            y_turned[k, i0] = yt
-
-        def turn_back(k, i0, banks):
-            yt = y_turned.pop((k, i0))
-            for a in range(2):
-                y_ps[k, i0 + a] = take(banks, [P, C], F32) + (banks,)
-                for j in range(PACK):
-                    nc.tensor.transpose(y_ps[k, i0 + a][0][:, j * TILE : (j + 1) * TILE], yt[:, j, a * TILE : (a + 1) * TILE], ident[:])
-
-        def turn_bo():
-            ps, tag = take(v_banks, [P, PACK, TILE], BF16)
-            for j in range(PACK):
-                nc.tensor.transpose(ps[:, j, :], bo[:, j * TILE : (j + 1) * TILE], ident_b[:])
-            nc.vector.tensor_copy(out=bo_cols[:], in_=ps[:, :, 0])
-            v_banks.append(tag)
+                nc.scalar.copy(out=y_sb[k][:, i, :], in_=ps[:])
+            home.append(tag)
 
         def add_out(k, i):
             nc.gpsimd.tensor_add(out=y_sb[k][:, i, :], in0=y_sb[k][:, i, :], in1=bo[:])
 
-        def store(k, a0, a1):
-            t0 = (k * NT + a0) * TILE
-            nc.sync.dma_start(out=out_rows[t0 : t0 + (a1 - a0) * TILE, :].rearrange("(a p) c -> p a c", p=P), in_=y_sb[k][:, a0:a1, :])
+        def mm2_turned(k):
+            codes, scales = gcodes[k]
+            pixels = slice(2 * TILE, NT * TILE)
+            yt_ps[k] = []
+            for u in range(2):
+                yt_ps[k].append(take("s", [P, 2, 2 * TILE], F32))
+                for e in range(2):
+                    cols = slice((2 * u + e) * TILE, (2 * u + e + 1) * TILE)
+                    nc.tensor.matmul_mx(out=yt_ps[k][u][0][:, e, :], lhsT=wo_codes[:, cols].bitcast(FP8X4), lhsT_scale=wo_scales[:, cols],
+                                        rhs=codes[:, pixels].bitcast(FP8X4), rhs_scale=scales[:, pixels], start=True, stop=True)
 
-        def empty_q(s, gates):
-            order = PLANE_ORDER if s else tuple(range(PACK))
+        def bias_turned(k):
+            yt_sb[k] = work.tile([P, PACK, 2 * TILE], F32, name="yt", bufs=2, align_bytes=64)
+            for u, (ps, tag, home) in enumerate(yt_ps.pop(k)):
+                for e in range(2):
+                    j = 2 * u + e
+                    nc.scalar.activation(out=yt_sb[k][:, j, :], in_=ps[:, e, :], func=ACT.Identity, bias=bo_cols[:, j : j + 1])
+                home.append(tag)
+
+        def turn_back(k):
+            for a in range(2):
+                y_ps[k, 2 + a] = take("s", [P, C], F32)
+                for j in range(PACK):
+                    nc.tensor.transpose(y_ps[k, 2 + a][0][:, j * TILE : (j + 1) * TILE], yt_sb[k][:, j, a * TILE : (a + 1) * TILE], ident[:])
+
+        def store(k, i0, i1):
+            t0 = (k * NT + i0) * TILE
+            nc.sync.dma_start(out=out_rows[t0 : t0 + (i1 - i0) * TILE, :].rearrange("(a p) c -> p a c", p=P), in_=y_sb[k][:, i0:i1, :])
+
+        def empty_q(k, order, gates, all_banks=False):
             for n, t in enumerate(order):
-                add_bias(s, t)
-                turn_q(s, order[: n + 1], range(n + 1))
+                add_bias(k, t)
+                turn_q(k, order[: n + 1], range(NT if all_banks else n + 1))
                 if n < len(gates):
-                    make_gate(s - 2, gates[n])
+                    make_gate(k - 2, gates[n])
+
+        def first_steps():
+            for t in range(PACK):
+                mm1(0, t)
+            for j in range(PACK):
+                widen(1, j, "v")
+            mask_factors()
+            interleave(1, "v")
+            mask_weights()
+            widen(2, 0, "v")
+            quantize_x(1)
+            for j in range(1, PACK):
+                widen(2, j, "v")
+            widen(3, 1, "v")
+            interleave(2, "v")
+            widen(3, 2, "v")
+            quantize_x(2)
+            empty_q(0, tuple(range(PACK)), ())
+            for t in range(PACK):
+                mm1(1, t, "v")
+            widen(3, 0, "s")
+            widen(3, LAST_PLANE, "v")
+            permute_kv(0)
+            interleave(3, "v")
+            for i in PAIRS:
+                squares(0, i)
+
+            empty_q(1, PAIRS, (), all_banks=True)
+            for t in range(PACK):
+                mm1(2, t, "v")
+            root(0)
+            interleave_on_vector(wo_grouped[:], wo_raw[:])
+            widen(4, 0, "v")
+            widen(4, 1, "v")
+            split_first(0)
+            select_kv(0)
+            split_second(0)
+            widen(4, 2, "v")
+            widen(4, LAST_PLANE, "v")
+            split_third(0)
+            permute_kv(1)
+            quantize(wo_codes[:], wo_scales[:], wo_grouped[:].rearrange("p w j -> p (w j)"))
+            widen(5, 2, "v")
+            squares(1, 3)
+            squares(1, 2)
+            turn_pieces(0)
+            squares(1, 1)
+            squares(1, 0)
+            widen(5, 0, "s")
+            unload_pieces(0)
+            free.update(s=free["v"], v=free["s"])
+            root(1)
+            select_kv(1)
+            turn_bo()
+            make_gate(0, 0)
 
         def step(s):
-            mid = 1 <= s
-            old = 2 <= s
-            older = 3 <= s
-            late = s + 2 >= NCHUNKS
-            fill = s + 3 < NCHUNKS
-            held = late
-            hold = not fill
-            if s == 0:
-                for j in range(PACK):
-                    widen(1, j, "v")
-                mask_weights()
-                interleave(1, "v")
-                for j in range(PACK):
-                    widen(2, j, "v")
-                quantize_x(1)
-                interleave(2, "v")
-            if mid:
-                split_first(s - 1)
-                quantize_x(s + 1)
-                split_second(s - 1)
-            if s == 1:
-                nc.vector.tensor_copy(out=wo_grouped[:].rearrange("p (c e) j -> p c j e", e=RUN), in_=wo_raw[:].rearrange("p j (c e) -> p c j e", e=RUN))
-            if s == 2:
-                interleave(4, "v")
-            if older and not late:
-                widen(s + 2, LAST, "v")
-            if late:
+            output = s >= 3
+            more_x = s + 2 < NCHUNKS
+            more_planes = s + 3 < NCHUNKS
+            split_first(s - 1)
+            quantize_x(s + 1)
+            split_second(s - 1)
+            if not output:
+                interleave(s + 2, "v")
+            elif more_x:
+                widen(s + 2, LAST_PLANE, "v")
+            else:
                 quantize_g(s - 3)
-            if mid:
-                split_third(s - 1)
-            if older and not late:
+            split_third(s - 1)
+            if output and more_x:
                 quantize_g(s - 3)
-            if s == 1:
-                select_kv(0)
-                widen(4, 1, "v")
-                widen(4, 2, "v")
-                widen(4, LAST, "v")
-                permute_kv(1)
-                nc.vector.quantize_mx(out=wo_codes[:].bitcast(FP8X4), scales=wo_scales[:], in_=wo_grouped[:].rearrange("p w j -> p (w j)"))
-                turn_bo()
-                widen(5, 1, "v")
-                widen(5, 2, "v")
-            if older and not late:
                 interleave(s + 2, "g")
-            if late or s == 2:
+            else:
                 weigh_last(s - 1)
-            if old:
-                gate_terms(s - 1)
-            if old:
-                make_gate(s - 2, LAST)
-            empty_q(s, () if not old else ((1,) if held else (1, 2)))
-            if held:
+            gate_terms(s - 1)
+            make_gate(s - 2, LAST)
+            empty_q(s, PAIRS, (1, 2) if more_x else (1,))
+            if not more_x:
                 finish(s - 4, LAST, "s")
                 make_gate(s - 2, 2)
                 add_out(s - 4, LAST)
                 store(s - 4, LAST, NT)
-            if fill:
-                widen(s + 3, 0, "s")
-                if older:
-                    widen(s + 3, 1, "s")
-            if s == 0:
-                widen(3, 1, "v")
-                widen(3, 2, "v")
-                widen(3, LAST, "v")
-                permute_kv(0)
-                interleave(3, "v")
-            if old:
-                gating(s - 2, 1)
-                gating(s - 2, 0)
-            if older:
+            if more_planes:
+                for j in range(2) if output else (1,):
+                    widen(s + 3, j, "s")
+            gating(s - 2, 1)
+            gating(s - 2, 0)
+            if output:
                 mm2(s - 3, 0)
                 mm2(s - 3, 1)
-            if old:
-                gating(s - 2, 3)
-                gating(s - 2, 2)
-            order = (3, 2, 1, 0) if fill and older else (1, 0, 3, 2)
+            gating(s - 2, LAST)
+            gating(s - 2, 2)
+            order = BACKWARDS if more_planes and output else PAIRS
             squares(s, order[0])
             squares(s, order[1])
-            if older:
+            if output:
                 mm2(s - 3, 2)
-            if mid:
-                turn_pieces(s - 1)
-            if older:
-                mm2(s - 3, 3)
+            turn_pieces(s - 1)
+            if output:
+                mm2(s - 3, LAST)
             mm1(s + 1, 0)
             squares(s, order[2])
             squares(s, order[3])
             mm1(s + 1, 1)
             mm1(s + 1, 2)
-            if mid:
-                unload_pieces(s - 1)
-            mm1(s + 1, 3)
-            if fill and older:
+            unload_pieces(s - 1)
+            mm1(s + 1, LAST_PLANE)
+            if more_planes and output:
                 widen(s + 3, 2, "s")
             root(s)
-            if s == 1:
-                select_kv(1)
-            if older:
+            if output:
                 finish(s - 3, 1, "v")
                 finish(s - 3, 0, "v")
-                if not hold:
+                if more_planes:
                     finish(s - 3, LAST, "v")
                 finish(s - 3, 2, "v")
-                store(s - 3, 0, LAST if hold else NT)
-            if mid:
-                make_gate(s - 1, 0)
+                store(s - 3, 0, NT if more_planes else LAST)
+            make_gate(s - 1, 0)
 
-        def quantize_half(k, h):
-            if h == 0:
-                codes = work.tile([P, CHUNK], U32, name="gcodes", bufs=2, align_bytes=64)
-                scales = work.tile([P, CHUNK], U8, name="gscales", bufs=2, align_bytes=64)
-                gcodes[k] = (codes, scales)
-            codes, scales = gcodes[k]
-            cols = slice(h * 2 * TILE, (h + 1) * 2 * TILE)
-            nc.vector.quantize_mx(out=codes[:, cols].bitcast(FP8X4), scales=scales[:, cols], in_=gated[k][:, cols, :].rearrange("p w j -> p (w j)"))
-
-        def drain():
+        def last_steps():
             k = NCHUNKS - 1
             make_gate(k - 2, LAST)
             quantize_g(k - 3)
@@ -516,12 +522,12 @@ def tile_hydraattention_pb_t_kernel(tc, x_bytes, x_scale, mask, W_q, b_q, kv_kno
             split_second(k - 1)
             gating(k - 2, LAST)
             split_third(k - 1)
-            empty_q(k, (1, 2))
+            empty_q(k, PAIRS, (1, 2))
             mm2(k - 3, 0)
             finish(k - 4, LAST, "s")
             add_out(k - 4, LAST)
             store(k - 4, LAST, NT)
-            turn_pieces(k - 1, v_banks)
+            turn_pieces(k - 1, "v")
             gating(k - 2, 1)
             mm2(k - 3, 1)
             squares(k, 1)
@@ -538,60 +544,60 @@ def tile_hydraattention_pb_t_kernel(tc, x_bytes, x_scale, mask, W_q, b_q, kv_kno
             finish(k - 3, 1, "v")
             make_gate(k - 1, 2)
             store(k - 3, 0, 2)
-            mm2_turned(k - 3, 2, s_banks)
+            mm2_turned(k - 3)
             quantize_g(k - 2)
-            bias_turned(k - 3, 2)
+            bias_turned(k - 3)
             gating(k - 1, 1)
             gating(k - 1, 0)
-            mm2(k - 2, 0, s_banks)
-            mm2(k - 2, 3, s_banks)
+            mm2(k - 2, 0, "s")
+            mm2(k - 2, LAST, "s")
             mm2(k - 2, 1)
             mm2(k - 2, 2)
-            turn_back(k - 3, 2, s_banks)
+            turn_back(k - 3)
             split_first(k)
             gating(k - 1, LAST)
             split_second(k)
             gating(k - 1, 2)
             split_third(k)
-            turn_pieces(k, v_banks)
+            turn_pieces(k, "v")
             finish(k - 3, 2, "s")
             unload_pieces(k)
-            finish(k - 3, 3, "s")
+            finish(k - 3, LAST, "s")
             store(k - 3, 2, NT)
             finish(k - 2, 1, "v")
             quantize_g(k - 1)
-            for i in (0, 1, 3):
+            for i in (0, 1, LAST):
                 make_gate(k, i)
-            mm2_turned(k - 1, 2, s_banks)
-            for i in (0, 3):
+            mm2_turned(k - 1)
+            for i in (0, LAST):
                 finish(k - 2, i, "s")
                 add_out(k - 2, i)
             finish(k - 2, 2, "v")
-            store(k - 2, 1, 3)
+            store(k - 2, 1, LAST)
             make_gate(k, 2)
-            mm2(k - 1, 0, s_banks)
-            mm2(k - 1, 1, s_banks)
-            bias_turned(k - 1, 2)
+            mm2(k - 1, 0, "s")
+            mm2(k - 1, 1, "s")
+            bias_turned(k - 1)
             store(k - 2, 0, 1)
             gating(k, 1)
             gating(k, 0)
-            turn_back(k - 1, 2, s_banks)
-            gating(k, 3)
-            store(k - 2, 3, 4)
+            turn_back(k - 1)
+            gating(k, LAST)
+            store(k - 2, LAST, NT)
             finish(k - 1, 0, "v")
             store(k - 1, 0, 1)
-            quantize_half(k, 0)
+            quantize_g_half(k, 0)
             mm2(k, 0)
             mm2(k, 1)
-            for i in (2, 3):
+            for i in (2, LAST):
                 finish(k - 1, i, "s")
                 store(k - 1, i, i + 1)
             gating(k, 2)
             finish(k - 1, 1, "v")
             store(k - 1, 1, 2)
-            quantize_half(k, 1)
+            quantize_g_half(k, 1)
             mm2(k, 2)
-            mm2(k, 3)
+            mm2(k, LAST)
             finish(k, 0, "s")
             add_out(k, 0)
             for i in (1, 2):
@@ -601,8 +607,7 @@ def tile_hydraattention_pb_t_kernel(tc, x_bytes, x_scale, mask, W_q, b_q, kv_kno
             finish(k, LAST, "v")
             store(k, LAST, NT)
 
-        for t in range(PACK):
-            mm1(0, t)
-        for s in range(NCHUNKS - 1):
+        first_steps()
+        for s in range(2, NCHUNKS - 1):
             step(s)
-        drain()
+        last_steps()

@@ -323,9 +323,9 @@ def tile_hydraattention_pb_t_kernel(tc, x_bytes, x_scale, mask, W_q, b_q, kv_kno
                 gated[k] = work.tile([P, CHUNK, PACK], BF16, name="gated", bufs=2, align_bytes=64)
             ps, tag, home = gate.pop((k, i))
             pixels = slice(i * TILE, (i + 1) * TILE)
-            nc.vector.tensor_tensor(out=gated[k][:, pixels, :].rearrange("p (c e) t -> p c t e", e=2),
-                                    in0=ps[:].rearrange("p t (c e) -> p c t e", e=2),
-                                    in1=q_sb[k][:, :, pixels].rearrange("p t (c e) -> p c t e", e=2), op=ALU.mult)
+            nc.vector.tensor_tensor(out=gated[k][:, pixels, :].rearrange("p (c e) t -> p c t e", e=RUN),
+                                    in0=ps[:].rearrange("p t (c e) -> p c t e", e=RUN),
+                                    in1=q_sb[k][:, :, pixels].rearrange("p t (c e) -> p c t e", e=RUN), op=ALU.mult)
             home.append(tag)
 
         def quantize_g(k):
@@ -395,10 +395,12 @@ def tile_hydraattention_pb_t_kernel(tc, x_bytes, x_scale, mask, W_q, b_q, kv_kno
                     make_gate(k - 2, gates[n])
 
         def first_steps():
+            widen(1, 0, "s")
+            widen(1, 1, "s")
             for t in range(PACK):
                 mm1(0, t)
-            for j in range(PACK):
-                widen(1, j, "v")
+            widen(1, 2, "v")
+            widen(1, LAST_PLANE, "v")
             mask_factors()
             interleave(1, "v")
             mask_weights()

@@ -158,6 +158,8 @@ def tile_hydraattention_pb_t_kernel(tc, x_bytes, x_scale, mask, W_q, b_q, kv_kno
             cols = slice(u * 2 * TILE, (u + 1) * 2 * TILE)
             quantize(wq_codes[:, cols], wq_scales[:, cols], wq_grouped[:, 2 * u : 2 * u + 2].rearrange("p t m j -> p (t m j)"))
 
+        warm = keep.tile([P, 1], F32, name="warm")
+        nc.scalar.activation(out=warm[:], in_=ident[:, 0:1], func=ACT.Abs_reciprocal_sqrt, bias=1.0)
         widen(0, LAST_PLANE, "s")
         for u in range(2):
             nc.scalar.copy(out=wq_grouped[:, 2 * u : 2 * u + 2].rearrange("p t m j -> p m j t"),

@@ -211,10 +211,16 @@ def tile_hydraattention_pb_t_kernel(tc, x_bytes, x_scale, mask, W_q, b_q, kv_kno
                 nc.vector.tensor_scalar(out=kv_rows[img][:, i, :], in0=kv_planes[img][:].rearrange("p t m -> p (t m)"),
                                         scalar1=sel[:, i : i + 1], scalar2=None, op0=ALU.mult)
 
+        bo_ps = []
+
         def turn_bo():
             ps, tag, home = take("v", [P, PACK, TILE], BF16)
             for j in range(PACK):
                 nc.tensor.transpose(ps[:, j, :], bo[:, j * TILE : (j + 1) * TILE], ident_b[:])
+            bo_ps.extend((ps, tag, home))
+
+        def unload_bo():
+            ps, tag, home = bo_ps
             nc.vector.tensor_copy(out=bo_cols[:], in_=ps[:, :, 0])
             home.append(tag)
 
@@ -303,15 +309,18 @@ def tile_hydraattention_pb_t_kernel(tc, x_bytes, x_scale, mask, W_q, b_q, kv_kno
             nc.scalar.copy(out=piece_rows[k][:], in_=ps[:])
             home.append(tag)
 
-        def gate_terms(k):
+        def gate_terms(k, eng="g"):
             terms[k] = work.tile([P, 2, PACK, TILE], F32, name="terms", bufs=2, align_bytes=64)
             col = weights[k].shape[2] - 1
             for h in range(2):
-                nc.gpsimd.tensor_scalar(out=terms[k][:, h], in0=by_plane(kv_all[k // PER_IMG][:, h, :]),
-                                        scalar1=weights[k][:, h, col : col + 1], scalar2=0.0, op0=ALU.mult, op1=ALU.add)
+                vec, weight = by_plane(kv_all[k // PER_IMG][:, h, :]), weights[k][:, h, col : col + 1]
+                if eng == "g":
+                    nc.gpsimd.tensor_scalar(out=terms[k][:, h], in0=vec, scalar1=weight, scalar2=0.0, op0=ALU.mult, op1=ALU.add)
+                else:
+                    nc.vector.tensor_scalar(out=terms[k][:, h], in0=vec, scalar1=weight, scalar2=None, op0=ALU.mult)
 
-        def make_gate(k, i):
-            gate[k, i] = take("v", [P, PACK, TILE], F32)
+        def make_gate(k, i, role="v"):
+            gate[k, i] = take(role, [P, PACK, TILE], F32)
             ps = gate[k, i][0]
             for t in range(PACK):
                 if k in TURNED and i == LAST:
@@ -389,14 +398,7 @@ def tile_hydraattention_pb_t_kernel(tc, x_bytes, x_scale, mask, W_q, b_q, kv_kno
             t0 = (k * NT + i0) * TILE
             nc.sync.dma_start(out=out_rows[t0 : t0 + (i1 - i0) * TILE, :].rearrange("(a p) c -> p a c", p=P), in_=y_sb[k][:, i0:i1, :])
 
-        def empty_q(k, order, gates, all_banks=False):
-            for n, t in enumerate(order):
-                add_bias(k, t)
-                turn_q(k, order[: n + 1], range(NT if all_banks else n + 1))
-                if n < len(gates):
-                    make_gate(k - 2, gates[n])
-
-        def first_steps():
+        def first_step():
             widen(1, 0, "s")
             widen(1, 1, "s")
             for t in range(PACK):
@@ -410,208 +412,170 @@ def tile_hydraattention_pb_t_kernel(tc, x_bytes, x_scale, mask, W_q, b_q, kv_kno
             quantize_x(1)
             for j in range(1, PACK):
                 widen(2, j, "v")
-            widen(3, 1, "v")
+            permute_kv(0)
             interleave(2, "v")
-            widen(3, 2, "v")
-            quantize_x(2)
-            empty_q(0, tuple(range(PACK)), ())
+            select_kv(0)
+            interleave_on_vector(wo_grouped[:], wo_raw[:])
+            for t in range(PACK):
+                add_bias(0, t)
+                turn_q(0, range(t + 1), range(t + 1))
             for t in range(PACK):
                 mm1(1, t, "v")
             widen(3, 0, "s")
-            widen(3, LAST_PLANE, "v")
-            permute_kv(0)
-            interleave(3, "v")
-            for i in PAIRS:
+            widen(3, 2, "s")
+            for i in BACKWARDS:
                 squares(0, i)
-
-            empty_q(1, PAIRS, (), all_banks=True)
-            for t in range(PACK):
-                mm1(2, t, "v")
+            free.update(s=free["v"], v=free["s"])
+            turn_bo()
+            add_bias(1, 1)
             root(0)
-            interleave_on_vector(wo_grouped[:], wo_raw[:])
-            widen(4, 0, "v")
-            widen(4, 1, "v")
+
+        def second_step():
             split_first(0)
-            select_kv(0)
+            quantize(wo_codes[:], wo_scales[:], wo_grouped[:].rearrange("p w j -> p (w j)"))
             split_second(0)
-            widen(4, 2, "v")
-            widen(4, LAST_PLANE, "v")
+            unload_bo()
+            widen(3, 1, "v")
             split_third(0)
             permute_kv(1)
-            quantize(wo_codes[:], wo_scales[:], wo_grouped[:].rearrange("p w j -> p (w j)"))
-            widen(5, 2, "v")
-            squares(1, 3)
-            squares(1, 2)
-            turn_pieces(0)
-            squares(1, 1)
-            squares(1, 0)
-            widen(5, 0, "s")
-            unload_pieces(0)
-            free.update(s=free["v"], v=free["s"])
-            root(1)
+            widen(4, LAST_PLANE, "v")
             select_kv(1)
-            turn_bo()
+            widen(3, LAST_PLANE, "v")
+            quantize_x(2)
+            interleave(3, "g")
+            add_bias(1, 0)
+            turn_q(1, PAIRS[:2], range(2))
+            add_bias(1, 3)
+            turn_pieces(0, "v")
+            turn_q(1, PAIRS[:3], range(3))
+            add_bias(1, 2)
+            unload_pieces(0)
+            turn_q(1, PAIRS, range(2))
             make_gate(0, 0)
+            make_gate(0, 1)
+            turn_q(1, PAIRS, range(2, NT))
+            make_gate(0, 2)
+            make_gate(0, LAST)
+            widen(4, 2, "s")
+            for i in (1, 0, 2, LAST):
+                squares(1, i)
+            for t in range(PACK):
+                mm1(2, t)
+            for i in PAIRS:
+                gating(0, i)
+            widen(4, 0, "s")
+            root(1)
 
         def step(s):
-            output = s >= 3
             more_x = s + 2 < NCHUNKS
             more_planes = s + 3 < NCHUNKS
+            last = s + 1 == NCHUNKS
+            turned = s - 1 in TURNED
+            if more_x and s > 3:
+                widen(s + 2, 0, "s")
             split_first(s - 1)
-            quantize_x(s + 1)
+            quantize_g(s - 2)
             split_second(s - 1)
-            if not output:
-                interleave(s + 2, "v")
-            elif more_x:
-                widen(s + 2, LAST_PLANE, "v")
-            else:
-                quantize_g(s - 3)
+            if more_x:
+                widen(s + 2, LAST_PLANE if s > 2 else 1, "v")
             split_third(s - 1)
-            if output and more_x:
-                quantize_g(s - 3)
-                interleave(s + 2, "g")
-            else:
+            if turned:
                 weigh_last(s - 1)
-            gate_terms(s - 1)
-            make_gate(s - 2, LAST)
-            empty_q(s, PAIRS, (1, 2) if more_x else (1,))
+            if not last:
+                quantize_x(s + 1)
+            if turned:
+                gate_terms(s - 1)
+            mm2(s - 2, 0)
+            mm2(s - 2, 1)
+            add_bias(s, 1)
             if not more_x:
-                finish(s - 4, LAST, "s")
-                make_gate(s - 2, 2)
-                add_out(s - 4, LAST)
-                store(s - 4, LAST, NT)
-            if more_planes:
-                for j in range(2) if output else (1,):
-                    widen(s + 3, j, "s")
-            gating(s - 2, 1)
-            gating(s - 2, 0)
-            if output:
-                mm2(s - 3, 0)
-                mm2(s - 3, 1)
-            gating(s - 2, LAST)
-            gating(s - 2, 2)
-            order = BACKWARDS if more_planes and output else PAIRS
-            squares(s, order[0])
-            squares(s, order[1])
-            if output:
-                mm2(s - 3, 2)
-            turn_pieces(s - 1)
-            if output:
-                mm2(s - 3, LAST)
-            mm1(s + 1, 0)
-            squares(s, order[2])
-            squares(s, order[3])
-            mm1(s + 1, 1)
-            mm1(s + 1, 2)
+                turn_pieces(s - 1)
+            mm2(s - 2, 2)
+            mm2(s - 2, LAST)
+            if more_x:
+                turn_pieces(s - 1)
+            add_bias(s, 0)
+            turn_q(s, PAIRS[:2], range(1))
+            add_bias(s, 3)
+            turn_q(s, PAIRS[:3], range(2))
+            add_bias(s, 2)
             unload_pieces(s - 1)
-            mm1(s + 1, LAST_PLANE)
-            if more_planes and output:
+            turn_q(s, PAIRS, range(2))
+            finish(s - 2, 1, "v")
+            finish(s - 2, 0, "v")
+            if not more_x:
+                store(s - 2, 0, 2)
+            if more_x:
+                widen(s + 2 if s > 2 else s + 3, 1 if s > 2 else 0, "s")
+                interleave(s + 2, "g")
+            make_gate(s - 1, 0)
+            make_gate(s - 1, 1)
+            turn_q(s, PAIRS, range(2, NT))
+            if more_x:
+                finish(s - 2, LAST, "v")
+            finish(s - 2, 2, "v")
+            if not more_x:
+                finish(s - 2, LAST, "s")
+                add_out(s - 2, LAST)
+                store(s - 2, 2, LAST)
+                store(s - 2, LAST, NT)
+            else:
+                store(s - 2, 0, NT)
+            make_gate(s - 1, 2)
+            make_gate(s - 1, LAST)
+            for i in (1, 0, 2, LAST):
+                squares(s, i)
+            if not last:
+                for t in range(PACK):
+                    mm1(s + 1, t)
+            for i in (1, 0, 2, LAST) if more_x else range(NT):
+                gating(s - 1, i)
+            if more_planes:
                 widen(s + 3, 2, "s")
             root(s)
-            if output:
-                finish(s - 3, 1, "v")
-                finish(s - 3, 0, "v")
-                if more_planes:
-                    finish(s - 3, LAST, "v")
-                finish(s - 3, 2, "v")
-                store(s - 3, 0, NT if more_planes else LAST)
-            make_gate(s - 1, 0)
 
         def last_steps():
             k = NCHUNKS - 1
-            make_gate(k - 2, LAST)
-            quantize_g(k - 3)
-            split_first(k - 1)
-            gating(k - 2, 0)
-            split_second(k - 1)
-            gating(k - 2, LAST)
-            split_third(k - 1)
-            empty_q(k, PAIRS, (1, 2))
-            mm2(k - 3, 0)
-            finish(k - 4, LAST, "s")
-            add_out(k - 4, LAST)
-            store(k - 4, LAST, NT)
-            turn_pieces(k - 1, "v")
-            gating(k - 2, 1)
-            mm2(k - 3, 1)
-            squares(k, 1)
-            squares(k, 0)
-            unload_pieces(k - 1)
-            make_gate(k - 1, 0)
-            gating(k - 2, 2)
-            make_gate(k - 1, 1)
-            squares(k, 3)
-            squares(k, 2)
-            root(k)
-            finish(k - 3, 0, "v")
-            make_gate(k - 1, LAST)
-            finish(k - 3, 1, "v")
-            make_gate(k - 1, 2)
-            store(k - 3, 0, 2)
-            mm2_turned(k - 3)
-            quantize_g(k - 2)
-            bias_turned(k - 3)
-            gating(k - 1, 1)
-            gating(k - 1, 0)
-            mm2(k - 2, 0, "s")
-            mm2(k - 2, LAST, "s")
-            mm2(k - 2, 1)
-            mm2(k - 2, 2)
-            turn_back(k - 3)
             split_first(k)
-            gating(k - 1, LAST)
-            split_second(k)
-            gating(k - 1, 2)
-            split_third(k)
-            turn_pieces(k, "v")
-            finish(k - 3, 2, "s")
-            unload_pieces(k)
-            finish(k - 3, LAST, "s")
-            store(k - 3, 2, NT)
-            finish(k - 2, 1, "v")
             quantize_g(k - 1)
-            for i in (0, 1, LAST):
-                make_gate(k, i)
-            mm2_turned(k - 1)
-            for i in (0, LAST):
-                finish(k - 2, i, "s")
-                add_out(k - 2, i)
-            finish(k - 2, 2, "v")
-            store(k - 2, 1, LAST)
-            make_gate(k, 2)
+            split_second(k)
             mm2(k - 1, 0, "s")
+            split_third(k)
+            turn_pieces(k, "s")
             mm2(k - 1, 1, "s")
-            bias_turned(k - 1)
-            store(k - 2, 0, 1)
-            gating(k, 1)
-            gating(k, 0)
-            turn_back(k - 1)
-            gating(k, LAST)
-            store(k - 2, LAST, NT)
             finish(k - 1, 0, "v")
             store(k - 1, 0, 1)
+            unload_pieces(k)
+            make_gate(k, 0)
+            make_gate(k, 1)
+            mm2_turned(k - 1)
+            make_gate(k, 2)
+            make_gate(k, LAST)
+            finish(k - 1, 1, "v")
+            store(k - 1, 1, 2)
+            bias_turned(k - 1)
+            turn_back(k - 1)
+            gating(k, 0)
+            gating(k, 1)
+            gating(k, 2)
             quantize_g_half(k, 0)
             mm2(k, 0)
             mm2(k, 1)
             for i in (2, LAST):
                 finish(k - 1, i, "s")
                 store(k - 1, i, i + 1)
-            gating(k, 2)
-            finish(k - 1, 1, "v")
-            store(k - 1, 1, 2)
+            gating(k, LAST)
+            finish(k, 0, "v")
+            store(k, 0, 1)
             quantize_g_half(k, 1)
             mm2(k, 2)
             mm2(k, LAST)
-            finish(k, 0, "s")
-            add_out(k, 0)
-            for i in (1, 2):
+            for i in range(1, NT):
                 finish(k, i, "v")
                 store(k, i, i + 1)
-            store(k, 0, 1)
-            finish(k, LAST, "v")
-            store(k, LAST, NT)
 
-        first_steps()
-        for s in range(2, NCHUNKS - 1):
+        first_step()
+        second_step()
+        for s in range(2, NCHUNKS):
             step(s)
         last_steps()

@@ -473,8 +473,9 @@ def tile_hydraattention_pb_t_kernel(tc, x_bytes, x_scale, mask, W_q, b_q, kv_kno
             turned = s - 1 in TURNED
             if more_x and s > 3:
                 widen(s + 2, 0, "s")
+            quantize_g_half(s - 2, 0)
             split_first(s - 1)
-            quantize_g(s - 2)
+            quantize_g_half(s - 2, 1)
             split_second(s - 1)
             if more_x:
                 widen(s + 2, LAST_PLANE if s > 2 else 1, "v")

@@ -28,6 +28,7 @@ NTILES = B * N // TILE
 NCHUNKS = B * N // CHUNK
 PER_IMG = N // CHUNK
 PIECES = 3
+SHARE = 128
 RUN = 4
 
 FLOPS = 2 * 2 * B * N * C * C
@@ -104,17 +105,17 @@ def tile_hydraattention_pb_t_kernel(tc, x_bytes, x_scale, mask, W_q, b_q, kv_kno
         xcodes = {}
         gcodes = {}
 
-        def widen(k, j, eng):
+        def widen(k, j, eng, first=0, end=CHUNK):
             t0 = k * CHUNK
             if k not in planes:
                 planes[k] = work.tile([P, PACK, CHUNK], BF16, name="planes", bufs=4, align_bytes=64)
             for start, width, t in x_tiles:
                 if start <= t0 < start + width:
-                    src = t[:, j, t0 - start : t0 - start + CHUNK].bitcast(FP8)
+                    src = t[:, j, t0 - start + first : t0 - start + end].bitcast(FP8)
             if eng == "s":
-                nc.scalar.activation(out=planes[k][:, j, :], in_=src, func=ACT.Copy, scale=xs[:, j : j + 1])
+                nc.scalar.activation(out=planes[k][:, j, first:end], in_=src, func=ACT.Copy, scale=xs[:, j : j + 1])
             else:
-                nc.vector.tensor_scalar(out=planes[k][:, j, :], in0=src, scalar1=xs[:, j : j + 1], scalar2=None, op0=ALU.mult)
+                nc.vector.tensor_scalar(out=planes[k][:, j, first:end], in0=src, scalar1=xs[:, j : j + 1], scalar2=None, op0=ALU.mult)
 
         def interleave_on_vector(dst, src):
             nc.vector.tensor_copy(out=dst.rearrange("p (c e) j -> p c j e", e=RUN), in_=src.rearrange("p j (c e) -> p c j e", e=RUN))
@@ -134,6 +135,12 @@ def tile_hydraattention_pb_t_kernel(tc, x_bytes, x_scale, mask, W_q, b_q, kv_kno
 
         def quantize(codes, scales, src):
             nc.vector.quantize_mx(out=codes.bitcast(FP8X4), scales=scales, in_=src)
+
+        def quantize_x_half(k, h):
+            if h == 0:
+                xcodes[k] = code_tiles("x")
+            pixels = slice(h * 2 * TILE, (h + 1) * 2 * TILE)
+            quantize(xcodes[k][0][:, pixels], xcodes[k][1][:, pixels], grouped[k][:, pixels, :].rearrange("p w j -> p (w j)"))
 
         def quantize_x(k):
             xcodes[k] = code_tiles("x")
@@ -176,7 +183,6 @@ def tile_hydraattention_pb_t_kernel(tc, x_bytes, x_scale, mask, W_q, b_q, kv_kno
         wo_codes = keep.tile([P, C], U32, name="wo_codes", align_bytes=64)
         wo_scales = keep.tile([P, C], U8, name="wo_scales", align_bytes=64)
         wo_grouped = keep.tile([P, C, PACK], BF16, name="wo_grouped", align_bytes=64)
-        bo_cols = keep.tile([P, PACK], F32, name="bo_cols")
         ab = keep.tile([P, 2, NTILES], F32, name="ab")
 
         m_ps, m_tag, m_home = take("v", [P, P], BF16)
@@ -211,19 +217,6 @@ def tile_hydraattention_pb_t_kernel(tc, x_bytes, x_scale, mask, W_q, b_q, kv_kno
                 nc.vector.tensor_scalar(out=kv_rows[img][:, i, :], in0=kv_planes[img][:].rearrange("p t m -> p (t m)"),
                                         scalar1=sel[:, i : i + 1], scalar2=None, op0=ALU.mult)
 
-        bo_ps = []
-
-        def turn_bo():
-            ps, tag, home = take("v", [P, PACK, TILE], BF16)
-            for j in range(PACK):
-                nc.tensor.transpose(ps[:, j, :], bo[:, j * TILE : (j + 1) * TILE], ident_b[:])
-            bo_ps.extend((ps, tag, home))
-
-        def unload_bo():
-            ps, tag, home = bo_ps
-            nc.vector.tensor_copy(out=bo_cols[:], in_=ps[:, :, 0])
-            home.append(tag)
-
         q_ps = {}
         q_sb = {}
         qt_ps = {}
@@ -231,6 +224,7 @@ def tile_hydraattention_pb_t_kernel(tc, x_bytes, x_scale, mask, W_q, b_q, kv_kno
         ss = {}
         rs = {}
         weights = {}
+        last_weights = {}
         rest = {}
         pieces_ps = {}
         piece_rows = {}
@@ -239,8 +233,6 @@ def tile_hydraattention_pb_t_kernel(tc, x_bytes, x_scale, mask, W_q, b_q, kv_kno
         gated = {}
         y_ps = {}
         y_sb = {}
-        yt_ps = {}
-        yt_sb = {}
 
         def mm1(k, t, role="s"):
             codes, scales = xcodes[k]
@@ -295,9 +287,9 @@ def tile_hydraattention_pb_t_kernel(tc, x_bytes, x_scale, mask, W_q, b_q, kv_kno
             nc.vector.tensor_sub(out=piece(k, 2), in0=rest.pop(k)[:], in1=piece(k, 1))
 
         def weigh_last(k):
-            weights[k] = work.tile([P, 2, 1], F32, name="pt")
+            last_weights[k] = work.tile([P, 2, 1], F32, name="pt")
             t = k * NT + LAST
-            nc.vector.tensor_scalar(out=weights[k][:], in0=ab[:, :, t : t + 1], scalar1=rs[k][:, LAST : LAST + 1], scalar2=None, op0=ALU.mult)
+            nc.vector.tensor_scalar(out=last_weights[k][:], in0=ab[:, :, t : t + 1], scalar1=rs[k][:, LAST : LAST + 1], scalar2=None, op0=ALU.mult)
 
         def turn_pieces(k, role="s"):
             pieces_ps[k] = take(role, [P, P], BF16)
@@ -309,18 +301,14 @@ def tile_hydraattention_pb_t_kernel(tc, x_bytes, x_scale, mask, W_q, b_q, kv_kno
             nc.scalar.copy(out=piece_rows[k][:], in_=ps[:])
             home.append(tag)
 
-        def gate_terms(k, eng="g"):
+        def gate_terms(k):
             terms[k] = work.tile([P, 2, PACK, TILE], F32, name="terms", bufs=2, align_bytes=64)
-            col = weights[k].shape[2] - 1
             for h in range(2):
-                vec, weight = by_plane(kv_all[k // PER_IMG][:, h, :]), weights[k][:, h, col : col + 1]
-                if eng == "g":
-                    nc.gpsimd.tensor_scalar(out=terms[k][:, h], in0=vec, scalar1=weight, scalar2=0.0, op0=ALU.mult, op1=ALU.add)
-                else:
-                    nc.vector.tensor_scalar(out=terms[k][:, h], in0=vec, scalar1=weight, scalar2=None, op0=ALU.mult)
+                nc.gpsimd.tensor_scalar(out=terms[k][:, h], in0=by_plane(kv_all[k // PER_IMG][:, h, :]),
+                                        scalar1=last_weights[k][:, h, :], scalar2=0.0, op0=ALU.mult, op1=ALU.add)
 
-        def make_gate(k, i, role="v"):
-            gate[k, i] = take(role, [P, PACK, TILE], F32)
+        def make_gate(k, i):
+            gate[k, i] = take("v", [P, PACK, TILE], F32)
             ps = gate[k, i][0]
             for t in range(PACK):
                 if k in TURNED and i == LAST:
@@ -339,10 +327,6 @@ def tile_hydraattention_pb_t_kernel(tc, x_bytes, x_scale, mask, W_q, b_q, kv_kno
                                     in1=q_sb[k][:, :, pixels].rearrange("p t (c e) -> p c t e", e=RUN), op=ALU.mult)
             home.append(tag)
 
-        def quantize_g(k):
-            gcodes[k] = code_tiles("g")
-            quantize(gcodes[k][0][:], gcodes[k][1][:], gated.pop(k)[:].rearrange("p w j -> p (w j)"))
-
         def quantize_g_half(k, h):
             if h == 0:
                 gcodes[k] = code_tiles("g")
@@ -358,7 +342,7 @@ def tile_hydraattention_pb_t_kernel(tc, x_bytes, x_scale, mask, W_q, b_q, kv_kno
 
         def finish(k, i, eng):
             if k not in y_sb:
-                y_sb[k] = work.tile([P, NT, C], F32, name="y", bufs=8)
+                y_sb[k] = work.tile([P, NT, C], F32, name="y", bufs=9)
             ps, tag, home = y_ps.pop((k, i))
             if eng == "v":
                 nc.vector.tensor_add(out=y_sb[k][:, i, :], in0=ps[:], in1=bo[:])
@@ -368,31 +352,6 @@ def tile_hydraattention_pb_t_kernel(tc, x_bytes, x_scale, mask, W_q, b_q, kv_kno
 
         def add_out(k, i):
             nc.gpsimd.tensor_add(out=y_sb[k][:, i, :], in0=y_sb[k][:, i, :], in1=bo[:])
-
-        def mm2_turned(k):
-            codes, scales = gcodes[k]
-            pixels = slice(2 * TILE, NT * TILE)
-            yt_ps[k] = []
-            for u in range(2):
-                yt_ps[k].append(take("s", [P, 2, 2 * TILE], F32))
-                for e in range(2):
-                    cols = slice((2 * u + e) * TILE, (2 * u + e + 1) * TILE)
-                    nc.tensor.matmul_mx(out=yt_ps[k][u][0][:, e, :], lhsT=wo_codes[:, cols].bitcast(FP8X4), lhsT_scale=wo_scales[:, cols],
-                                        rhs=codes[:, pixels].bitcast(FP8X4), rhs_scale=scales[:, pixels], start=True, stop=True)
-
-        def bias_turned(k):
-            yt_sb[k] = work.tile([P, PACK, 2 * TILE], F32, name="yt", bufs=2, align_bytes=64)
-            for u, (ps, tag, home) in enumerate(yt_ps.pop(k)):
-                for e in range(2):
-                    j = 2 * u + e
-                    nc.scalar.activation(out=yt_sb[k][:, j, :], in_=ps[:, e, :], func=ACT.Identity, bias=bo_cols[:, j : j + 1])
-                home.append(tag)
-
-        def turn_back(k):
-            for a in range(2):
-                y_ps[k, 2 + a] = take("s", [P, C], F32)
-                for j in range(PACK):
-                    nc.tensor.transpose(y_ps[k, 2 + a][0][:, j * TILE : (j + 1) * TILE], yt_sb[k][:, j, a * TILE : (a + 1) * TILE], ident[:])
 
         def store(k, i0, i1):
             t0 = (k * NT + i0) * TILE
@@ -426,29 +385,27 @@ def tile_hydraattention_pb_t_kernel(tc, x_bytes, x_scale, mask, W_q, b_q, kv_kno
             for i in BACKWARDS:
                 squares(0, i)
             free.update(s=free["v"], v=free["s"])
-            turn_bo()
             add_bias(1, 1)
             root(0)
 
         def second_step():
             split_first(0)
-            quantize(wo_codes[:], wo_scales[:], wo_grouped[:].rearrange("p w j -> p (w j)"))
+            quantize_x(2)
             split_second(0)
-            unload_bo()
             widen(3, 1, "v")
-            split_third(0)
             permute_kv(1)
-            widen(4, LAST_PLANE, "v")
+            split_third(0)
             select_kv(1)
             widen(3, LAST_PLANE, "v")
-            quantize_x(2)
+            quantize(wo_codes[:], wo_scales[:], wo_grouped[:].rearrange("p w j -> p (w j)"))
             interleave(3, "g")
             add_bias(1, 0)
             turn_q(1, PAIRS[:2], range(2))
             add_bias(1, 3)
-            turn_pieces(0, "v")
             turn_q(1, PAIRS[:3], range(3))
+            turn_pieces(0, "v")
             add_bias(1, 2)
+            widen(4, 2, "s")
             unload_pieces(0)
             turn_q(1, PAIRS, range(2))
             make_gate(0, 0)
@@ -456,7 +413,6 @@ def tile_hydraattention_pb_t_kernel(tc, x_bytes, x_scale, mask, W_q, b_q, kv_kno
             turn_q(1, PAIRS, range(2, NT))
             make_gate(0, 2)
             make_gate(0, LAST)
-            widen(4, 2, "s")
             for i in (1, 0, 2, LAST):
                 squares(1, i)
             for t in range(PACK):
@@ -471,30 +427,36 @@ def tile_hydraattention_pb_t_kernel(tc, x_bytes, x_scale, mask, W_q, b_q, kv_kno
             more_planes = s + 3 < NCHUNKS
             last = s + 1 == NCHUNKS
             turned = s - 1 in TURNED
+            if s == 2:
+                widen(s + 2, 1, "s")
             if more_x and s > 3:
-                widen(s + 2, 0, "s")
+                widen(s + 2, 0, "s", SHARE)
+            if more_x:
+                split_first(s - 1)
             quantize_g_half(s - 2, 0)
-            split_first(s - 1)
+            if not more_x:
+                split_first(s - 1)
             quantize_g_half(s - 2, 1)
+            if more_x and s > 3:
+                widen(s + 2, 0, "v", 0, SHARE)
             split_second(s - 1)
             if more_x:
-                widen(s + 2, LAST_PLANE if s > 2 else 1, "v")
-            split_third(s - 1)
+                widen(s + 2, LAST_PLANE, "v")
+            if not last:
+                quantize_x_half(s + 1, 0)
             if turned:
                 weigh_last(s - 1)
+            split_third(s - 1)
             if not last:
-                quantize_x(s + 1)
+                quantize_x_half(s + 1, 1)
             if turned:
                 gate_terms(s - 1)
             mm2(s - 2, 0)
             mm2(s - 2, 1)
             add_bias(s, 1)
-            if not more_x:
-                turn_pieces(s - 1)
             mm2(s - 2, 2)
             mm2(s - 2, LAST)
-            if more_x:
-                turn_pieces(s - 1)
+            turn_pieces(s - 1)
             add_bias(s, 0)
             turn_q(s, PAIRS[:2], range(1))
             add_bias(s, 3)
@@ -537,41 +499,38 @@ def tile_hydraattention_pb_t_kernel(tc, x_bytes, x_scale, mask, W_q, b_q, kv_kno
 
         def last_steps():
             k = NCHUNKS - 1
+            quantize_g_half(k - 1, 0)
             split_first(k)
-            quantize_g(k - 1)
+            quantize_g_half(k - 1, 1)
+            mm2(k - 1, 0)
+            mm2(k - 1, 1)
+            mm2(k - 1, 2)
+            mm2(k - 1, LAST, "s")
             split_second(k)
-            mm2(k - 1, 0, "s")
-            split_third(k)
-            turn_pieces(k, "s")
-            mm2(k - 1, 1, "s")
             finish(k - 1, 0, "v")
             store(k - 1, 0, 1)
-            unload_pieces(k)
-            make_gate(k, 0)
-            make_gate(k, 1)
-            mm2_turned(k - 1)
-            make_gate(k, 2)
-            make_gate(k, LAST)
+            split_third(k)
+            turn_pieces(k, "s")
             finish(k - 1, 1, "v")
             store(k - 1, 1, 2)
-            bias_turned(k - 1)
-            turn_back(k - 1)
-            gating(k, 0)
-            gating(k, 1)
-            gating(k, 2)
+            finish(k - 1, LAST, "s")
+            add_out(k - 1, LAST)
+            unload_pieces(k)
+            finish(k - 1, 2, "v")
+            store(k - 1, 2, LAST)
+            store(k - 1, LAST, NT)
+            for i in range(NT):
+                make_gate(k, i)
+            for i in range(LAST):
+                gating(k, i)
             quantize_g_half(k, 0)
             mm2(k, 0)
             mm2(k, 1)
-            for i in (2, LAST):
-                finish(k - 1, i, "s")
-                store(k - 1, i, i + 1)
             gating(k, LAST)
-            finish(k, 0, "v")
-            store(k, 0, 1)
             quantize_g_half(k, 1)
             mm2(k, 2)
             mm2(k, LAST)
-            for i in range(1, NT):
+            for i in range(NT):
                 finish(k, i, "v")
                 store(k, i, i + 1)
 

@@ -265,41 +265,44 @@ def tile_hydraattention_pb_t_kernel(tc, x_bytes, x_scale, mask, W_q, b_q, kv_kno
             nc.scalar.activation(out=junk[:], in_=ps[:].rearrange("p t m -> p (t m)"), func=ACT.Square, accum_out=ss[k][:, i : i + 1])
             home.append(tag)
 
-        def root(k):
-            rs[k] = work.tile([P, NT], F32, name="rs")
-            nc.scalar.activation(out=rs[k][:], in_=ss.pop(k)[:], func=ACT.Abs_reciprocal_sqrt)
+        def root(k, first=0, end=NT):
+            rs[k, first] = work.tile([P, end - first], F32, name="rs")
+            nc.scalar.activation(out=rs[k, first][:], in_=ss[k][:, first:end], func=ACT.Abs_reciprocal_sqrt)
 
-        def piece(k, q):
-            return pieces[k % 2][:, :, q * NT : (q + 1) * NT]
+        def piece(k, q, first, end):
+            return pieces[(k + first // 2) % 2][:, :, q * NT + first : q * NT + end]
 
-        def split_first(k):
-            weights[k] = work.tile([P, 2, NT], F32, name="pw")
-            spread = rs[k][:].unsqueeze(1).to_broadcast([P, 2, NT])
-            nc.vector.tensor_mul(out=weights[k][:], in0=ab[:, :, k * NT : (k + 1) * NT], in1=spread)
-            nc.vector.tensor_mul(out=piece(k, 0), in0=ab[:, :, k * NT : (k + 1) * NT], in1=spread)
+        def split_first(k, first=0, end=NT):
+            weights[k, first] = work.tile([P, 2, end - first], F32, name="pw")
+            spread = rs[k, first][:].unsqueeze(1).to_broadcast([P, 2, end - first])
+            both = ab[:, :, k * NT + first : k * NT + end]
+            nc.vector.tensor_mul(out=weights[k, first][:], in0=both, in1=spread)
+            nc.vector.tensor_mul(out=piece(k, 0, first, end), in0=both, in1=spread)
 
-        def split_second(k):
-            rest[k] = work.tile([P, 2, NT], F32, name="rest")
-            nc.vector.tensor_sub(out=rest[k][:], in0=weights[k][:], in1=piece(k, 0))
-            nc.vector.tensor_sub(out=piece(k, 1), in0=weights[k][:], in1=piece(k, 0))
+        def split_second(k, first=0, end=NT):
+            rest[k, first] = work.tile([P, 2, end - first], F32, name="rest")
+            nc.vector.tensor_sub(out=rest[k, first][:], in0=weights[k, first][:], in1=piece(k, 0, first, end))
+            nc.vector.tensor_sub(out=piece(k, 1, first, end), in0=weights[k, first][:], in1=piece(k, 0, first, end))
 
-        def split_third(k):
-            nc.vector.tensor_sub(out=piece(k, 2), in0=rest.pop(k)[:], in1=piece(k, 1))
+        def split_third(k, first=0, end=NT):
+            nc.vector.tensor_sub(out=piece(k, 2, first, end), in0=rest.pop((k, first))[:], in1=piece(k, 1, first, end))
 
         def weigh_last(k):
             last_weights[k] = work.tile([P, 2, 1], F32, name="pt")
             t = k * NT + LAST
-            nc.vector.tensor_scalar(out=last_weights[k][:], in0=ab[:, :, t : t + 1], scalar1=rs[k][:, LAST : LAST + 1], scalar2=None, op0=ALU.mult)
+            nc.vector.tensor_scalar(out=last_weights[k][:], in0=ab[:, :, t : t + 1], scalar1=rs[k, 0][:, LAST : LAST + 1], scalar2=None, op0=ALU.mult)
 
-        def turn_pieces(k, role="s"):
-            pieces_ps[k] = take(role, [P, P], BF16)
-            nc.tensor.transpose(pieces_ps[k][0][:], pieces[k % 2][:].rearrange("p h x -> p (h x)"), ident_b[:])
+        def turn_pieces(k, role="s", first=0):
+            pieces_ps[k, first] = take(role, [P, P], BF16)
+            nc.tensor.transpose(pieces_ps[k, first][0][:], pieces[(k + first // 2) % 2][:].rearrange("p h x -> p (h x)"), ident_b[:])
 
-        def unload_pieces(k):
-            piece_rows[k] = work.tile([P, P], BF16, name="rows_of", bufs=2, align_bytes=64)
-            ps, tag, home = pieces_ps.pop(k)
-            nc.scalar.copy(out=piece_rows[k][:], in_=ps[:])
+        def unload_pieces(k, first=0, end=NT):
+            rows = work.tile([P, P], BF16, name="rows_of", bufs=2, align_bytes=64)
+            ps, tag, home = pieces_ps.pop((k, first))
+            nc.scalar.copy(out=rows[:], in_=ps[:])
             home.append(tag)
+            for i in range(first, end):
+                piece_rows[k, i] = rows
 
         def gate_terms(k):
             terms[k] = work.tile([P, 2, PACK, TILE], F32, name="terms", bufs=2, align_bytes=64)
@@ -315,7 +318,7 @@ def tile_hydraattention_pb_t_kernel(tc, x_bytes, x_scale, mask, W_q, b_q, kv_kno
                     for h in range(2):
                         nc.tensor.matmul(ps[:, t, :], lhsT=terms[k][:, h, t, :], rhs=ident[:], is_transpose=True, start=h == 0, stop=h == 1)
                 else:
-                    nc.tensor.matmul(ps[:, t, :], lhsT=kv_rows[k // PER_IMG][:, i, t * TILE : (t + 1) * TILE], rhs=piece_rows[k][:], start=True, stop=True)
+                    nc.tensor.matmul(ps[:, t, :], lhsT=kv_rows[k // PER_IMG][:, i, t * TILE : (t + 1) * TILE], rhs=piece_rows[k, i][:], start=True, stop=True)
 
         def gating(k, i):
             if k not in gated:
@@ -392,8 +395,8 @@ def tile_hydraattention_pb_t_kernel(tc, x_bytes, x_scale, mask, W_q, b_q, kv_kno
             split_first(0)
             quantize_x(2)
             split_second(0)
-            widen(3, 1, "v")
             permute_kv(1)
+            widen(3, 1, "v")
             split_third(0)
             select_kv(1)
             widen(3, LAST_PLANE, "v")
@@ -444,9 +447,9 @@ def tile_hydraattention_pb_t_kernel(tc, x_bytes, x_scale, mask, W_q, b_q, kv_kno
                 widen(s + 2, LAST_PLANE, "v")
             if not last:
                 quantize_x_half(s + 1, 0)
+            split_third(s - 1)
             if turned:
                 weigh_last(s - 1)
-            split_third(s - 1)
             if not last:
                 quantize_x_half(s + 1, 1)
             if turned:
@@ -486,11 +489,12 @@ def tile_hydraattention_pb_t_kernel(tc, x_bytes, x_scale, mask, W_q, b_q, kv_kno
                 store(s - 2, 0, NT)
             make_gate(s - 1, 2)
             make_gate(s - 1, LAST)
+            if last:
+                return
             for i in (1, 0, 2, LAST):
                 squares(s, i)
-            if not last:
-                for t in range(PACK):
-                    mm1(s + 1, t)
+            for t in range(PACK):
+                mm1(s + 1, t)
             for i in (1, 0, 2, LAST) if more_x else range(NT):
                 gating(s - 1, i)
             if more_planes:
@@ -499,34 +503,49 @@ def tile_hydraattention_pb_t_kernel(tc, x_bytes, x_scale, mask, W_q, b_q, kv_kno
 
         def last_steps():
             k = NCHUNKS - 1
+            for i in (1, 0, 2):
+                squares(k, i)
+            root(k, 0, 2)
+            squares(k, LAST)
+            root(k, 2, NT)
+            for i in range(LAST):
+                gating(k - 1, i)
+            split_first(k, 0, 2)
+            gating(k - 1, LAST)
+            split_second(k, 0, 2)
             quantize_g_half(k - 1, 0)
-            split_first(k)
+            split_first(k, 2, NT)
             quantize_g_half(k - 1, 1)
+            split_third(k, 0, 2)
+            split_second(k, 2, NT)
             mm2(k - 1, 0)
             mm2(k - 1, 1)
-            mm2(k - 1, 2)
+            turn_pieces(k, "s", 0)
+            mm2(k - 1, 2, "s")
             mm2(k - 1, LAST, "s")
-            split_second(k)
             finish(k - 1, 0, "v")
             store(k - 1, 0, 1)
-            split_third(k)
-            turn_pieces(k, "s")
+            split_third(k, 2, NT)
+            unload_pieces(k, 0, 2)
+            make_gate(k, 0)
+            turn_pieces(k, "s", 2)
+            make_gate(k, 1)
             finish(k - 1, 1, "v")
             store(k - 1, 1, 2)
-            finish(k - 1, LAST, "s")
-            add_out(k - 1, LAST)
-            unload_pieces(k)
-            finish(k - 1, 2, "v")
+            finish(k - 1, 2, "s")
+            add_out(k - 1, 2)
+            unload_pieces(k, 2, NT)
+            make_gate(k, 2)
+            make_gate(k, LAST)
             store(k - 1, 2, LAST)
-            store(k - 1, LAST, NT)
-            for i in range(NT):
-                make_gate(k, i)
             for i in range(LAST):
                 gating(k, i)
             quantize_g_half(k, 0)
             mm2(k, 0)
             mm2(k, 1)
             gating(k, LAST)
+            finish(k - 1, LAST, "v")
+            store(k - 1, LAST, NT)
             quantize_g_half(k, 1)
             mm2(k, 2)
             mm2(k, LAST)

@@ -34,7 +34,7 @@ RUN = 4
 FLOPS = 2 * 2 * B * N * C * C
 
 X_LOADS = ((0, 0, 512), (0, 512, 512), (0, 1024, 1024), (0, 2048, 2048), (1, 0, 2048), (1, 2048, 2048))
-TURNED = range(1, 14)
+TURNED = (*range(1, 13), 14)
 PAIRS = (1, 0, 3, 2)
 BACKWARDS = (3, 2, 1, 0)
 
@@ -430,17 +430,15 @@ def tile_hydraattention_pb_t_kernel(tc, x_bytes, x_scale, mask, W_q, b_q, kv_kno
             more_planes = s + 3 < NCHUNKS
             last = s + 1 == NCHUNKS
             turned = s - 1 in TURNED
-            if s == 2:
-                widen(s + 2, 1, "s")
-            if more_x and s > 3:
-                widen(s + 2, 0, "s", SHARE)
+            if more_x and s > 2:
+                widen(s + 2, 0, "s", SHARE, CHUNK - TILE)
             if more_x:
                 split_first(s - 1)
             quantize_g_half(s - 2, 0)
             if not more_x:
                 split_first(s - 1)
             quantize_g_half(s - 2, 1)
-            if more_x and s > 3:
+            if more_x and s > 2:
                 widen(s + 2, 0, "v", 0, SHARE)
             split_second(s - 1)
             if more_x:
@@ -465,6 +463,11 @@ def tile_hydraattention_pb_t_kernel(tc, x_bytes, x_scale, mask, W_q, b_q, kv_kno
             add_bias(s, 3)
             turn_q(s, PAIRS[:3], range(2))
             add_bias(s, 2)
+            if more_x:
+                turn_q(s, PAIRS, range(LAST))
+                widen(s + 2, 1, "s")
+                if s > 2:
+                    widen(s + 2, 0, "s", CHUNK - TILE)
             unload_pieces(s - 1)
             turn_q(s, PAIRS, range(2))
             finish(s - 2, 1, "v")
@@ -472,7 +475,6 @@ def tile_hydraattention_pb_t_kernel(tc, x_bytes, x_scale, mask, W_q, b_q, kv_kno
             if not more_x:
                 store(s - 2, 0, 2)
             if more_x:
-                widen(s + 2 if s > 2 else s + 3, 1 if s > 2 else 0, "s")
                 interleave(s + 2, "g")
             make_gate(s - 1, 0)
             make_gate(s - 1, 1)

from contextlib import ExitStack

import concourse.mybir as mybir
from concourse.masks import make_identity

F32 = mybir.dt.float32
BF16 = mybir.dt.bfloat16
U32 = mybir.dt.uint32
U8 = mybir.dt.uint8
FP8 = mybir.dt.float8_e4m3fn
FP8X4 = mybir.dt.float8_e4m3fn_x4
ALU = mybir.AluOpType
ACT = mybir.ActivationFunctionType
AXIS = mybir.AxisListType

B = 2
C = 512
N = 4096
P = 128
HALF = P // 2
PACK = 4
TILE = 128
CHUNK = 512
NT = CHUNK // TILE
LAST = NT - 1
LAST_PLANE = PACK - 1
NTILES = B * N // TILE
NCHUNKS = B * N // CHUNK
PER_IMG = N // CHUNK
PIECES = 3
SHARE = 128
RUN = 4

FLOPS = 2 * 2 * B * N * C * C

X_LOADS = ((0, 0, 512), (0, 512, 512), (0, 1024, 1024), (0, 2048, 2048), (1, 0, 2048), (1, 2048, 2048))
TURNED = (*range(1, 13), 14)
PAIRS = (1, 0, 3, 2)
BACKWARDS = (3, 2, 1, 0)


def tile_hydraattention_pb_t_kernel(tc, x_bytes, x_scale, mask, W_q, b_q, kv_know, kv_mask, W_out, b_out, out):
    nc = tc.nc
    out_rows = out.rearrange("b t c -> (b t) c")

    with ExitStack() as ctx:
        keep = ctx.enter_context(tc.tile_pool(name="keep", bufs=1))
        work = ctx.enter_context(tc.tile_pool(name="work", bufs=3))
        psum = ctx.enter_context(tc.psum_pool(name="psum", bufs=1))
        ctx.enter_context(tc.manual_schedule())

        free = {"s": [f"a{i}" for i in range(4)], "v": [f"b{i}" for i in range(4)]}

        def take(role, shape, dtype):
            home = free[role]
            tag = home.pop(0)
            return psum.tile(shape, dtype, name="bank_" + tag, tag=tag), tag, home

        x_tiles = []

        def load_x(i):
            img, t0, width = X_LOADS[i]
            t = keep.tile([P, PACK, width], U8, name=f"xb{i}", align_bytes=64)
            nc.sync.dma_start(out=t[:], in_=x_bytes[img].rearrange("(p j) h w -> p j (h w)", j=PACK)[:, :, t0 : t0 + width])
            x_tiles.append((img * N + t0, width, t))

        kv_all = {}
        kv_half = {}

        def load_kv_all(img):
            kv_all[img] = keep.tile([P, 2, C], BF16, name=f"kv_all{img}")
            for h, vec in enumerate((kv_know, kv_mask)):
                nc.sync.dma_start(out=kv_all[img][:, h, :], in_=vec[img].rearrange("o c -> (o c)").partition_broadcast(P))

        def load_kv_half(img):
            kv_half[img] = keep.tile([P, C], BF16, name=f"kv_half{img}")
            for h, vec in enumerate((kv_know, kv_mask)):
                nc.sync.dma_start(out=kv_half[img][h * HALF : (h + 1) * HALF, :], in_=vec[img].rearrange("o c -> (o c)").partition_broadcast(HALF))

        xs = keep.tile([P, PACK], F32, name="xs")
        nc.sync.dma_start(out=xs[:], in_=x_scale.rearrange("o (p j) a b -> p (o j a b)", j=PACK))
        load_x(0)
        wq_raw = keep.tile([P, PACK, C], BF16, name="wq_raw")
        nc.sync.dma_start(out=wq_raw[:], in_=W_q.rearrange("(p j) w -> p j w", j=PACK))
        bq_raw = keep.tile([P, PACK], BF16, name="bq_raw")
        nc.sync.dma_start(out=bq_raw[:], in_=b_q.rearrange("(p t) -> p t", t=PACK))
        load_x(1)
        mrow = keep.tile([P, P], BF16, name="mrow", align_bytes=64)
        nc.sync.dma_start(out=mrow[0:NTILES, :], in_=mask.rearrange("b o (r q) w -> (b o r) (q w)", q=2))
        load_x(2)
        load_kv_half(0)
        wo_raw = keep.tile([P, PACK, C], BF16, name="wo_raw")
        nc.sync.dma_start(out=wo_raw[:], in_=W_out.rearrange("(p j) w -> p j w", j=PACK))
        load_x(3)
        bo = keep.tile([P, C], BF16, name="bo", align_bytes=64)
        nc.sync.dma_start(out=bo[:], in_=b_out.partition_broadcast(P))
        load_kv_half(1)
        load_kv_all(0)
        load_x(4)
        load_kv_all(1)
        load_x(5)

        planes = {}
        grouped = {}
        xcodes = {}
        gcodes = {}

        def widen(k, j, eng, first=0, end=CHUNK):
            t0 = k * CHUNK
            if k not in planes:
                planes[k] = work.tile([P, PACK, CHUNK], BF16, name="planes", bufs=4, align_bytes=64)
            for start, width, t in x_tiles:
                if start <= t0 < start + width:
                    src = t[:, j, t0 - start + first : t0 - start + end].bitcast(FP8)
            if eng == "s":
                nc.scalar.activation(out=planes[k][:, j, first:end], in_=src, func=ACT.Copy, scale=xs[:, j : j + 1])
            else:
                nc.vector.tensor_scalar(out=planes[k][:, j, first:end], in0=src, scalar1=xs[:, j : j + 1], scalar2=None, op0=ALU.mult)

        def interleave_on_vector(dst, src):
            nc.vector.tensor_copy(out=dst.rearrange("p (c e) j -> p c j e", e=RUN), in_=src.rearrange("p j (c e) -> p c j e", e=RUN))

        def interleave(k, eng):
            grouped[k] = work.tile([P, CHUNK, PACK], BF16, name="grouped", bufs=2, align_bytes=64)
            src = planes.pop(k)[:]
            if eng == "g":
                nc.gpsimd.tensor_scalar(out=grouped[k][:], in0=src.rearrange("p j w -> p w j"), scalar1=1.0, scalar2=0.0, op0=ALU.mult, op1=ALU.add)
            else:
                interleave_on_vector(grouped[k][:], src)

        def code_tiles(name):
            codes = work.tile([P, CHUNK], U32, name=name + "codes", bufs=2, align_bytes=64)
            scales = work.tile([P, CHUNK], U8, name=name + "scales", bufs=2, align_bytes=64)
            return codes, scales

        def quantize(codes, scales, src):
            nc.vector.quantize_mx(out=codes.bitcast(FP8X4), scales=scales, in_=src)

        def quantize_x_half(k, h):
            if h == 0:
                xcodes[k] = code_tiles("x")
            pixels = slice(h * 2 * TILE, (h + 1) * 2 * TILE)
            quantize(xcodes[k][0][:, pixels], xcodes[k][1][:, pixels], grouped[k][:, pixels, :].rearrange("p w j -> p (w j)"))

        def quantize_x(k):
            xcodes[k] = code_tiles("x")
            quantize(xcodes[k][0][:], xcodes[k][1][:], grouped.pop(k)[:].rearrange("p w j -> p (w j)"))

        ident = keep.tile([P, P], F32, name="ident", align_bytes=64)
        make_identity(nc, ident[:])
        nc.vector.memset(mrow[HALF:P, :], 0.0)
        pieces = [keep.tile([P, 2, HALF], BF16, name=f"pieces{i}", align_bytes=64) for i in range(2)]
        for t in pieces:
            nc.vector.memset(t[:], 0.0)
        ident_b = keep.tile([P, P], BF16, name="ident_b", align_bytes=64)
        nc.vector.tensor_copy(out=ident_b[:], in_=ident[:])
        sel = keep.tile([P, NT], F32, name="sel")
        nc.vector.tensor_reduce(out=sel[:], in_=ident[:].rearrange("p (h q i) -> p i h q", h=2, i=NT)[:, :, :, 0:PIECES], axis=AXIS.XY, op=ALU.add)

        wq_grouped = keep.tile([P, PACK, TILE, PACK], BF16, name="wq_grouped", align_bytes=64)
        wq_codes = keep.tile([P, C], U32, name="wq_codes", align_bytes=64)
        wq_scales = keep.tile([P, C], U8, name="wq_scales", align_bytes=64)

        def quantize_wq(u):
            cols = slice(u * 2 * TILE, (u + 1) * 2 * TILE)
            quantize(wq_codes[:, cols], wq_scales[:, cols], wq_grouped[:, 2 * u : 2 * u + 2].rearrange("p t m j -> p (t m j)"))

        warm = keep.tile([P, 1], F32, name="warm")
        nc.scalar.activation(out=warm[:], in_=ident[:, 0:1], func=ACT.Abs_reciprocal_sqrt, bias=1.0)
        widen(0, LAST_PLANE, "s")
        for u in range(2):
            nc.scalar.copy(out=wq_grouped[:, 2 * u : 2 * u + 2].rearrange("p t m j -> p m j t"),
                           in_=wq_raw[:].rearrange("p j (m t) -> p m j t", t=PACK)[:, :, :, 2 * u : 2 * u + 2])
        bq = keep.tile([P, PACK], F32, name="bq")
        nc.scalar.copy(out=bq[:], in_=bq_raw[:])
        for j in range(LAST_PLANE):
            widen(0, j, "v")
        interleave(0, "v")
        quantize_wq(0)
        quantize_x(0)
        quantize_wq(1)

        wo_codes = keep.tile([P, C], U32, name="wo_codes", align_bytes=64)
        wo_scales = keep.tile([P, C], U8, name="wo_scales", align_bytes=64)
        wo_grouped = keep.tile([P, C, PACK], BF16, name="wo_grouped", align_bytes=64)
        ab = keep.tile([P, 2, NTILES], F32, name="ab")

        m_ps, m_tag, m_home = take("v", [P, P], BF16)
        nc.tensor.transpose(m_ps[:], mrow[:], ident_b[:])
        m = m_ps[:, 0:NTILES]
        inv = keep.tile([P, NTILES], F32, name="inv")
        damp = keep.tile([P, NTILES], F32, name="damp")
        m07 = keep.tile([P, NTILES], F32, name="m07")

        def mask_factors():
            nc.vector.tensor_scalar(out=inv[:], in0=m, scalar1=-1.0, scalar2=1.0, op0=ALU.mult, op1=ALU.add)
            nc.vector.tensor_scalar(out=damp[:], in0=m, scalar1=-0.7, scalar2=1.0, op0=ALU.mult, op1=ALU.add)
            nc.vector.tensor_scalar(out=m07[:], in0=m, scalar1=0.7, scalar2=None, op0=ALU.mult)

        def mask_weights():
            nc.vector.tensor_mul(out=ab[:, 0, :], in0=inv[:], in1=damp[:])
            nc.vector.tensor_mul(out=ab[:, 1, :], in0=m, in1=m07[:])
            m_home.append(m_tag)

        def by_plane(vec):
            return vec.rearrange("p (m t) -> p t m", t=PACK)

        kv_rows = {img: keep.tile([P, NT, C], BF16, name=f"kv_rows{img}", align_bytes=64) for img in range(B)}
        kv_planes = {}

        def permute_kv(img):
            kv_planes[img] = keep.tile([P, PACK, TILE], BF16, name=f"kv_planes{img}", align_bytes=64)
            nc.vector.tensor_copy(out=kv_planes[img][:], in_=by_plane(kv_half[img][:]))

        def select_kv(img):
            for i in range(NT):
                nc.vector.tensor_scalar(out=kv_rows[img][:, i, :], in0=kv_planes[img][:].rearrange("p t m -> p (t m)"),
                                        scalar1=sel[:, i : i + 1], scalar2=None, op0=ALU.mult)

        q_ps = {}
        q_sb = {}
        qt_ps = {}
        q_turned = set()
        ss = {}
        rs = {}
        weights = {}
        last_weights = {}
        rest = {}
        pieces_ps = {}
        piece_rows = {}
        terms = {}
        gate = {}
        gated = {}
        y_ps = {}
        y_sb = {}

        def mm1(k, t, role="s"):
            codes, scales = xcodes[k]
            cols = slice(t * TILE, (t + 1) * TILE)
            q_ps[k, t] = take(role, [P, CHUNK], F32)
            nc.tensor.matmul_mx(out=q_ps[k, t][0][:], lhsT=wq_codes[:, cols].bitcast(FP8X4), lhsT_scale=wq_scales[:, cols],
                                rhs=codes[:].bitcast(FP8X4), rhs_scale=scales[:], start=True, stop=True)

        def add_bias(k, t):
            if k not in q_sb:
                q_sb[k] = work.tile([P, PACK, CHUNK], F32, name="qb", bufs=4, align_bytes=64)
            ps, tag, home = q_ps.pop((k, t))
            nc.scalar.activation(out=q_sb[k][:, t, :], in_=ps[:], func=ACT.Identity, bias=bq[:, t : t + 1])
            home.append(tag)

        def turn_q(k, planes_done, tiles):
            for i in tiles:
                if (k, i) not in qt_ps:
                    qt_ps[k, i] = take("s", [P, PACK, TILE], F32)
                for t in planes_done:
                    if (k, i, t) not in q_turned:
                        q_turned.add((k, i, t))
                        nc.tensor.transpose(qt_ps[k, i][0][:, t, :], q_sb[k][:, t, i * TILE : (i + 1) * TILE], ident[:])

        def squares(k, i):
            if k not in ss:
                ss[k] = work.tile([P, NT], F32, name="ss")
            junk = work.tile([P, C], BF16, name="junk", bufs=NT)
            ps, tag, home = qt_ps.pop((k, i))
            nc.scalar.activation(out=junk[:], in_=ps[:].rearrange("p t m -> p (t m)"), func=ACT.Square, accum_out=ss[k][:, i : i + 1])
            home.append(tag)

        def root(k, first=0, end=NT):
            rs[k, first] = work.tile([P, end - first], F32, name="rs")
            nc.scalar.activation(out=rs[k, first][:], in_=ss[k][:, first:end], func=ACT.Abs_reciprocal_sqrt)

        def piece(k, q, first, end):
            return pieces[(k + first // 2) % 2][:, :, q * NT + first : q * NT + end]

        def split_first(k, first=0, end=NT):
            weights[k, first] = work.tile([P, 2, end - first], F32, name="pw")
            spread = rs[k, first][:].unsqueeze(1).to_broadcast([P, 2, end - first])
            both = ab[:, :, k * NT + first : k * NT + end]
            nc.vector.tensor_mul(out=weights[k, first][:], in0=both, in1=spread)
            nc.vector.tensor_mul(out=piece(k, 0, first, end), in0=both, in1=spread)

        def split_second(k, first=0, end=NT):
            rest[k, first] = work.tile([P, 2, end - first], F32, name="rest")
            nc.vector.tensor_sub(out=rest[k, first][:], in0=weights[k, first][:], in1=piece(k, 0, first, end))
            nc.vector.tensor_sub(out=piece(k, 1, first, end), in0=weights[k, first][:], in1=piece(k, 0, first, end))

        def split_third(k, first=0, end=NT):
            nc.vector.tensor_sub(out=piece(k, 2, first, end), in0=rest.pop((k, first))[:], in1=piece(k, 1, first, end))

        def weigh_last(k):
            last_weights[k] = work.tile([P, 2, 1], F32, name="pt")
            t = k * NT + LAST
            nc.vector.tensor_scalar(out=last_weights[k][:], in0=ab[:, :, t : t + 1], scalar1=rs[k, 0][:, LAST : LAST + 1], scalar2=None, op0=ALU.mult)

        def turn_pieces(k, role="s", first=0):
            pieces_ps[k, first] = take(role, [P, P], BF16)
            nc.tensor.transpose(pieces_ps[k, first][0][:], pieces[(k + first // 2) % 2][:].rearrange("p h x -> p (h x)"), ident_b[:])

        def unload_pieces(k, first=0, end=NT):
            rows = work.tile([P, P], BF16, name="rows_of", bufs=2, align_bytes=64)
            ps, tag, home = pieces_ps.pop((k, first))
            nc.scalar.copy(out=rows[:], in_=ps[:])
            home.append(tag)
            for i in range(first, end):
                piece_rows[k, i] = rows

        def gate_terms(k):
            terms[k] = work.tile([P, 2, PACK, TILE], F32, name="terms", bufs=2, align_bytes=64)
            for h in range(2):
                nc.gpsimd.tensor_scalar(out=terms[k][:, h], in0=by_plane(kv_all[k // PER_IMG][:, h, :]),
                                        scalar1=last_weights[k][:, h, :], scalar2=0.0, op0=ALU.mult, op1=ALU.add)

        def make_gate(k, i):
            gate[k, i] = take("v", [P, PACK, TILE], F32)
            ps = gate[k, i][0]
            for t in range(PACK):
                if k in TURNED and i == LAST:
                    for h in range(2):
                        nc.tensor.matmul(ps[:, t, :], lhsT=terms[k][:, h, t, :], rhs=ident[:], is_transpose=True, start=h == 0, stop=h == 1)
                else:
                    nc.tensor.matmul(ps[:, t, :], lhsT=kv_rows[k // PER_IMG][:, i, t * TILE : (t + 1) * TILE], rhs=piece_rows[k, i][:], start=True, stop=True)

        def gating(k, i):
            if k not in gated:
                gated[k] = work.tile([P, CHUNK, PACK], BF16, name="gated", bufs=2, align_bytes=64)
            ps, tag, home = gate.pop((k, i))
            pixels = slice(i * TILE, (i + 1) * TILE)
            nc.vector.tensor_tensor(out=gated[k][:, pixels, :].rearrange("p (c e) t -> p c t e", e=RUN),
                                    in0=ps[:].rearrange("p t (c e) -> p c t e", e=RUN),
                                    in1=q_sb[k][:, :, pixels].rearrange("p t (c e) -> p c t e", e=RUN), op=ALU.mult)
            home.append(tag)

        def quantize_g_half(k, h):
            if h == 0:
                gcodes[k] = code_tiles("g")
            pixels = slice(h * 2 * TILE, (h + 1) * 2 * TILE)
            quantize(gcodes[k][0][:, pixels], gcodes[k][1][:, pixels], gated[k][:, pixels, :].rearrange("p w j -> p (w j)"))

        def mm2(k, i, role="v"):
            codes, scales = gcodes[k]
            pixels = slice(i * TILE, (i + 1) * TILE)
            y_ps[k, i] = take(role, [P, C], F32)
            nc.tensor.matmul_mx(out=y_ps[k, i][0][:], lhsT=codes[:, pixels].bitcast(FP8X4), lhsT_scale=scales[:, pixels],
                                rhs=wo_codes[:].bitcast(FP8X4), rhs_scale=wo_scales[:], start=True, stop=True)

        def finish(k, i, eng):
            if k not in y_sb:
                y_sb[k] = work.tile([P, NT, C], F32, name="y", bufs=9)
            ps, tag, home = y_ps.pop((k, i))
            if eng == "v":
                nc.vector.tensor_add(out=y_sb[k][:, i, :], in0=ps[:], in1=bo[:])
            else:
                nc.scalar.copy(out=y_sb[k][:, i, :], in_=ps[:])
            home.append(tag)

        def add_out(k, i):
            nc.gpsimd.tensor_add(out=y_sb[k][:, i, :], in0=y_sb[k][:, i, :], in1=bo[:])

        def store(k, i0, i1):
            t0 = (k * NT + i0) * TILE
            nc.sync.dma_start(out=out_rows[t0 : t0 + (i1 - i0) * TILE, :].rearrange("(a p) c -> p a c", p=P), in_=y_sb[k][:, i0:i1, :])

        def first_step():
            widen(1, 0, "s")
            widen(1, 1, "s")
            for t in range(PACK):
                mm1(0, t)
            widen(1, 2, "v")
            widen(1, LAST_PLANE, "v")
            mask_factors()
            interleave(1, "v")
            mask_weights()
            widen(2, 0, "v")
            quantize_x(1)
            for j in range(1, PACK):
                widen(2, j, "v")
            permute_kv(0)
            interleave(2, "v")
            select_kv(0)
            interleave_on_vector(wo_grouped[:], wo_raw[:])
            for t in range(PACK):
                add_bias(0, t)
                turn_q(0, range(t + 1), range(t + 1))
            for t in range(PACK):
                mm1(1, t, "v")
            widen(3, 0, "s")
            widen(3, 2, "s")
            for i in BACKWARDS:
                squares(0, i)
            free.update(s=free["v"], v=free["s"])
            add_bias(1, 1)
            root(0)

        def second_step():
            split_first(0)
            quantize_x(2)
            split_second(0)
            permute_kv(1)
            widen(3, 1, "v")
            split_third(0)
            select_kv(1)
            widen(3, LAST_PLANE, "v")
            quantize(wo_codes[:], wo_scales[:], wo_grouped[:].rearrange("p w j -> p (w j)"))
            interleave(3, "g")
            add_bias(1, 0)
            turn_q(1, PAIRS[:2], range(2))
            add_bias(1, 3)
            turn_q(1, PAIRS[:3], range(3))
            turn_pieces(0, "v")
            add_bias(1, 2)
            widen(4, 2, "s")
            unload_pieces(0)
            turn_q(1, PAIRS, range(2))
            make_gate(0, 0)
            make_gate(0, 1)
            turn_q(1, PAIRS, range(2, NT))
            make_gate(0, 2)
            make_gate(0, LAST)
            for i in (1, 0, 2, LAST):
                squares(1, i)
            for t in range(PACK):
                mm1(2, t)
            for i in PAIRS:
                gating(0, i)
            widen(4, 0, "s")
            root(1)

        def step(s):
            more_x = s + 2 < NCHUNKS
            more_planes = s + 3 < NCHUNKS
            last = s + 1 == NCHUNKS
            turned = s - 1 in TURNED
            if more_x and s > 2:
                widen(s + 2, 0, "s", SHARE, CHUNK - TILE)
            if more_x:
                split_first(s - 1)
            quantize_g_half(s - 2, 0)
            if not more_x:
                split_first(s - 1)
            quantize_g_half(s - 2, 1)
            if more_x and s > 2:
                widen(s + 2, 0, "v", 0, SHARE)
            split_second(s - 1)
            if more_x:
                widen(s + 2, LAST_PLANE, "v")
            if not last:
                quantize_x_half(s + 1, 0)
            split_third(s - 1)
            if turned:
                weigh_last(s - 1)
            if not last:
                quantize_x_half(s + 1, 1)
            if turned:
                gate_terms(s - 1)
            mm2(s - 2, 0)
            mm2(s - 2, 1)
            add_bias(s, 1)
            mm2(s - 2, 2)
            mm2(s - 2, LAST)
            turn_pieces(s - 1)
            add_bias(s, 0)
            turn_q(s, PAIRS[:2], range(1))
            add_bias(s, 3)
            turn_q(s, PAIRS[:3], range(2))
            add_bias(s, 2)
            if more_x:
                turn_q(s, PAIRS, range(LAST))
                widen(s + 2, 1, "s")
                if s > 2:
                    widen(s + 2, 0, "s", CHUNK - TILE)
            unload_pieces(s - 1)
            turn_q(s, PAIRS, range(2))
            finish(s - 2, 1, "v")
            finish(s - 2, 0, "v")
            if not more_x:
                store(s - 2, 0, 2)
            if more_x:
                interleave(s + 2, "g")
            make_gate(s - 1, 0)
            make_gate(s - 1, 1)
            turn_q(s, PAIRS, range(2, NT))
            if more_x:
                finish(s - 2, LAST, "v")
            finish(s - 2, 2, "v")
            if not more_x:
                finish(s - 2, LAST, "s")
                add_out(s - 2, LAST)
                store(s - 2, 2, LAST)
                store(s - 2, LAST, NT)
            else:
                store(s - 2, 0, NT)
            make_gate(s - 1, 2)
            make_gate(s - 1, LAST)
            if last:
                return
            for i in (1, 0, 2, LAST):
                squares(s, i)
            for t in range(PACK):
                mm1(s + 1, t)
            for i in (1, 0, 2, LAST) if more_x else range(NT):
                gating(s - 1, i)
            if more_planes:
                widen(s + 3, 2, "s")
            root(s)

        def last_steps():
            k = NCHUNKS - 1
            for i in (1, 0, 2):
                squares(k, i)
            root(k, 0, 2)
            squares(k, LAST)
            root(k, 2, NT)
            for i in range(LAST):
                gating(k - 1, i)
            split_first(k, 0, 2)
            gating(k - 1, LAST)
            split_second(k, 0, 2)
            quantize_g_half(k - 1, 0)
            split_first(k, 2, NT)
            quantize_g_half(k - 1, 1)
            split_third(k, 0, 2)
            split_second(k, 2, NT)
            mm2(k - 1, 0)
            mm2(k - 1, 1)
            turn_pieces(k, "s", 0)
            mm2(k - 1, 2, "s")
            mm2(k - 1, LAST, "s")
            finish(k - 1, 0, "v")
            store(k - 1, 0, 1)
            split_third(k, 2, NT)
            unload_pieces(k, 0, 2)
            make_gate(k, 0)
            turn_pieces(k, "s", 2)
            make_gate(k, 1)
            finish(k - 1, 1, "v")
            store(k - 1, 1, 2)
            finish(k - 1, 2, "s")
            add_out(k - 1, 2)
            unload_pieces(k, 2, NT)
            make_gate(k, 2)
            make_gate(k, LAST)
            store(k - 1, 2, LAST)
            for i in range(LAST):
                gating(k, i)
            quantize_g_half(k, 0)
            mm2(k, 0)
            mm2(k, 1)
            gating(k, LAST)
            finish(k - 1, LAST, "v")
            store(k - 1, LAST, NT)
            quantize_g_half(k, 1)
            mm2(k, 2)
            mm2(k, LAST)
            for i in range(NT):
                finish(k, i, "v")
                store(k, i, i + 1)

        first_step()
        second_step()
        for s in range(2, NCHUNKS):
            step(s)
        last_steps()
